import numpy as np
import ml_dtypes


def mxq(x, axis, fmt="e4m3"):
    dtype, down = {"e4m3": (ml_dtypes.float8_e4m3fn, 7), "e5m2": (ml_dtypes.float8_e5m2, 14)}[fmt]
    v = np.moveaxis(np.asarray(x, np.float32).astype(ml_dtypes.bfloat16).astype(np.float64), axis, -1)
    blocks = v.reshape(v.shape[:-1] + (-1, 32))
    amax = np.abs(blocks).max(-1, keepdims=True)
    byte = np.maximum(np.where(amax > 0, np.frexp(amax)[1] - 1 + 127, 0) - down, 1)
    scale = np.exp2(byte - 127.0)
    codes = (blocks / scale).astype(np.float32).astype(dtype).astype(np.float64)
    return np.moveaxis((codes * scale).reshape(v.shape), -1, axis)


WIDE = False


def mx_kscale(k):
    if not WIDE:
        return np.ones(k)
    levels = np.array([10, -10, 5, -5, 0])
    a = np.random.permutation(np.resize(levels, k // 512 * 4)).reshape(k // 512, 4)
    idx = np.arange(k)
    return np.exp2(a[idx // 512, idx % 128 // 32])


BF16 = ml_dtypes.bfloat16


def bf(x):
    return np.asarray(x, np.float32).astype(BF16)


def f64(x):
    return np.asarray(x).astype(np.float64)


B, C, GH, GW, F, D, K, T = 3, 1536, 32, 32, 512, 512, 128, 256
N = GH * GW
EPS_NORM = 1e-12
EPS_DENOM = 1e-6


def l2norm(x, axis):
    n = np.sqrt(np.sum(x * x, axis=axis, keepdims=True))
    return x / np.maximum(n, EPS_NORM)


def sigmoid(z):
    return 1.0 / (1.0 + np.exp(-z))


def setup_inputs():
    t = mx_kscale(F)
    c = np.random.standard_normal((B, D))
    g = np.random.standard_normal((B, N))
    f = c[:, :, None] * g[:, None, :] + np.random.standard_normal((B, D, N))
    return {"f_clu": bf(f),
            "h_score": bf(np.maximum(np.random.standard_normal((B, F, N)), 0.0) * t[None, :, None]),
            "W_s2": bf(np.random.standard_normal((K, F)) * 2.5 / np.sqrt(F) / t[None, :]),
            "b_s2": bf(np.random.standard_normal(K) * 0.5),
            "burst_par": bf([5.0 + 0.25 * np.random.standard_normal(),
                             -2.5 + 0.25 * np.random.standard_normal(),
                             0.75 + 0.05 * np.random.standard_normal()])}


def reference(f_clu, h_score, W_s2, b_s2, burst_par):
    f = f64(f_clu)
    a_par, b_par, p_par = f64(burst_par)
    scores = (mxq(f64(W_s2), 1, "e4m3") @ mxq(f64(h_score), 1, "e4m3")) + f64(b_s2)[None, :, None]
    e = np.exp(scores - scores.max(axis=1, keepdims=True))
    alpha = e / e.sum(axis=1, keepdims=True)
    fq = mxq(l2norm(f, 1), 1, "e4m3")
    sim = fq.transpose(0, 2, 1) @ fq
    w = sigmoid(a_par * sim + b_par).sum(axis=2)
    pmat = alpha / (np.power(w, p_par)[:, None, :] + EPS_DENOM)
    v = mxq(f, 2, "e4m3") @ mxq(pmat, 2, "e4m3").transpose(0, 2, 1)
    return l2norm(v, 1)

@@ -1,0 +1,361 @@
+from contextlib import ExitStack
+
+import concourse.mybir as mybir
+from concourse.masks import make_identity
+
+F32 = mybir.dt.float32
+BF16 = mybir.dt.bfloat16
+U32 = mybir.dt.uint32
+U8 = mybir.dt.uint8
+FP8X4 = mybir.dt.float8_e4m3fn_x4
+ACT = mybir.ActivationFunctionType
+ALU = mybir.AluOpType
+AX = mybir.AxisListType
+
+P = 128
+PACK = 4
+PASS = P * PACK
+IMAGES = 3
+CHANNELS = 512
+PIXELS = 1024
+CLUSTERS = 128
+HALVES = PIXELS // PASS
+TILES = HALVES * PACK
+EPS_NORM_SQ = 1e-24
+EPS_DENOM = 1e-6
+
+FLOPS = IMAGES * 2 * (CLUSTERS * CHANNELS * PIXELS + PIXELS * PIXELS * CHANNELS + CHANNELS * CLUSTERS * PIXELS)
+
+
+def tile_salad_pa_kernel(tc, f_clu, h_score, W_s2, b_s2, burst_par, out):
+    nc = tc.nc
+    with ExitStack() as stack:
+        const = stack.enter_context(tc.tile_pool(name="const", bufs=1))
+        inputs = stack.enter_context(tc.tile_pool(name="inputs", bufs=IMAGES))
+        kept = stack.enter_context(tc.tile_pool(name="kept", bufs=IMAGES * HALVES))
+        work = stack.enter_context(tc.tile_pool(name="work", bufs=2))
+        scratch = stack.enter_context(tc.tile_pool(name="scratch", bufs=4))
+        psum_sim = stack.enter_context(tc.psum_pool(name="psum_sim", bufs=4))
+        psum_rn = stack.enter_context(tc.psum_pool(name="psum_rn", bufs=2))
+        psum_work = stack.enter_context(tc.psum_pool(name="psum_work", bufs=2))
+        stack.enter_context(tc.manual_schedule())
+
+        def half(g):
+            return slice(g * PASS, (g + 1) * PASS)
+
+        w_sb = const.tile([P, CHANNELS], BF16)
+        nc.scalar.dma_start(out=w_sb[:], in_=W_s2)
+        bias_bc = const.tile([P, CLUSTERS], BF16)
+        nc.scalar.dma_start(out=bias_bc[:], in_=b_s2.partition_broadcast(P))
+        par_bf = const.tile([P, 3], BF16)
+        nc.scalar.dma_start(out=par_bf[:], in_=burst_par.partition_broadcast(P))
+
+        f_sb = [inputs.tile([P, PACK * PIXELS], BF16, name="f_sb") for i in range(IMAGES)]
+        h_sb = [inputs.tile([P, PACK * PIXELS], BF16, name="h_sb") for i in range(IMAGES)]
+        for g in range(HALVES):
+            nc.sync.dma_start(
+                out=f_sb[0][:].rearrange("q (j n) -> q j n", j=PACK)[:, :, half(g)],
+                in_=f_clu[0].rearrange("(q j) n -> q j n", j=PACK)[:, :, half(g)],
+            )
+        nc.sync.dma_start(out=f_sb[1][:], in_=f_clu[1].rearrange("(q j) n -> q (j n)", j=PACK))
+        nc.sync.dma_start(out=h_sb[0][:], in_=h_score[0].rearrange("(q j) n -> q (j n)", j=PACK))
+        nc.sync.dma_start(out=f_sb[2][:], in_=f_clu[2].rearrange("(q j) n -> q (j n)", j=PACK))
+        nc.sync.dma_start(out=h_sb[1][:], in_=h_score[1].rearrange("(q j) n -> q (j n)", j=PACK))
+        nc.sync.dma_start(out=h_sb[2][:], in_=h_score[2].rearrange("(q j) n -> q (j n)", j=PACK))
+
+        ident = const.tile([P, P], F32)
+        make_identity(nc, ident[:])
+        neg_half = const.tile([P, PACK], F32)
+        nc.gpsimd.memset(neg_half[:], -0.5)
+        warm = const.tile([P, 1], F32)
+        nc.scalar.activation(out=warm[:], in_=neg_half[:, 0:1], func=ACT.Sigmoid)
+        par = const.tile([P, 3], F32)
+        slope = par[:, 0:1]
+        offset = par[:, 1:2]
+        exponent = par[:, 2:3]
+
+        ft_grouped, ft_codes, ft_scales = {}, {}, {}
+        inv_norm, rn_bank = {}, {}
+        fn_grouped, fn_codes, fn_scales = {}, {}, {}
+        h_grouped, h_codes, h_scales = {}, {}, {}
+        logits, neg_max, expd, exp_sum = {}, {}, {}, {}
+        row_sums, powered = {}, {}
+        pm_grouped, vt_bank, v_inv, out_bank = {}, {}, {}, {}
+
+        w_codes = const.tile([P, CLUSTERS], U32, align_bytes=64)
+        w_scales = const.tile([P, CLUSTERS], U8, align_bytes=64)
+
+        def prepare_weights():
+            w_words = w_sb[:].bitcast(F32).rearrange("k (q u) -> k u q", u=2)
+            w_ps = psum_work.tile([P, 2, CLUSTERS], F32, name="bank")
+            for u in range(2):
+                nc.tensor.transpose(out=w_ps[:, u, :], in_=w_words[:, u, :], identity=ident[:])
+            w_grouped = const.tile([P, CLUSTERS * PACK], BF16, align_bytes=64)
+            nc.vector.tensor_copy(
+                out=w_grouped[:].bitcast(F32).rearrange("q (k u) -> q k u", u=2),
+                in_=w_ps[:].rearrange("q u k -> q k u"),
+            )
+            nc.vector.quantize_mx(out=w_codes[:].bitcast(FP8X4), scales=w_scales[:], in_=w_grouped[:])
+
+        def transpose_features(i, g):
+            f_words = f_sb[i][:].bitcast(F32).rearrange("q (j g p u) -> q j g u p", j=PACK, g=HALVES, u=2)
+            ft_grouped[i, g] = work.tile([P, CHANNELS * PACK], BF16, name="ft_grouped", bufs=4, align_bytes=64)
+            grouped_words = ft_grouped[i, g][:].bitcast(F32).rearrange("p (c u) -> p c u", u=2)
+            for pair in range(2):
+                ft_ps = psum_work.tile([P, 2, 2, P], F32, name="bank")
+                for u in range(2):
+                    for jj in range(2):
+                        nc.tensor.transpose(
+                            out=ft_ps[:, u, jj, :], in_=f_words[:, 2 * pair + jj, g, u, :], identity=ident[:]
+                        )
+                copy = nc.vector.tensor_copy if pair == 0 else nc.scalar.copy
+                copy(
+                    out=grouped_words[:, pair * 2 * P : (pair + 1) * 2 * P, :],
+                    in_=ft_ps[:].rearrange("p u jj q -> p (jj q) u"),
+                )
+
+        def inverse_norms(i, g):
+            sum_sq = work.tile([P, PACK], F32, name="sum_sq")
+            by_tile = ft_grouped[i, g][:].rearrange("p (c t) -> p t c", t=PACK)
+            for t in range(PACK):
+                unread = scratch.tile([P, CHANNELS], BF16, name="unread")
+                nc.scalar.activation(
+                    out=unread[:], in_=by_tile[:, t, :], func=ACT.Square, accum_out=sum_sq[:, t : t + 1]
+                )
+            floored = work.tile([P, PACK], F32, name="floored")
+            nc.gpsimd.tensor_scalar_max(out=floored[:], in0=sum_sq[:], scalar1=EPS_NORM_SQ)
+            inv_norm[i, g] = work.tile([P, PACK], F32, name="inv_norm", bufs=4)
+            nc.gpsimd.tensor_tensor(out=inv_norm[i, g][:], in0=floored[:], in1=neg_half[:], op=ALU.pow)
+
+        def spread_inverse_norms(i, g):
+            rn_bank[i, g] = psum_rn.tile([P, PACK, P], F32, name="rn_bank")
+            for t in range(PACK):
+                nc.tensor.transpose(
+                    out=rn_bank[i, g][:, t, :], in_=inv_norm[i, g][:, t : t + 1].to_broadcast([P, P]), identity=ident[:]
+                )
+
+        def normalise(i, g):
+            f_view = f_sb[i][:].rearrange("q (j g p t) -> q g t p j", j=PACK, g=HALVES, t=PACK)
+            fn_grouped[i, g] = work.tile([P, PASS * PACK], BF16, name="fn_grouped", align_bytes=64)
+            nc.vector.tensor_tensor(
+                out=fn_grouped[i, g][:].rearrange("q (t p j) -> q t p j", t=PACK, j=PACK),
+                in0=f_view[:, g],
+                in1=rn_bank[i, g][:].unsqueeze(3).to_broadcast([P, PACK, P, PACK]),
+                op=ALU.mult,
+            )
+
+        def quantise_fn(i, g):
+            if g == 0:
+                fn_codes[i] = work.tile([P, PIXELS], U32, name="fn_codes", align_bytes=64)
+                fn_scales[i] = work.tile([P, PIXELS], U8, name="fn_scales", align_bytes=64)
+            nc.vector.quantize_mx(
+                out=fn_codes[i][:, half(g)].bitcast(FP8X4), scales=fn_scales[i][:, half(g)], in_=fn_grouped[i, g][:]
+            )
+
+        def quantise_ft(i, g):
+            ft_codes[i, g] = kept.tile([P, CHANNELS], U32, name="ft_codes", align_bytes=64)
+            ft_scales[i, g] = kept.tile([P, CHANNELS], U8, name="ft_scales", align_bytes=64)
+            nc.vector.quantize_mx(
+                out=ft_codes[i, g][:].bitcast(FP8X4), scales=ft_scales[i, g][:], in_=ft_grouped[i, g][:]
+            )
+
+        def regroup_h(i, g):
+            h_view = h_sb[i][:].rearrange("q (j g p t) -> q g t p j", j=PACK, g=HALVES, t=PACK)
+            h_grouped[i, g] = work.tile([P, PASS * PACK], BF16, name="h_grouped", align_bytes=64)
+            nc.vector.tensor_copy(
+                out=h_grouped[i, g][:].rearrange("q (t p j) -> q t p j", t=PACK, j=PACK), in_=h_view[:, g]
+            )
+
+        def quantise_h(i, g):
+            if g == 0:
+                h_codes[i] = work.tile([P, PIXELS], U32, name="h_codes", align_bytes=64)
+                h_scales[i] = work.tile([P, PIXELS], U8, name="h_scales", align_bytes=64)
+            nc.vector.quantize_mx(
+                out=h_codes[i][:, half(g)].bitcast(FP8X4), scales=h_scales[i][:, half(g)], in_=h_grouped[i, g][:]
+            )
+
+        def score_logits(i, g):
+            score_ps = psum_work.tile([P, PACK, CLUSTERS], F32, name="bank")
+            for t in range(PACK):
+                cols = slice((g * PACK + t) * P, (g * PACK + t + 1) * P)
+                nc.tensor.matmul_mx(
+                    out=score_ps[:, t, :],
+                    lhsT=h_codes[i][:, cols].bitcast(FP8X4),
+                    lhsT_scale=h_scales[i][:, cols],
+                    rhs=w_codes[:].bitcast(FP8X4),
+                    rhs_scale=w_scales[:],
+                    start=True,
+                    stop=True,
+                )
+            logits[i, g] = kept.tile([P, PACK, CLUSTERS], F32, name="logits")
+            nc.vector.tensor_tensor(
+                out=logits[i, g][:],
+                in0=score_ps[:],
+                in1=bias_bc[:].unsqueeze(1).to_broadcast([P, PACK, CLUSTERS]),
+                op=ALU.add,
+            )
+            neg_max[i, g] = kept.tile([P, PACK], F32, name="neg_max")
+            nc.vector.tensor_reduce(out=neg_max[i, g][:], in_=logits[i, g][:], axis=AX.X, op=ALU.max, negate=True)
+
+        def burst_sums(i, g, m):
+            if m == 0:
+                row_sums[i, g] = kept.tile([P, PACK * HALVES], F32, name="row_sums")
+            for t in range(PACK):
+                rows = slice((g * PACK + t) * P, (g * PACK + t + 1) * P)
+                sim_ps = psum_sim.tile([P, PASS], F32, name="sim_ps")
+                nc.tensor.matmul_mx(
+                    out=sim_ps[:],
+                    lhsT=fn_codes[i][:, rows].bitcast(FP8X4),
+                    lhsT_scale=fn_scales[i][:, rows],
+                    rhs=fn_codes[i][:, half(m)].bitcast(FP8X4),
+                    rhs_scale=fn_scales[i][:, half(m)],
+                    start=True,
+                    stop=True,
+                )
+                unread = scratch.tile([P, PASS], BF16, name="unread")
+                nc.scalar.activation(
+                    out=unread[:],
+                    in_=sim_ps[:],
+                    func=ACT.Sigmoid,
+                    scale=slope,
+                    bias=offset,
+                    accum_out=row_sums[i, g][:, t * HALVES + m : t * HALVES + m + 1],
+                )
+
+        def burst_power(i, g):
+            burst = work.tile([P, PACK], F32, name="burst")
+            nc.vector.tensor_reduce(
+                out=burst[:], in_=row_sums[i, g][:].rearrange("p (t m) -> p t m", m=HALVES), axis=AX.X, op=ALU.add
+            )
+            powered[i, g] = kept.tile([P, PACK], F32, name="powered")
+            nc.gpsimd.tensor_tensor(
+                out=powered[i, g][:], in0=burst[:], in1=exponent.to_broadcast([P, PACK]), op=ALU.pow
+            )
+
+        def softmax_numerators(i, g):
+            expd[i, g] = kept.tile([P, PACK, CLUSTERS], F32, name="expd")
+            exp_sum[i, g] = kept.tile([P, PACK], F32, name="exp_sum")
+            for t in range(PACK):
+                nc.scalar.activation(
+                    out=expd[i, g][:, t, :],
+                    in_=logits[i, g][:, t, :],
+                    func=ACT.Exp,
+                    bias=neg_max[i, g][:, t : t + 1],
+                    accum_out=exp_sum[i, g][:, t : t + 1],
+                )
+
+        def weigh(i, g):
+            denom = work.tile([P, PACK], F32, name="denom")
+            nc.vector.scalar_tensor_tensor(
+                out=denom[:], in0=powered[i, g][:], scalar=EPS_DENOM, in1=exp_sum[i, g][:], op0=ALU.add, op1=ALU.mult
+            )
+            weight = work.tile([P, PACK], F32, name="weight")
+            nc.vector.reciprocal(out=weight[:], in_=denom[:])
+            pm_grouped[i, g] = work.tile([P, CLUSTERS * PACK], BF16, name="pm_grouped", align_bytes=64)
+            nc.vector.tensor_tensor(
+                out=pm_grouped[i, g][:].rearrange("p (k t) -> p k t", t=PACK),
+                in0=expd[i, g][:].rearrange("p t k -> p k t"),
+                in1=weight[:].unsqueeze(1).to_broadcast([P, CLUSTERS, PACK]),
+                op=ALU.mult,
+            )
+
+        def aggregate(i, g):
+            pm_codes = work.tile([P, CLUSTERS], U32, name="pm_codes", align_bytes=64)
+            pm_scales = work.tile([P, CLUSTERS], U8, name="pm_scales", align_bytes=64)
+            nc.vector.quantize_mx(out=pm_codes[:].bitcast(FP8X4), scales=pm_scales[:], in_=pm_grouped[i, g][:])
+            if g == 0:
+                vt_bank[i] = psum_work.tile([P, CHANNELS], F32, name="bank")
+            nc.tensor.matmul_mx(
+                out=vt_bank[i][:],
+                lhsT=pm_codes[:].bitcast(FP8X4),
+                lhsT_scale=pm_scales[:],
+                rhs=ft_codes[i, g][:].bitcast(FP8X4),
+                rhs_scale=ft_scales[i, g][:],
+                start=(g == 0),
+                stop=(g == HALVES - 1),
+            )
+
+        def cluster_norms(i):
+            v_sq = work.tile([P, 1], F32, name="v_sq")
+            unread = scratch.tile([P, CHANNELS], BF16, name="unread")
+            nc.scalar.activation(out=unread[:], in_=vt_bank[i][:], func=ACT.Square, accum_out=v_sq[:])
+            v_floored = work.tile([P, 1], F32, name="v_floored")
+            nc.gpsimd.tensor_scalar_max(out=v_floored[:], in0=v_sq[:], scalar1=EPS_NORM_SQ)
+            v_inv[i] = work.tile([P, 1], F32, name="v_inv")
+            nc.gpsimd.tensor_tensor(out=v_inv[i][:], in0=v_floored[:], in1=neg_half[:, 0:1], op=ALU.pow)
+
+        def unit_columns(i):
+            v_unit = work.tile([P, CHANNELS], F32, name="v_unit")
+            nc.vector.tensor_scalar_mul(out=v_unit[:], in0=vt_bank[i][:], scalar1=v_inv[i][:])
+            out_bank[i] = psum_work.tile([P, PACK, CLUSTERS], F32, name="bank")
+            for j in range(PACK):
+                nc.tensor.transpose(out=out_bank[i][:, j, :], in_=v_unit[:, j * P : (j + 1) * P], identity=ident[:])
+
+        def store(i):
+            out_sb = work.tile([P, PACK, CLUSTERS], F32, name="out_sb")
+            nc.vector.tensor_copy(out=out_sb[:], in_=out_bank[i][:])
+            nc.sync.dma_start(out=out[i].rearrange("(q j) k -> q j k", j=PACK), in_=out_sb[:])
+
+        for i, g in ((0, 0), (0, 1), (1, 0)):
+            transpose_features(i, g)
+            inverse_norms(i, g)
+        nc.vector.tensor_copy(out=par[:], in_=par_bf[:])
+        spread_inverse_norms(0, 0)
+        normalise(0, 0)
+        quantise_fn(0, 0)
+        transpose_features(1, 1)
+        spread_inverse_norms(0, 1)
+        normalise(0, 1)
+        quantise_fn(0, 1)
+        quantise_ft(0, 0)
+        quantise_ft(0, 1)
+        prepare_weights()
+
+        for i in range(IMAGES):
+            following = i + 1 < IMAGES
+            burst_sums(i, 0, 0)
+            if following:
+                inverse_norms(i + 1, 1)
+            for g in range(HALVES):
+                regroup_h(i, g)
+            for g in range(HALVES):
+                quantise_h(i, g)
+            if i > 0:
+                burst_power(i - 1, 1)
+            burst_sums(i, 0, 1)
+            if following:
+                spread_inverse_norms(i + 1, 0)
+                normalise(i + 1, 0)
+                quantise_ft(i + 1, 0)
+                quantise_fn(i + 1, 0)
+            burst_sums(i, 1, 0)
+            if i + 2 < IMAGES:
+                transpose_features(i + 2, 0)
+                inverse_norms(i + 2, 0)
+            for g in range(HALVES):
+                score_logits(i, g)
+            burst_power(i, 0)
+            if i + 2 < IMAGES:
+                transpose_features(i + 2, 1)
+            if following:
+                spread_inverse_norms(i + 1, 1)
+                normalise(i + 1, 1)
+                quantise_ft(i + 1, 1)
+                quantise_fn(i + 1, 1)
+            burst_sums(i, 1, 1)
+        burst_power(IMAGES - 1, 1)
+
+        for i in range(IMAGES):
+            for g in range(HALVES):
+                softmax_numerators(i, g)
+        for step in range(IMAGES + 2):
+            if step < IMAGES:
+                for g in range(HALVES):
+                    weigh(step, g)
+                for g in range(HALVES):
+                    aggregate(step, g)
+                cluster_norms(step)
+            if 1 <= step <= IMAGES:
+                unit_columns(step - 1)
+            if step >= 2:
+                store(step - 2)

@@ -21,6 +21,12 @@ PIXELS = 1024
 CLUSTERS = 128
 HALVES = PIXELS // PASS
 TILES = HALVES * PACK
+HALF_IMAGES = IMAGES * HALVES
+UNITS = HALF_IMAGES * HALVES
+LEAD_TRANSPOSE = 7
+LEAD_SQUARES = 6
+LEAD_SPREAD = 4
+LEAD_NORMALISE = 3
 EPS_NORM_SQ = 1e-24
 EPS_DENOM = 1e-6
 
@@ -36,19 +42,12 @@ def tile_salad_pa_kernel(tc, f_clu, h_score, W_s2, b_s2, burst_par, out):
         work = stack.enter_context(tc.tile_pool(name="work", bufs=2))
         scratch = stack.enter_context(tc.tile_pool(name="scratch", bufs=4))
         psum_sim = stack.enter_context(tc.psum_pool(name="psum_sim", bufs=4))
-        psum_rn = stack.enter_context(tc.psum_pool(name="psum_rn", bufs=2))
-        psum_work = stack.enter_context(tc.psum_pool(name="psum_work", bufs=2))
+        psum_rn = stack.enter_context(tc.psum_pool(name="psum_rn", bufs=1))
+        psum_work = stack.enter_context(tc.psum_pool(name="psum_work", bufs=3))
         stack.enter_context(tc.manual_schedule())
 
         def half(g):
             return slice(g * PASS, (g + 1) * PASS)
-
-        w_sb = const.tile([P, CHANNELS], BF16)
-        nc.scalar.dma_start(out=w_sb[:], in_=W_s2)
-        bias_bc = const.tile([P, CLUSTERS], BF16)
-        nc.scalar.dma_start(out=bias_bc[:], in_=b_s2.partition_broadcast(P))
-        par_bf = const.tile([P, 3], BF16)
-        nc.scalar.dma_start(out=par_bf[:], in_=burst_par.partition_broadcast(P))
 
         f_sb = [inputs.tile([P, PACK * PIXELS], BF16, name="f_sb") for i in range(IMAGES)]
         h_sb = [inputs.tile([P, PACK * PIXELS], BF16, name="h_sb") for i in range(IMAGES)]
@@ -57,9 +56,15 @@ def tile_salad_pa_kernel(tc, f_clu, h_score, W_s2, b_s2, burst_par, out):
                 out=f_sb[0][:].rearrange("q (j n) -> q j n", j=PACK)[:, :, half(g)],
                 in_=f_clu[0].rearrange("(q j) n -> q j n", j=PACK)[:, :, half(g)],
             )
+        par_bf = const.tile([P, 3], BF16)
+        nc.sync.dma_start(out=par_bf[:], in_=burst_par.partition_broadcast(P))
+        w_sb = const.tile([P, CHANNELS], BF16)
+        bias_bc = const.tile([P, CLUSTERS], BF16)
         nc.sync.dma_start(out=f_sb[1][:], in_=f_clu[1].rearrange("(q j) n -> q (j n)", j=PACK))
+        nc.sync.dma_start(out=w_sb[:], in_=W_s2)
         nc.sync.dma_start(out=h_sb[0][:], in_=h_score[0].rearrange("(q j) n -> q (j n)", j=PACK))
         nc.sync.dma_start(out=f_sb[2][:], in_=f_clu[2].rearrange("(q j) n -> q (j n)", j=PACK))
+        nc.sync.dma_start(out=bias_bc[:], in_=b_s2.partition_broadcast(P))
         nc.sync.dma_start(out=h_sb[1][:], in_=h_score[1].rearrange("(q j) n -> q (j n)", j=PACK))
         nc.sync.dma_start(out=h_sb[2][:], in_=h_score[2].rearrange("(q j) n -> q (j n)", j=PACK))
 
@@ -70,6 +75,7 @@ def tile_salad_pa_kernel(tc, f_clu, h_score, W_s2, b_s2, burst_par, out):
         warm = const.tile([P, 1], F32)
         nc.scalar.activation(out=warm[:], in_=neg_half[:, 0:1], func=ACT.Sigmoid)
         par = const.tile([P, 3], F32)
+        nc.gpsimd.tensor_copy(out=par[:], in_=par_bf[:])
         slope = par[:, 0:1]
         offset = par[:, 1:2]
         exponent = par[:, 2:3]
@@ -78,7 +84,7 @@ def tile_salad_pa_kernel(tc, f_clu, h_score, W_s2, b_s2, burst_par, out):
         inv_norm, rn_bank = {}, {}
         fn_grouped, fn_codes, fn_scales = {}, {}, {}
         h_grouped, h_codes, h_scales = {}, {}, {}
-        logits, neg_max, expd, exp_sum = {}, {}, {}, {}
+        score_bank, logits, neg_max, expd, exp_sum = {}, {}, {}, {}, {}
         row_sums, powered = {}, {}
         pm_grouped, vt_bank, v_inv, out_bank = {}, {}, {}, {}
 
@@ -135,12 +141,12 @@ def tile_salad_pa_kernel(tc, f_clu, h_score, W_s2, b_s2, burst_par, out):
                 )
 
         def normalise(i, g):
-            f_view = f_sb[i][:].rearrange("q (j g p t) -> q g t p j", j=PACK, g=HALVES, t=PACK)
+            f_view = f_sb[i][:].rearrange("q (j g p t) -> q g p j t", j=PACK, g=HALVES, t=PACK)
             fn_grouped[i, g] = work.tile([P, PASS * PACK], BF16, name="fn_grouped", align_bytes=64)
             nc.vector.tensor_tensor(
-                out=fn_grouped[i, g][:].rearrange("q (t p j) -> q t p j", t=PACK, j=PACK),
+                out=fn_grouped[i, g][:].rearrange("q (t p j) -> q p j t", t=PACK, j=PACK),
                 in0=f_view[:, g],
-                in1=rn_bank[i, g][:].unsqueeze(3).to_broadcast([P, PACK, P, PACK]),
+                in1=rn_bank[i, g][:].rearrange("q t p -> q p t").unsqueeze(2).to_broadcast([P, P, PACK, PACK]),
                 op=ALU.mult,
             )
 
@@ -160,10 +166,10 @@ def tile_salad_pa_kernel(tc, f_clu, h_score, W_s2, b_s2, burst_par, out):
             )
 
         def regroup_h(i, g):
-            h_view = h_sb[i][:].rearrange("q (j g p t) -> q g t p j", j=PACK, g=HALVES, t=PACK)
+            h_view = h_sb[i][:].rearrange("q (j g p t) -> q g p j t", j=PACK, g=HALVES, t=PACK)
             h_grouped[i, g] = work.tile([P, PASS * PACK], BF16, name="h_grouped", align_bytes=64)
             nc.vector.tensor_copy(
-                out=h_grouped[i, g][:].rearrange("q (t p j) -> q t p j", t=PACK, j=PACK), in_=h_view[:, g]
+                out=h_grouped[i, g][:].rearrange("q (t p j) -> q p j t", t=PACK, j=PACK), in_=h_view[:, g]
             )
 
         def quantise_h(i, g):
@@ -174,12 +180,12 @@ def tile_salad_pa_kernel(tc, f_clu, h_score, W_s2, b_s2, burst_par, out):
                 out=h_codes[i][:, half(g)].bitcast(FP8X4), scales=h_scales[i][:, half(g)], in_=h_grouped[i, g][:]
             )
 
-        def score_logits(i, g):
-            score_ps = psum_work.tile([P, PACK, CLUSTERS], F32, name="bank")
+        def score_passes(i, g):
+            score_bank[i, g] = psum_work.tile([P, PACK, CLUSTERS], F32, name="bank")
             for t in range(PACK):
                 cols = slice((g * PACK + t) * P, (g * PACK + t + 1) * P)
                 nc.tensor.matmul_mx(
-                    out=score_ps[:, t, :],
+                    out=score_bank[i, g][:, t, :],
                     lhsT=h_codes[i][:, cols].bitcast(FP8X4),
                     lhsT_scale=h_scales[i][:, cols],
                     rhs=w_codes[:].bitcast(FP8X4),
@@ -187,13 +193,17 @@ def tile_salad_pa_kernel(tc, f_clu, h_score, W_s2, b_s2, burst_par, out):
                     start=True,
                     stop=True,
                 )
+
+        def add_bias(i, g):
             logits[i, g] = kept.tile([P, PACK, CLUSTERS], F32, name="logits")
             nc.vector.tensor_tensor(
                 out=logits[i, g][:],
-                in0=score_ps[:],
+                in0=score_bank[i, g][:],
                 in1=bias_bc[:].unsqueeze(1).to_broadcast([P, PACK, CLUSTERS]),
                 op=ALU.add,
             )
+
+        def negative_maxima(i, g):
             neg_max[i, g] = kept.tile([P, PACK], F32, name="neg_max")
             nc.vector.tensor_reduce(out=neg_max[i, g][:], in_=logits[i, g][:], axis=AX.X, op=ALU.max, negate=True)
 
@@ -227,53 +237,57 @@ def tile_salad_pa_kernel(tc, f_clu, h_score, W_s2, b_s2, burst_par, out):
             nc.vector.tensor_reduce(
                 out=burst[:], in_=row_sums[i, g][:].rearrange("p (t m) -> p t m", m=HALVES), axis=AX.X, op=ALU.add
             )
-            powered[i, g] = kept.tile([P, PACK], F32, name="powered")
-            nc.gpsimd.tensor_tensor(
-                out=powered[i, g][:], in0=burst[:], in1=exponent.to_broadcast([P, PACK]), op=ALU.pow
-            )
-
-        def softmax_numerators(i, g):
-            expd[i, g] = kept.tile([P, PACK, CLUSTERS], F32, name="expd")
-            exp_sum[i, g] = kept.tile([P, PACK], F32, name="exp_sum")
-            for t in range(PACK):
-                nc.scalar.activation(
-                    out=expd[i, g][:, t, :],
-                    in_=logits[i, g][:, t, :],
-                    func=ACT.Exp,
-                    bias=neg_max[i, g][:, t : t + 1],
-                    accum_out=exp_sum[i, g][:, t : t + 1],
-                )
-
-        def weigh(i, g):
-            denom = work.tile([P, PACK], F32, name="denom")
-            nc.vector.scalar_tensor_tensor(
-                out=denom[:], in0=powered[i, g][:], scalar=EPS_DENOM, in1=exp_sum[i, g][:], op0=ALU.add, op1=ALU.mult
-            )
-            weight = work.tile([P, PACK], F32, name="weight")
-            nc.vector.reciprocal(out=weight[:], in_=denom[:])
-            pm_grouped[i, g] = work.tile([P, CLUSTERS * PACK], BF16, name="pm_grouped", align_bytes=64)
-            nc.vector.tensor_tensor(
-                out=pm_grouped[i, g][:].rearrange("p (k t) -> p k t", t=PACK),
-                in0=expd[i, g][:].rearrange("p t k -> p k t"),
-                in1=weight[:].unsqueeze(1).to_broadcast([P, CLUSTERS, PACK]),
-                op=ALU.mult,
-            )
-
-        def aggregate(i, g):
-            pm_codes = work.tile([P, CLUSTERS], U32, name="pm_codes", align_bytes=64)
-            pm_scales = work.tile([P, CLUSTERS], U8, name="pm_scales", align_bytes=64)
-            nc.vector.quantize_mx(out=pm_codes[:].bitcast(FP8X4), scales=pm_scales[:], in_=pm_grouped[i, g][:])
             if g == 0:
-                vt_bank[i] = psum_work.tile([P, CHANNELS], F32, name="bank")
-            nc.tensor.matmul_mx(
-                out=vt_bank[i][:],
-                lhsT=pm_codes[:].bitcast(FP8X4),
-                lhsT_scale=pm_scales[:],
-                rhs=ft_codes[i, g][:].bitcast(FP8X4),
-                rhs_scale=ft_scales[i, g][:],
-                start=(g == 0),
-                stop=(g == HALVES - 1),
+                powered[i] = kept.tile([P, TILES], F32, name="powered")
+            nc.gpsimd.tensor_tensor(
+                out=powered[i][:, g * PACK : (g + 1) * PACK],
+                in0=burst[:],
+                in1=exponent.to_broadcast([P, PACK]),
+                op=ALU.pow,
             )
+
+        def softmax_numerators(i):
+            exp_sum[i] = kept.tile([P, TILES], F32, name="exp_sum")
+            for g in range(HALVES):
+                expd[i, g] = kept.tile([P, PACK, CLUSTERS], F32, name="expd")
+                for t in range(PACK):
+                    nc.scalar.activation(
+                        out=expd[i, g][:, t, :],
+                        in_=logits[i, g][:, t, :],
+                        func=ACT.Exp,
+                        bias=neg_max[i, g][:, t : t + 1],
+                        accum_out=exp_sum[i][:, g * PACK + t : g * PACK + t + 1],
+                    )
+
+        def aggregate(i):
+            denom = work.tile([P, TILES], F32, name="denom")
+            nc.vector.scalar_tensor_tensor(
+                out=denom[:], in0=powered[i][:], scalar=EPS_DENOM, in1=exp_sum[i][:], op0=ALU.add, op1=ALU.mult
+            )
+            weight = work.tile([P, TILES], F32, name="weight")
+            nc.vector.reciprocal(out=weight[:], in_=denom[:])
+            for g in range(HALVES):
+                pm_grouped[i, g] = work.tile([P, CLUSTERS * PACK], BF16, name="pm_grouped", align_bytes=64)
+                nc.vector.tensor_tensor(
+                    out=pm_grouped[i, g][:].rearrange("p (k t) -> p k t", t=PACK),
+                    in0=expd[i, g][:].rearrange("p t k -> p k t"),
+                    in1=weight[:, g * PACK : (g + 1) * PACK].unsqueeze(1).to_broadcast([P, CLUSTERS, PACK]),
+                    op=ALU.mult,
+                )
+            vt_bank[i] = psum_work.tile([P, CHANNELS], F32, name="bank")
+            for g in range(HALVES):
+                pm_codes = work.tile([P, CLUSTERS], U32, name="pm_codes", align_bytes=64)
+                pm_scales = work.tile([P, CLUSTERS], U8, name="pm_scales", align_bytes=64)
+                nc.vector.quantize_mx(out=pm_codes[:].bitcast(FP8X4), scales=pm_scales[:], in_=pm_grouped[i, g][:])
+                nc.tensor.matmul_mx(
+                    out=vt_bank[i][:],
+                    lhsT=pm_codes[:].bitcast(FP8X4),
+                    lhsT_scale=pm_scales[:],
+                    rhs=ft_codes[i, g][:].bitcast(FP8X4),
+                    rhs_scale=ft_scales[i, g][:],
+                    start=(g == 0),
+                    stop=(g == HALVES - 1),
+                )
 
         def cluster_norms(i):
             v_sq = work.tile([P, 1], F32, name="v_sq")
@@ -286,74 +300,62 @@ def tile_salad_pa_kernel(tc, f_clu, h_score, W_s2, b_s2, burst_par, out):
 
         def unit_columns(i):
             v_unit = work.tile([P, CHANNELS], F32, name="v_unit")
-            nc.vector.tensor_scalar_mul(out=v_unit[:], in0=vt_bank[i][:], scalar1=v_inv[i][:])
+            nc.scalar.activation(out=v_unit[:], in_=vt_bank[i][:], func=ACT.Copy, scale=v_inv[i][:])
             out_bank[i] = psum_work.tile([P, PACK, CLUSTERS], F32, name="bank")
             for j in range(PACK):
                 nc.tensor.transpose(out=out_bank[i][:, j, :], in_=v_unit[:, j * P : (j + 1) * P], identity=ident[:])
 
         def store(i):
             out_sb = work.tile([P, PACK, CLUSTERS], F32, name="out_sb")
-            nc.vector.tensor_copy(out=out_sb[:], in_=out_bank[i][:])
+            nc.scalar.copy(out=out_sb[:], in_=out_bank[i][:])
             nc.sync.dma_start(out=out[i].rearrange("(q j) k -> q j k", j=PACK), in_=out_sb[:])
 
-        for i, g in ((0, 0), (0, 1), (1, 0)):
-            transpose_features(i, g)
-            inverse_norms(i, g)
-        nc.vector.tensor_copy(out=par[:], in_=par_bf[:])
-        spread_inverse_norms(0, 0)
-        normalise(0, 0)
-        quantise_fn(0, 0)
-        transpose_features(1, 1)
-        spread_inverse_norms(0, 1)
-        normalise(0, 1)
-        quantise_fn(0, 1)
-        quantise_ft(0, 0)
-        quantise_ft(0, 1)
-        prepare_weights()
+        def due(slot, lead):
+            x, odd = divmod(slot + lead, 2)
+            if odd or not 0 <= x < HALF_IMAGES:
+                return None
+            return divmod(x, HALVES)
+
+        for slot in range(-LEAD_TRANSPOSE, UNITS + 1):
+            if 0 <= slot < UNITS:
+                i, rest = divmod(slot, HALVES * HALVES)
+                burst_sums(i, rest // HALVES, rest % HALVES)
+            if slot == 0:
+                prepare_weights()
+            stage = due(slot, LEAD_TRANSPOSE)
+            if stage:
+                transpose_features(*stage)
+            stage = due(slot, LEAD_SQUARES)
+            if stage:
+                inverse_norms(*stage)
+            stage = due(slot, LEAD_SPREAD)
+            if stage:
+                spread_inverse_norms(*stage)
+            stage = due(slot, LEAD_NORMALISE)
+            if stage:
+                normalise(*stage)
+                quantise_ft(*stage)
+                quantise_fn(*stage)
+            fresh = due(slot, 0)
+            scored = due(slot, -2)
+            if fresh:
+                regroup_h(*fresh)
+            if scored:
+                add_bias(*scored)
+            if fresh:
+                quantise_h(*fresh)
+            if scored:
+                negative_maxima(*scored)
+                burst_power(*scored)
+            stage = due(slot, -1)
+            if stage:
+                score_passes(*stage)
 
         for i in range(IMAGES):
-            following = i + 1 < IMAGES
-            burst_sums(i, 0, 0)
-            if following:
-                inverse_norms(i + 1, 1)
-            for g in range(HALVES):
-                regroup_h(i, g)
-            for g in range(HALVES):
-                quantise_h(i, g)
-            if i > 0:
-                burst_power(i - 1, 1)
-            burst_sums(i, 0, 1)
-            if following:
-                spread_inverse_norms(i + 1, 0)
-                normalise(i + 1, 0)
-                quantise_ft(i + 1, 0)
-                quantise_fn(i + 1, 0)
-            burst_sums(i, 1, 0)
-            if i + 2 < IMAGES:
-                transpose_features(i + 2, 0)
-                inverse_norms(i + 2, 0)
-            for g in range(HALVES):
-                score_logits(i, g)
-            burst_power(i, 0)
-            if i + 2 < IMAGES:
-                transpose_features(i + 2, 1)
-            if following:
-                spread_inverse_norms(i + 1, 1)
-                normalise(i + 1, 1)
-                quantise_ft(i + 1, 1)
-                quantise_fn(i + 1, 1)
-            burst_sums(i, 1, 1)
-        burst_power(IMAGES - 1, 1)
-
-        for i in range(IMAGES):
-            for g in range(HALVES):
-                softmax_numerators(i, g)
+            softmax_numerators(i)
         for step in range(IMAGES + 2):
             if step < IMAGES:
-                for g in range(HALVES):
-                    weigh(step, g)
-                for g in range(HALVES):
-                    aggregate(step, g)
+                aggregate(step)
                 cluster_norms(step)
             if 1 <= step <= IMAGES:
                 unit_columns(step - 1)

@@ -141,12 +141,12 @@ def tile_salad_pa_kernel(tc, f_clu, h_score, W_s2, b_s2, burst_par, out):
                 )
 
         def normalise(i, g):
-            f_view = f_sb[i][:].rearrange("q (j g p t) -> q g p j t", j=PACK, g=HALVES, t=PACK)
+            f_view = f_sb[i][:].rearrange("q (j g p t) -> q g t p j", j=PACK, g=HALVES, t=PACK)
             fn_grouped[i, g] = work.tile([P, PASS * PACK], BF16, name="fn_grouped", align_bytes=64)
             nc.vector.tensor_tensor(
-                out=fn_grouped[i, g][:].rearrange("q (t p j) -> q p j t", t=PACK, j=PACK),
+                out=fn_grouped[i, g][:].rearrange("q (t p j) -> q t p j", t=PACK, j=PACK),
                 in0=f_view[:, g],
-                in1=rn_bank[i, g][:].rearrange("q t p -> q p t").unsqueeze(2).to_broadcast([P, P, PACK, PACK]),
+                in1=rn_bank[i, g][:].unsqueeze(3).to_broadcast([P, PACK, P, PACK]),
                 op=ALU.mult,
             )
 
@@ -166,10 +166,10 @@ def tile_salad_pa_kernel(tc, f_clu, h_score, W_s2, b_s2, burst_par, out):
             )
 
         def regroup_h(i, g):
-            h_view = h_sb[i][:].rearrange("q (j g p t) -> q g p j t", j=PACK, g=HALVES, t=PACK)
+            h_view = h_sb[i][:].rearrange("q (j g p t) -> q g t p j", j=PACK, g=HALVES, t=PACK)
             h_grouped[i, g] = work.tile([P, PASS * PACK], BF16, name="h_grouped", align_bytes=64)
             nc.vector.tensor_copy(
-                out=h_grouped[i, g][:].rearrange("q (t p j) -> q p j t", t=PACK, j=PACK), in_=h_view[:, g]
+                out=h_grouped[i, g][:].rearrange("q (t p j) -> q t p j", t=PACK, j=PACK), in_=h_view[:, g]
             )
 
         def quantise_h(i, g):

@@ -114,8 +114,7 @@ def tile_salad_pa_kernel(tc, f_clu, h_score, W_s2, b_s2, burst_par, out):
                         nc.tensor.transpose(
                             out=ft_ps[:, u, jj, :], in_=f_words[:, 2 * pair + jj, g, u, :], identity=ident[:]
                         )
-                copy = nc.vector.tensor_copy if pair == 0 else nc.scalar.copy
-                copy(
+                nc.scalar.copy(
                     out=grouped_words[:, pair * 2 * P : (pair + 1) * 2 * P, :],
                     in_=ft_ps[:].rearrange("p u jj q -> p (jj q) u"),
                 )
@@ -141,12 +140,12 @@ def tile_salad_pa_kernel(tc, f_clu, h_score, W_s2, b_s2, burst_par, out):
                 )
 
         def normalise(i, g):
-            f_view = f_sb[i][:].rearrange("q (j g p t) -> q g t p j", j=PACK, g=HALVES, t=PACK)
+            f_view = f_sb[i][:].rearrange("q (j g p t) -> q g p j t", j=PACK, g=HALVES, t=PACK)
             fn_grouped[i, g] = work.tile([P, PASS * PACK], BF16, name="fn_grouped", align_bytes=64)
             nc.vector.tensor_tensor(
-                out=fn_grouped[i, g][:].rearrange("q (t p j) -> q t p j", t=PACK, j=PACK),
+                out=fn_grouped[i, g][:].rearrange("q (t p j) -> q p j t", t=PACK, j=PACK),
                 in0=f_view[:, g],
-                in1=rn_bank[i, g][:].unsqueeze(3).to_broadcast([P, PACK, P, PACK]),
+                in1=rn_bank[i, g][:].rearrange("q t p -> q p t").unsqueeze(2).to_broadcast([P, P, PACK, PACK]),
                 op=ALU.mult,
             )
 
@@ -166,10 +165,10 @@ def tile_salad_pa_kernel(tc, f_clu, h_score, W_s2, b_s2, burst_par, out):
             )
 
         def regroup_h(i, g):
-            h_view = h_sb[i][:].rearrange("q (j g p t) -> q g t p j", j=PACK, g=HALVES, t=PACK)
+            h_view = h_sb[i][:].rearrange("q (j g p t) -> q g p j t", j=PACK, g=HALVES, t=PACK)
             h_grouped[i, g] = work.tile([P, PASS * PACK], BF16, name="h_grouped", align_bytes=64)
             nc.vector.tensor_copy(
-                out=h_grouped[i, g][:].rearrange("q (t p j) -> q t p j", t=PACK, j=PACK), in_=h_view[:, g]
+                out=h_grouped[i, g][:].rearrange("q (t p j) -> q p j t", t=PACK, j=PACK), in_=h_view[:, g]
             )
 
         def quantise_h(i, g):

@@ -22,11 +22,9 @@ CLUSTERS = 128
 HALVES = PIXELS // PASS
 TILES = HALVES * PACK
 HALF_IMAGES = IMAGES * HALVES
-UNITS = HALF_IMAGES * HALVES
-LEAD_TRANSPOSE = 7
-LEAD_SQUARES = 6
-LEAD_SPREAD = 4
-LEAD_NORMALISE = 3
+PARTS = ((0, 0), (0, 1), (1, 1))
+UNITS = IMAGES * len(PARTS)
+HALVES_ON_TENSOR = 4
 EPS_NORM_SQ = 1e-24
 EPS_DENOM = 1e-6
 
@@ -41,39 +39,54 @@ def tile_salad_pa_kernel(tc, f_clu, h_score, W_s2, b_s2, burst_par, out):
         kept = stack.enter_context(tc.tile_pool(name="kept", bufs=IMAGES * HALVES))
         work = stack.enter_context(tc.tile_pool(name="work", bufs=2))
         scratch = stack.enter_context(tc.tile_pool(name="scratch", bufs=4))
-        psum_sim = stack.enter_context(tc.psum_pool(name="psum_sim", bufs=4))
-        psum_rn = stack.enter_context(tc.psum_pool(name="psum_rn", bufs=1))
-        psum_work = stack.enter_context(tc.psum_pool(name="psum_work", bufs=3))
-        stack.enter_context(tc.manual_schedule())
+        psum_sim = stack.enter_context(tc.psum_pool(name="psum_sim", bufs=3))
+        psum_col = stack.enter_context(tc.psum_pool(name="psum_col", bufs=1))
+        psum_rn = stack.enter_context(tc.psum_pool(name="psum_rn", bufs=2))
+        psum_work = stack.enter_context(tc.psum_pool(name="psum_work", bufs=2))
+        ordered = {mybir.EngineType.DVE, mybir.EngineType.Activation, mybir.EngineType.Pool, mybir.EngineType.SP}
+        stack.enter_context(tc.manual_schedule(engines=ordered))
 
         def half(g):
             return slice(g * PASS, (g + 1) * PASS)
 
         f_sb = [inputs.tile([P, PACK * PIXELS], BF16, name="f_sb") for i in range(IMAGES)]
-        h_sb = [inputs.tile([P, PACK * PIXELS], BF16, name="h_sb") for i in range(IMAGES)]
-        for g in range(HALVES):
-            nc.sync.dma_start(
-                out=f_sb[0][:].rearrange("q (j n) -> q j n", j=PACK)[:, :, half(g)],
-                in_=f_clu[0].rearrange("(q j) n -> q j n", j=PACK)[:, :, half(g)],
-            )
-        par_bf = const.tile([P, 3], BF16)
-        nc.sync.dma_start(out=par_bf[:], in_=burst_par.partition_broadcast(P))
+        first_h = [inputs.tile([P, PACK * PASS], BF16, name="first_h") for g in range(HALVES)]
+        h_sb = [None] + [inputs.tile([P, PACK * PIXELS], BF16, name="h_sb") for i in range(1, IMAGES)]
         w_sb = const.tile([P, CHANNELS], BF16)
+        par_bf = const.tile([P, 3], BF16)
         bias_bc = const.tile([P, CLUSTERS], BF16)
-        nc.sync.dma_start(out=f_sb[1][:], in_=f_clu[1].rearrange("(q j) n -> q (j n)", j=PACK))
+
+        def load(tile, source):
+            nc.sync.dma_start(out=tile[:], in_=source.rearrange("(q j) n -> q (j n)", j=PACK))
+
+        def load_half(tile, source, g):
+            nc.sync.dma_start(
+                out=tile[:].rearrange("q (j n) -> q j n", j=PACK),
+                in_=source.rearrange("(q j) n -> q j n", j=PACK)[:, :, half(g)],
+            )
+
+        load_half(first_h[0], h_score[0], 0)
         nc.sync.dma_start(out=w_sb[:], in_=W_s2)
-        nc.sync.dma_start(out=h_sb[0][:], in_=h_score[0].rearrange("(q j) n -> q (j n)", j=PACK))
-        nc.sync.dma_start(out=f_sb[2][:], in_=f_clu[2].rearrange("(q j) n -> q (j n)", j=PACK))
+        load_half(first_h[1], h_score[0], 1)
         nc.sync.dma_start(out=bias_bc[:], in_=b_s2.partition_broadcast(P))
-        nc.sync.dma_start(out=h_sb[1][:], in_=h_score[1].rearrange("(q j) n -> q (j n)", j=PACK))
-        nc.sync.dma_start(out=h_sb[2][:], in_=h_score[2].rearrange("(q j) n -> q (j n)", j=PACK))
+        load(h_sb[1], h_score[1])
+        load(f_sb[0], f_clu[0])
+        nc.sync.dma_start(out=par_bf[:], in_=burst_par.partition_broadcast(P))
+        load(f_sb[2], f_clu[2])
+        load(f_sb[1], f_clu[1])
+        load(h_sb[2], h_score[2])
 
         ident = const.tile([P, P], F32)
         make_identity(nc, ident[:])
         neg_half = const.tile([P, PACK], F32)
         nc.gpsimd.memset(neg_half[:], -0.5)
+        burst_terms = {}
+        for i in range(IMAGES):
+            for g in range(HALVES):
+                burst_terms[i, g] = kept.tile([P, len(PARTS), PACK], F32, name="burst_terms")
+                nc.gpsimd.memset(burst_terms[i, g][:], 0.0)
         warm = const.tile([P, 1], F32)
-        nc.scalar.activation(out=warm[:], in_=neg_half[:, 0:1], func=ACT.Sigmoid)
+        nc.scalar.activation(out=warm[:], in_=neg_half[:, 0:1], func=ACT.Exp)
         par = const.tile([P, 3], F32)
         nc.gpsimd.tensor_copy(out=par[:], in_=par_bf[:])
         slope = par[:, 0:1]
@@ -81,12 +94,12 @@ def tile_salad_pa_kernel(tc, f_clu, h_score, W_s2, b_s2, burst_par, out):
         exponent = par[:, 2:3]
 
         ft_grouped, ft_codes, ft_scales = {}, {}, {}
-        inv_norm, rn_bank = {}, {}
+        norm_bank, sums_of_squares, inv_norm, rn_bank = {}, {}, {}, {}
         fn_grouped, fn_codes, fn_scales = {}, {}, {}
         h_grouped, h_codes, h_scales = {}, {}, {}
         score_bank, logits, neg_max, expd, exp_sum = {}, {}, {}, {}, {}
-        row_sums, powered = {}, {}
-        pm_grouped, vt_bank, v_inv, out_bank = {}, {}, {}, {}
+        powered, sigmoids, col_bank = {}, {}, {}
+        weight, pm_grouped, pm_codes, pm_scales, vt_bank, v_inv, out_bank = {}, {}, {}, {}, {}, {}, {}
 
         w_codes = const.tile([P, CLUSTERS], U32, align_bytes=64)
         w_scales = const.tile([P, CLUSTERS], U8, align_bytes=64)
@@ -105,7 +118,7 @@ def tile_salad_pa_kernel(tc, f_clu, h_score, W_s2, b_s2, burst_par, out):
 
         def transpose_features(i, g):
             f_words = f_sb[i][:].bitcast(F32).rearrange("q (j g p u) -> q j g u p", j=PACK, g=HALVES, u=2)
-            ft_grouped[i, g] = work.tile([P, CHANNELS * PACK], BF16, name="ft_grouped", bufs=4, align_bytes=64)
+            ft_grouped[i, g] = work.tile([P, CHANNELS * PACK], BF16, name="ft_grouped", bufs=6, align_bytes=64)
             grouped_words = ft_grouped[i, g][:].bitcast(F32).rearrange("p (c u) -> p c u", u=2)
             for pair in range(2):
                 ft_ps = psum_work.tile([P, 2, 2, P], F32, name="bank")
@@ -119,33 +132,67 @@ def tile_salad_pa_kernel(tc, f_clu, h_score, W_s2, b_s2, burst_par, out):
                     in_=ft_ps[:].rearrange("p u jj q -> p (jj q) u"),
                 )
 
+        def on_tensor(i, g):
+            return i * HALVES + g < HALVES_ON_TENSOR
+
+        def products(i, g):
+            norm_bank[i, g] = psum_col.tile([P, PACK, P], F32, name="col_bank")
+            for r in range(PACK):
+                for j in range(PACK):
+                    first = j * PIXELS + g * PASS + r * P
+                    run = f_sb[i][:, first : first + P]
+                    nc.tensor.matmul(
+                        out=norm_bank[i, g][:, r, :], lhsT=run, rhs=run, start=(j == 0), stop=(j == PACK - 1)
+                    )
+
+        def squared_norms(i, g):
+            sum_sq = work.tile([P, PACK], F32, name="sum_sq", bufs=6)
+            if on_tensor(i, g):
+                for r in range(PACK):
+                    unread = scratch.tile([P, P], F32, name="masked")
+                    nc.vector.scalar_tensor_tensor(
+                        out=unread[:],
+                        in0=norm_bank[i, g][:, r, :],
+                        scalar=1.0,
+                        in1=ident[:],
+                        op0=ALU.mult,
+                        op1=ALU.mult,
+                        accum_out=sum_sq[:, r : r + 1],
+                    )
+            else:
+                by_tile = ft_grouped[i, g][:].rearrange("p (c t) -> p t c", t=PACK)
+                for t in range(PACK):
+                    unread = scratch.tile([P, CHANNELS], BF16, name="unread")
+                    nc.scalar.activation(
+                        out=unread[:], in_=by_tile[:, t, :], func=ACT.Square, accum_out=sum_sq[:, t : t + 1]
+                    )
+            sums_of_squares[i, g] = sum_sq
+
         def inverse_norms(i, g):
-            sum_sq = work.tile([P, PACK], F32, name="sum_sq")
-            by_tile = ft_grouped[i, g][:].rearrange("p (c t) -> p t c", t=PACK)
-            for t in range(PACK):
-                unread = scratch.tile([P, CHANNELS], BF16, name="unread")
-                nc.scalar.activation(
-                    out=unread[:], in_=by_tile[:, t, :], func=ACT.Square, accum_out=sum_sq[:, t : t + 1]
-                )
+            sum_sq = sums_of_squares[i, g]
             floored = work.tile([P, PACK], F32, name="floored")
             nc.gpsimd.tensor_scalar_max(out=floored[:], in0=sum_sq[:], scalar1=EPS_NORM_SQ)
-            inv_norm[i, g] = work.tile([P, PACK], F32, name="inv_norm", bufs=4)
+            inv_norm[i, g] = work.tile([P, PACK], F32, name="inv_norm", bufs=6)
             nc.gpsimd.tensor_tensor(out=inv_norm[i, g][:], in0=floored[:], in1=neg_half[:], op=ALU.pow)
 
         def spread_inverse_norms(i, g):
             rn_bank[i, g] = psum_rn.tile([P, PACK, P], F32, name="rn_bank")
-            for t in range(PACK):
+            for r in range(PACK):
                 nc.tensor.transpose(
-                    out=rn_bank[i, g][:, t, :], in_=inv_norm[i, g][:, t : t + 1].to_broadcast([P, P]), identity=ident[:]
+                    out=rn_bank[i, g][:, r, :], in_=inv_norm[i, g][:, r : r + 1].to_broadcast([P, P]), identity=ident[:]
                 )
 
         def normalise(i, g):
             f_view = f_sb[i][:].rearrange("q (j g p t) -> q g p j t", j=PACK, g=HALVES, t=PACK)
+            if on_tensor(i, g):
+                rn_view = rn_bank[i, g][:].rearrange("q r c -> q (r c)").rearrange("q (p t) -> q p t", t=PACK)
+            else:
+                rn_view = rn_bank[i, g][:].rearrange("q t p -> q p t")
             fn_grouped[i, g] = work.tile([P, PASS * PACK], BF16, name="fn_grouped", align_bytes=64)
             nc.vector.tensor_tensor(
                 out=fn_grouped[i, g][:].rearrange("q (t p j) -> q p j t", t=PACK, j=PACK),
                 in0=f_view[:, g],
-                in1=rn_bank[i, g][:].rearrange("q t p -> q p t").unsqueeze(2).to_broadcast([P, P, PACK, PACK]),
+                in1=rn_view.unsqueeze(2).to_broadcast([P, P, PACK, PACK]),
                 op=ALU.mult,
             )
 
@@ -165,11 +212,13 @@ def tile_salad_pa_kernel(tc, f_clu, h_score, W_s2, b_s2, burst_par, out):
             )
 
         def regroup_h(i, g):
-            h_view = h_sb[i][:].rearrange("q (j g p t) -> q g p j t", j=PACK, g=HALVES, t=PACK)
-            h_grouped[i, g] = work.tile([P, PASS * PACK], BF16, name="h_grouped", align_bytes=64)
-            nc.vector.tensor_copy(
-                out=h_grouped[i, g][:].rearrange("q (t p j) -> q p j t", t=PACK, j=PACK), in_=h_view[:, g]
-            )
+            if i == 0:
+                h_view = first_h[g][:].rearrange("q (j p t) -> q p j t", j=PACK, t=PACK)
+            else:
+                h_view = h_sb[i][:].rearrange("q (j g p t) -> q g p j t", j=PACK, g=HALVES, t=PACK)[:, g]
+            h_grouped[i, g] = work.tile([P, PASS * PACK], BF16, name="h_grouped", bufs=4, align_bytes=64)
+            copy = nc.scalar.copy if i == 1 else nc.vector.tensor_copy
+            copy(out=h_grouped[i, g][:].rearrange("q (t p j) -> q p j t", t=PACK, j=PACK), in_=h_view)
 
         def quantise_h(i, g):
             if g == 0:
@@ -180,7 +229,7 @@ def tile_salad_pa_kernel(tc, f_clu, h_score, W_s2, b_s2, burst_par, out):
             )
 
         def score_passes(i, g):
-            score_bank[i, g] = psum_work.tile([P, PACK, CLUSTERS], F32, name="bank")
+            score_bank[i, g] = psum_sim.tile([P, PACK, CLUSTERS], F32, name="sim_ps")
             for t in range(PACK):
                 cols = slice((g * PACK + t) * P, (g * PACK + t + 1) * P)
                 nc.tensor.matmul_mx(
@@ -206,82 +255,109 @@ def tile_salad_pa_kernel(tc, f_clu, h_score, W_s2, b_s2, burst_par, out):
             neg_max[i, g] = kept.tile([P, PACK], F32, name="neg_max")
             nc.vector.tensor_reduce(out=neg_max[i, g][:], in_=logits[i, g][:], axis=AX.X, op=ALU.max, negate=True)
 
-        def burst_sums(i, g, m):
-            if m == 0:
-                row_sums[i, g] = kept.tile([P, PACK * HALVES], F32, name="row_sums")
+        def burst_rows(i, part):
+            g, m = PARTS[part]
             for t in range(PACK):
+                first = t * P if m == g else 0
                 rows = slice((g * PACK + t) * P, (g * PACK + t + 1) * P)
                 sim_ps = psum_sim.tile([P, PASS], F32, name="sim_ps")
-                nc.tensor.matmul_mx(
-                    out=sim_ps[:],
-                    lhsT=fn_codes[i][:, rows].bitcast(FP8X4),
-                    lhsT_scale=fn_scales[i][:, rows],
-                    rhs=fn_codes[i][:, half(m)].bitcast(FP8X4),
-                    rhs_scale=fn_scales[i][:, half(m)],
-                    start=True,
-                    stop=True,
-                )
-                unread = scratch.tile([P, PASS], BF16, name="unread")
+                for lo, hi in {0: ((0, 4),), 1: ((1, 2), (2, 4)), 2: ((2, 4),), 3: ((3, 4),)}[first // P]:
+                    cols = slice(m * PASS + lo * P, m * PASS + hi * P)
+                    nc.tensor.matmul_mx(
+                        out=sim_ps[:, lo * P : hi * P],
+                        lhsT=fn_codes[i][:, rows].bitcast(FP8X4),
+                        lhsT_scale=fn_scales[i][:, rows],
+                        rhs=fn_codes[i][:, cols].bitcast(FP8X4),
+                        rhs_scale=fn_scales[i][:, cols],
+                        start=True,
+                        stop=True,
+                    )
+                sigmoids[i, g, m, t] = scratch.tile([P, PASS], F32, name="sigmoids", bufs=14)
                 nc.scalar.activation(
-                    out=unread[:],
-                    in_=sim_ps[:],
+                    out=sigmoids[i, g, m, t][:, first:],
+                    in_=sim_ps[:, first:],
                     func=ACT.Sigmoid,
                     scale=slope,
                     bias=offset,
-                    accum_out=row_sums[i, g][:, t * HALVES + m : t * HALVES + m + 1],
+                    accum_out=burst_terms[i, g][:, part, t : t + 1],
                 )
+
+        def mirror(i, part):
+            g, m = PARTS[part]
+            col_bank[i, part] = psum_col.tile([P, PACK, P], F32, name="col_bank")
+            for t in range(PACK):
+                rows = range(t if g == m else PACK)
+                for r in rows:
+                    nc.tensor.matmul(
+                        out=col_bank[i, part][:, t, :],
+                        lhsT=sigmoids[i, g, m, r][:, t * P : (t + 1) * P],
+                        rhs=ident[:],
+                        is_transpose=True,
+                        start=(r == 0),
+                        stop=(r == len(rows) - 1),
+                    )
+
+        def mirror_sums(i, part):
+            g, m = PARTS[part]
+            first = 1 if g == m else 0
+            place = {0: 2, 1: 1, 2: 0}[part]
+            nc.vector.tensor_reduce(
+                out=burst_terms[i, m][:, place, first:], in_=col_bank[i, part][:, first:, :], axis=AX.X, op=ALU.add
+            )
 
         def burst_power(i, g):
             burst = work.tile([P, PACK], F32, name="burst")
             nc.vector.tensor_reduce(
-                out=burst[:], in_=row_sums[i, g][:].rearrange("p (t m) -> p t m", m=HALVES), axis=AX.X, op=ALU.add
+                out=burst[:], in_=burst_terms[i, g][:].rearrange("p s t -> p t s"), axis=AX.X, op=ALU.add
             )
-            if g == 0:
-                powered[i] = kept.tile([P, TILES], F32, name="powered")
+            powered[i, g] = kept.tile([P, PACK], F32, name="powered")
             nc.gpsimd.tensor_tensor(
-                out=powered[i][:, g * PACK : (g + 1) * PACK],
-                in0=burst[:],
-                in1=exponent.to_broadcast([P, PACK]),
-                op=ALU.pow,
+                out=powered[i, g][:], in0=burst[:], in1=exponent.to_broadcast([P, PACK]), op=ALU.pow
             )
 
-        def softmax_numerators(i):
-            exp_sum[i] = kept.tile([P, TILES], F32, name="exp_sum")
-            for g in range(HALVES):
-                expd[i, g] = kept.tile([P, PACK, CLUSTERS], F32, name="expd")
-                for t in range(PACK):
-                    nc.scalar.activation(
-                        out=expd[i, g][:, t, :],
-                        in_=logits[i, g][:, t, :],
-                        func=ACT.Exp,
-                        bias=neg_max[i, g][:, t : t + 1],
-                        accum_out=exp_sum[i][:, g * PACK + t : g * PACK + t + 1],
-                    )
+        def softmax_numerators(i, g):
+            exp_sum[i, g] = kept.tile([P, PACK], F32, name="exp_sum")
+            expd[i, g] = kept.tile([P, PACK, CLUSTERS], F32, name="expd")
+            for t in range(PACK):
+                nc.scalar.activation(
+                    out=expd[i, g][:, t, :],
+                    in_=logits[i, g][:, t, :],
+                    func=ACT.Exp,
+                    bias=neg_max[i, g][:, t : t + 1],
+                    accum_out=exp_sum[i, g][:, t : t + 1],
+                )
+
+        def pixel_weights(i, g):
+            denom = work.tile([P, PACK], F32, name="denom")
+            nc.vector.scalar_tensor_tensor(
+                out=denom[:], in0=powered[i, g][:], scalar=EPS_DENOM, in1=exp_sum[i, g][:], op0=ALU.add, op1=ALU.mult
+            )
+            weight[i, g] = work.tile([P, PACK], F32, name="weight")
+            nc.vector.reciprocal(out=weight[i, g][:], in_=denom[:])
+
+        def scale_numerators(i, g):
+            pm_grouped[i, g] = work.tile([P, CLUSTERS * PACK], BF16, name="pm_grouped", align_bytes=64)
+            nc.vector.tensor_tensor(
+                out=pm_grouped[i, g][:].rearrange("p (k t) -> p k t", t=PACK),
+                in0=expd[i, g][:].rearrange("p t k -> p k t"),
+                in1=weight[i, g][:].unsqueeze(1).to_broadcast([P, CLUSTERS, PACK]),
+                op=ALU.mult,
+            )
+
+        def quantise_pm(i, g):
+            pm_codes[i, g] = work.tile([P, CLUSTERS], U32, name="pm_codes", align_bytes=64)
+            pm_scales[i, g] = work.tile([P, CLUSTERS], U8, name="pm_scales", align_bytes=64)
+            nc.vector.quantize_mx(
+                out=pm_codes[i, g][:].bitcast(FP8X4), scales=pm_scales[i, g][:], in_=pm_grouped[i, g][:]
+            )
 
         def aggregate(i):
-            denom = work.tile([P, TILES], F32, name="denom")
-            nc.vector.scalar_tensor_tensor(
-                out=denom[:], in0=powered[i][:], scalar=EPS_DENOM, in1=exp_sum[i][:], op0=ALU.add, op1=ALU.mult
-            )
-            weight = work.tile([P, TILES], F32, name="weight")
-            nc.vector.reciprocal(out=weight[:], in_=denom[:])
-            for g in range(HALVES):
-                pm_grouped[i, g] = work.tile([P, CLUSTERS * PACK], BF16, name="pm_grouped", align_bytes=64)
-                nc.vector.tensor_tensor(
-                    out=pm_grouped[i, g][:].rearrange("p (k t) -> p k t", t=PACK),
-                    in0=expd[i, g][:].rearrange("p t k -> p k t"),
-                    in1=weight[:, g * PACK : (g + 1) * PACK].unsqueeze(1).to_broadcast([P, CLUSTERS, PACK]),
-                    op=ALU.mult,
-                )
             vt_bank[i] = psum_work.tile([P, CHANNELS], F32, name="bank")
             for g in range(HALVES):
-                pm_codes = work.tile([P, CLUSTERS], U32, name="pm_codes", align_bytes=64)
-                pm_scales = work.tile([P, CLUSTERS], U8, name="pm_scales", align_bytes=64)
-                nc.vector.quantize_mx(out=pm_codes[:].bitcast(FP8X4), scales=pm_scales[:], in_=pm_grouped[i, g][:])
                 nc.tensor.matmul_mx(
                     out=vt_bank[i][:],
-                    lhsT=pm_codes[:].bitcast(FP8X4),
-                    lhsT_scale=pm_scales[:],
+                    lhsT=pm_codes[i, g][:].bitcast(FP8X4),
+                    lhsT_scale=pm_scales[i, g][:],
                     rhs=ft_codes[i, g][:].bitcast(FP8X4),
                     rhs_scale=ft_scales[i, g][:],
                     start=(g == 0),
@@ -309,54 +385,138 @@ def tile_salad_pa_kernel(tc, f_clu, h_score, W_s2, b_s2, burst_par, out):
             nc.scalar.copy(out=out_sb[:], in_=out_bank[i][:])
             nc.sync.dma_start(out=out[i].rearrange("(q j) k -> q j k", j=PACK), in_=out_sb[:])
 
-        def due(slot, lead):
-            x, odd = divmod(slot + lead, 2)
-            if odd or not 0 <= x < HALF_IMAGES:
-                return None
-            return divmod(x, HALVES)
+        def pm_stage(i):
+            for g in range(HALVES):
+                pixel_weights(i, g)
+            for g in range(HALVES):
+                scale_numerators(i, g)
+            for g in range(HALVES):
+                quantise_pm(i, g)
+            aggregate(i)
+            cluster_norms(i)
 
-        for slot in range(-LEAD_TRANSPOSE, UNITS + 1):
-            if 0 <= slot < UNITS:
-                i, rest = divmod(slot, HALVES * HALVES)
-                burst_sums(i, rest // HALVES, rest % HALVES)
-            if slot == 0:
-                prepare_weights()
-            stage = due(slot, LEAD_TRANSPOSE)
-            if stage:
-                transpose_features(*stage)
-            stage = due(slot, LEAD_SQUARES)
-            if stage:
-                inverse_norms(*stage)
-            stage = due(slot, LEAD_SPREAD)
-            if stage:
-                spread_inverse_norms(*stage)
-            stage = due(slot, LEAD_NORMALISE)
-            if stage:
-                normalise(*stage)
-                quantise_ft(*stage)
-                quantise_fn(*stage)
-            fresh = due(slot, 0)
-            scored = due(slot, -2)
-            if fresh:
-                regroup_h(*fresh)
-            if scored:
-                add_bias(*scored)
-            if fresh:
-                quantise_h(*fresh)
-            if scored:
-                negative_maxima(*scored)
-                burst_power(*scored)
-            stage = due(slot, -1)
-            if stage:
-                score_passes(*stage)
-
-        for i in range(IMAGES):
-            softmax_numerators(i)
-        for step in range(IMAGES + 2):
-            if step < IMAGES:
-                aggregate(step)
-                cluster_norms(step)
-            if 1 <= step <= IMAGES:
-                unit_columns(step - 1)
-            if step >= 2:
-                store(step - 2)
+        regroup_h(0, 0)
+        prepare_weights()
+        quantise_h(0, 0)
+        score_passes(0, 0)
+        regroup_h(0, 1)
+        add_bias(0, 0)
+        quantise_h(0, 1)
+        score_passes(0, 1)
+        regroup_h(1, 0)
+        regroup_h(1, 1)
+        negative_maxima(0, 0)
+        add_bias(0, 1)
+        products(0, 0)
+        quantise_h(1, 0)
+        score_passes(1, 0)
+        negative_maxima(0, 1)
+        softmax_numerators(0, 0)
+        softmax_numerators(0, 1)
+        squared_norms(0, 0)
+        inverse_norms(0, 0)
+        products(0, 1)
+        add_bias(1, 0)
+        transpose_features(2, 0)
+        quantise_h(1, 1)
+        score_passes(1, 1)
+        spread_inverse_norms(0, 0)
+        negative_maxima(1, 0)
+        squared_norms(0, 1)
+        inverse_norms(0, 1)
+        squared_norms(2, 0)
+        products(1, 0)
+        spread_inverse_norms(0, 1)
+        add_bias(1, 1)
+        negative_maxima(1, 1)
+        softmax_numerators(1, 0)
+        softmax_numerators(1, 1)
+        normalise(0, 0)
+        squared_norms(1, 0)
+        inverse_norms(1, 0)
+        products(1, 1)
+        quantise_fn(0, 0)
+        transpose_features(2, 1)
+        burst_rows(0, 0)
+        normalise(0, 1)
+        spread_inverse_norms(1, 0)
+        squared_norms(2, 1)
+        squared_norms(1, 1)
+        inverse_norms(1, 1)
+        inverse_norms(2, 0)
+        inverse_norms(2, 1)
+        quantise_fn(0, 1)
+        spread_inverse_norms(1, 1)
+        burst_rows(0, 1)
+        normalise(1, 0)
+        transpose_features(0, 0)
+        mirror(0, 0)
+        burst_rows(0, 2)
+        spread_inverse_norms(2, 0)
+        quantise_ft(2, 0)
+        quantise_fn(1, 0)
+        normalise(1, 1)
+        mirror_sums(0, 0)
+        mirror(0, 1)
+        transpose_features(0, 1)
+        burst_rows(1, 0)
+        quantise_fn(1, 1)
+        burst_power(0, 0)
+        spread_inverse_norms(2, 1)
+        normalise(2, 0)
+        mirror_sums(0, 1)
+        mirror(0, 2)
+        transpose_features(1, 0)
+        burst_rows(1, 1)
+        quantise_fn(2, 0)
+        normalise(2, 1)
+        mirror_sums(0, 2)
+        burst_power(0, 1)
+        mirror(1, 0)
+        burst_rows(1, 2)
+        quantise_fn(2, 1)
+        quantise_ft(0, 0)
+        transpose_features(1, 1)
+        mirror_sums(1, 0)
+        mirror(1, 1)
+        burst_rows(2, 0)
+        regroup_h(2, 0)
+        quantise_ft(0, 1)
+        burst_rows(2, 1)
+        pm_stage(0)
+        mirror_sums(1, 1)
+        mirror(1, 2)
+        burst_power(1, 0)
+        quantise_ft(2, 1)
+        mirror_sums(1, 2)
+        burst_power(1, 1)
+        mirror(2, 0)
+        burst_rows(2, 2)
+        regroup_h(2, 1)
+        quantise_h(2, 0)
+        score_passes(2, 0)
+        quantise_ft(1, 0)
+        quantise_ft(1, 1)
+        mirror_sums(2, 0)
+        mirror(2, 1)
+        unit_columns(0)
+        pm_stage(1)
+        quantise_h(2, 1)
+        score_passes(2, 1)
+        add_bias(2, 0)
+        mirror_sums(2, 1)
+        burst_power(2, 0)
+        negative_maxima(2, 0)
+        mirror(2, 2)
+        add_bias(2, 1)
+        store(0)
+        negative_maxima(2, 1)
+        mirror_sums(2, 2)
+        burst_power(2, 1)
+        softmax_numerators(2, 0)
+        softmax_numerators(2, 1)
+        unit_columns(1)
+        pm_stage(2)
+        store(1)
+        unit_columns(2)
+        store(2)

@@ -23,8 +23,8 @@ HALVES = PIXELS // PASS
 TILES = HALVES * PACK
 HALF_IMAGES = IMAGES * HALVES
 PARTS = ((0, 0), (0, 1), (1, 1))
-UNITS = IMAGES * len(PARTS)
-HALVES_ON_TENSOR = 4
+MIRRORED = 1
+HALVES_ON_TENSOR = 5
 EPS_NORM_SQ = 1e-24
 EPS_DENOM = 1e-6
 
@@ -39,19 +39,17 @@ def tile_salad_pa_kernel(tc, f_clu, h_score, W_s2, b_s2, burst_par, out):
         kept = stack.enter_context(tc.tile_pool(name="kept", bufs=IMAGES * HALVES))
         work = stack.enter_context(tc.tile_pool(name="work", bufs=2))
         scratch = stack.enter_context(tc.tile_pool(name="scratch", bufs=4))
-        psum_sim = stack.enter_context(tc.psum_pool(name="psum_sim", bufs=3))
-        psum_col = stack.enter_context(tc.psum_pool(name="psum_col", bufs=1))
+        psum_sim = stack.enter_context(tc.psum_pool(name="psum_sim", bufs=4))
         psum_rn = stack.enter_context(tc.psum_pool(name="psum_rn", bufs=2))
         psum_work = stack.enter_context(tc.psum_pool(name="psum_work", bufs=2))
-        ordered = {mybir.EngineType.DVE, mybir.EngineType.Activation, mybir.EngineType.Pool, mybir.EngineType.SP}
-        stack.enter_context(tc.manual_schedule(engines=ordered))
+        stack.enter_context(tc.manual_schedule())
 
         def half(g):
             return slice(g * PASS, (g + 1) * PASS)
 
-        f_sb = [inputs.tile([P, PACK * PIXELS], BF16, name="f_sb") for i in range(IMAGES)]
-        first_h = [inputs.tile([P, PACK * PASS], BF16, name="first_h") for g in range(HALVES)]
-        h_sb = [None] + [inputs.tile([P, PACK * PIXELS], BF16, name="h_sb") for i in range(1, IMAGES)]
+        first_f = [inputs.tile([P, PACK * PASS], BF16, name="first_f") for g in range(HALVES)]
+        f_sb = [None] + [inputs.tile([P, PACK * PIXELS], BF16, name="f_sb") for i in range(1, IMAGES)]
+        h_sb = [inputs.tile([P, PACK * PIXELS], BF16, name="h_sb") for i in range(IMAGES)]
         w_sb = const.tile([P, CHANNELS], BF16)
         par_bf = const.tile([P, 3], BF16)
         bias_bc = const.tile([P, CLUSTERS], BF16)
@@ -65,16 +63,21 @@ def tile_salad_pa_kernel(tc, f_clu, h_score, W_s2, b_s2, burst_par, out):
                 in_=source.rearrange("(q j) n -> q j n", j=PACK)[:, :, half(g)],
             )
 
-        load_half(first_h[0], h_score[0], 0)
-        nc.sync.dma_start(out=w_sb[:], in_=W_s2)
-        load_half(first_h[1], h_score[0], 1)
-        nc.sync.dma_start(out=bias_bc[:], in_=b_s2.partition_broadcast(P))
-        load(h_sb[1], h_score[1])
-        load(f_sb[0], f_clu[0])
+        load_half(first_f[0], f_clu[0], 0)
+        load_half(first_f[1], f_clu[0], 1)
         nc.sync.dma_start(out=par_bf[:], in_=burst_par.partition_broadcast(P))
+        nc.sync.dma_start(out=w_sb[:], in_=W_s2)
         load(f_sb[2], f_clu[2])
         load(f_sb[1], f_clu[1])
+        load(h_sb[0], h_score[0])
+        nc.sync.dma_start(out=bias_bc[:], in_=b_s2.partition_broadcast(P))
+        load(h_sb[1], h_score[1])
         load(h_sb[2], h_score[2])
+
+        def pixels_of(i, g, tiles, first):
+            if i == 0:
+                return first[g][:].rearrange("q (j n) -> q j n", j=PACK)
+            return tiles[i][:].rearrange("q (j n) -> q j n", j=PACK)[:, :, half(g)]
 
         ident = const.tile([P, P], F32)
         make_identity(nc, ident[:])
@@ -83,12 +86,10 @@ def tile_salad_pa_kernel(tc, f_clu, h_score, W_s2, b_s2, burst_par, out):
         burst_terms = {}
         for i in range(IMAGES):
             for g in range(HALVES):
-                burst_terms[i, g] = kept.tile([P, len(PARTS), PACK], F32, name="burst_terms")
-                nc.gpsimd.memset(burst_terms[i, g][:], 0.0)
+                burst_terms[i, g] = kept.tile([P, HALVES, PACK], F32, name="burst_terms")
         warm = const.tile([P, 1], F32)
-        nc.scalar.activation(out=warm[:], in_=neg_half[:, 0:1], func=ACT.Exp)
+        nc.scalar.activation(out=warm[:], in_=neg_half[:, 0:1], func=ACT.Sigmoid)
         par = const.tile([P, 3], F32)
-        nc.gpsimd.tensor_copy(out=par[:], in_=par_bf[:])
         slope = par[:, 0:1]
         offset = par[:, 1:2]
         exponent = par[:, 2:3]
@@ -98,13 +99,14 @@ def tile_salad_pa_kernel(tc, f_clu, h_score, W_s2, b_s2, burst_par, out):
         fn_grouped, fn_codes, fn_scales = {}, {}, {}
         h_grouped, h_codes, h_scales = {}, {}, {}
         score_bank, logits, neg_max, expd, exp_sum = {}, {}, {}, {}, {}
-        powered, sigmoids, col_bank = {}, {}, {}
+        powered, sigmoids, mirror_bank = {}, {}, {}
         weight, pm_grouped, pm_codes, pm_scales, vt_bank, v_inv, out_bank = {}, {}, {}, {}, {}, {}, {}
 
+        w_tiles = {}
         w_codes = const.tile([P, CLUSTERS], U32, align_bytes=64)
         w_scales = const.tile([P, CLUSTERS], U8, align_bytes=64)
 
-        def prepare_weights():
+        def prepare_weights_1():
             w_words = w_sb[:].bitcast(F32).rearrange("k (q u) -> k u q", u=2)
             w_ps = psum_work.tile([P, 2, CLUSTERS], F32, name="bank")
             for u in range(2):
@@ -114,10 +116,16 @@ def tile_salad_pa_kernel(tc, f_clu, h_score, W_s2, b_s2, burst_par, out):
                 out=w_grouped[:].bitcast(F32).rearrange("q (k u) -> q k u", u=2),
                 in_=w_ps[:].rearrange("q u k -> q k u"),
             )
-            nc.vector.quantize_mx(out=w_codes[:].bitcast(FP8X4), scales=w_scales[:], in_=w_grouped[:])
+            w_tiles["grouped"] = w_grouped
+
+        def prepare_weights_2():
+            nc.vector.quantize_mx(out=w_codes[:].bitcast(FP8X4), scales=w_scales[:], in_=w_tiles["grouped"][:])
 
         def transpose_features(i, g):
-            f_words = f_sb[i][:].bitcast(F32).rearrange("q (j g p u) -> q j g u p", j=PACK, g=HALVES, u=2)
+            if i == 0:
+                f_words = first_f[g][:].bitcast(F32).rearrange("q (j p u) -> q j u p", j=PACK, u=2)
+            else:
+                f_words = f_sb[i][:].bitcast(F32).rearrange("q (j g p u) -> q j g u p", j=PACK, g=HALVES, u=2)[:, :, g]
             ft_grouped[i, g] = work.tile([P, CHANNELS * PACK], BF16, name="ft_grouped", bufs=6, align_bytes=64)
             grouped_words = ft_grouped[i, g][:].bitcast(F32).rearrange("p (c u) -> p c u", u=2)
             for pair in range(2):
@@ -125,7 +133,7 @@ def tile_salad_pa_kernel(tc, f_clu, h_score, W_s2, b_s2, burst_par, out):
                 for u in range(2):
                     for jj in range(2):
                         nc.tensor.transpose(
-                            out=ft_ps[:, u, jj, :], in_=f_words[:, 2 * pair + jj, g, u, :], identity=ident[:]
+                            out=ft_ps[:, u, jj, :], in_=f_words[:, 2 * pair + jj, u, :], identity=ident[:]
                         )
                 nc.scalar.copy(
                     out=grouped_words[:, pair * 2 * P : (pair + 1) * 2 * P, :],
@@ -136,11 +144,10 @@ def tile_salad_pa_kernel(tc, f_clu, h_score, W_s2, b_s2, burst_par, out):
             return i * HALVES + g < HALVES_ON_TENSOR
 
         def products(i, g):
-            norm_bank[i, g] = psum_col.tile([P, PACK, P], F32, name="col_bank")
+            norm_bank[i, g] = psum_work.tile([P, PACK, P], F32, name="bank")
             for r in range(PACK):
                 for j in range(PACK):
-                    first = j * PIXELS + g * PASS + r * P
-                    run = f_sb[i][:, first : first + P]
+                    run = pixels_of(i, g, f_sb, first_f)[:, j, r * P : (r + 1) * P]
                     nc.tensor.matmul(
                         out=norm_bank[i, g][:, r, :], lhsT=run, rhs=run, start=(j == 0), stop=(j == PACK - 1)
                     )
@@ -183,7 +190,7 @@ def tile_salad_pa_kernel(tc, f_clu, h_score, W_s2, b_s2, burst_par, out):
                 )
 
         def normalise(i, g):
-            f_view = f_sb[i][:].rearrange("q (j g p t) -> q g p j t", j=PACK, g=HALVES, t=PACK)
+            f_view = pixels_of(i, g, f_sb, first_f).rearrange("q j (p t) -> q p j t", t=PACK)
             if on_tensor(i, g):
                 rn_view = rn_bank[i, g][:].rearrange("q r c -> q (r c)").rearrange("q (p t) -> q p t", t=PACK)
             else:
@@ -191,7 +198,7 @@ def tile_salad_pa_kernel(tc, f_clu, h_score, W_s2, b_s2, burst_par, out):
             fn_grouped[i, g] = work.tile([P, PASS * PACK], BF16, name="fn_grouped", align_bytes=64)
             nc.vector.tensor_tensor(
                 out=fn_grouped[i, g][:].rearrange("q (t p j) -> q p j t", t=PACK, j=PACK),
-                in0=f_view[:, g],
+                in0=f_view,
                 in1=rn_view.unsqueeze(2).to_broadcast([P, P, PACK, PACK]),
                 op=ALU.mult,
             )
@@ -212,12 +219,9 @@ def tile_salad_pa_kernel(tc, f_clu, h_score, W_s2, b_s2, burst_par, out):
             )
 
         def regroup_h(i, g):
-            if i == 0:
-                h_view = first_h[g][:].rearrange("q (j p t) -> q p j t", j=PACK, t=PACK)
-            else:
-                h_view = h_sb[i][:].rearrange("q (j g p t) -> q g p j t", j=PACK, g=HALVES, t=PACK)[:, g]
+            h_view = h_sb[i][:].rearrange("q (j g p t) -> q g p j t", j=PACK, g=HALVES, t=PACK)[:, g]
             h_grouped[i, g] = work.tile([P, PASS * PACK], BF16, name="h_grouped", bufs=4, align_bytes=64)
-            copy = nc.scalar.copy if i == 1 else nc.vector.tensor_copy
+            copy = nc.scalar.copy if i == 2 else nc.vector.tensor_copy
             copy(out=h_grouped[i, g][:].rearrange("q (t p j) -> q p j t", t=PACK, j=PACK), in_=h_view)
 
         def quantise_h(i, g):
@@ -229,7 +233,7 @@ def tile_salad_pa_kernel(tc, f_clu, h_score, W_s2, b_s2, burst_par, out):
             )
 
         def score_passes(i, g):
-            score_bank[i, g] = psum_sim.tile([P, PACK, CLUSTERS], F32, name="sim_ps")
+            score_bank[i, g] = psum_rn.tile([P, PACK, CLUSTERS], F32, name="rn_bank")
             for t in range(PACK):
                 cols = slice((g * PACK + t) * P, (g * PACK + t + 1) * P)
                 nc.tensor.matmul_mx(
@@ -258,57 +262,51 @@ def tile_salad_pa_kernel(tc, f_clu, h_score, W_s2, b_s2, burst_par, out):
         def burst_rows(i, part):
             g, m = PARTS[part]
             for t in range(PACK):
-                first = t * P if m == g else 0
                 rows = slice((g * PACK + t) * P, (g * PACK + t + 1) * P)
                 sim_ps = psum_sim.tile([P, PASS], F32, name="sim_ps")
-                for lo, hi in {0: ((0, 4),), 1: ((1, 2), (2, 4)), 2: ((2, 4),), 3: ((3, 4),)}[first // P]:
-                    cols = slice(m * PASS + lo * P, m * PASS + hi * P)
-                    nc.tensor.matmul_mx(
-                        out=sim_ps[:, lo * P : hi * P],
-                        lhsT=fn_codes[i][:, rows].bitcast(FP8X4),
-                        lhsT_scale=fn_scales[i][:, rows],
-                        rhs=fn_codes[i][:, cols].bitcast(FP8X4),
-                        rhs_scale=fn_scales[i][:, cols],
-                        start=True,
-                        stop=True,
-                    )
-                sigmoids[i, g, m, t] = scratch.tile([P, PASS], F32, name="sigmoids", bufs=14)
+                nc.tensor.matmul_mx(
+                    out=sim_ps[:],
+                    lhsT=fn_codes[i][:, rows].bitcast(FP8X4),
+                    lhsT_scale=fn_scales[i][:, rows],
+                    rhs=fn_codes[i][:, half(m)].bitcast(FP8X4),
+                    rhs_scale=fn_scales[i][:, half(m)],
+                    start=True,
+                    stop=True,
+                )
+                if part == MIRRORED:
+                    values = scratch.tile([P, PASS], F32, name="mirrored", bufs=2 * PACK)
+                    sigmoids[i, t] = values
+                else:
+                    values = scratch.tile([P, PASS], BF16, name="unread")
                 nc.scalar.activation(
-                    out=sigmoids[i, g, m, t][:, first:],
-                    in_=sim_ps[:, first:],
+                    out=values[:],
+                    in_=sim_ps[:],
                     func=ACT.Sigmoid,
                     scale=slope,
                     bias=offset,
-                    accum_out=burst_terms[i, g][:, part, t : t + 1],
+                    accum_out=burst_terms[i, g][:, m, t : t + 1],
                 )
 
-        def mirror(i, part):
-            g, m = PARTS[part]
-            col_bank[i, part] = psum_col.tile([P, PACK, P], F32, name="col_bank")
+        def mirror(i):
+            mirror_bank[i] = psum_work.tile([P, PACK, P], F32, name="bank")
             for t in range(PACK):
-                rows = range(t if g == m else PACK)
-                for r in rows:
+                for r in range(PACK):
                     nc.tensor.matmul(
-                        out=col_bank[i, part][:, t, :],
-                        lhsT=sigmoids[i, g, m, r][:, t * P : (t + 1) * P],
+                        out=mirror_bank[i][:, t, :],
+                        lhsT=sigmoids[i, r][:, t * P : (t + 1) * P],
                         rhs=ident[:],
                         is_transpose=True,
                         start=(r == 0),
-                        stop=(r == len(rows) - 1),
+                        stop=(r == PACK - 1),
                     )
 
-        def mirror_sums(i, part):
-            g, m = PARTS[part]
-            first = 1 if g == m else 0
-            place = {0: 2, 1: 1, 2: 0}[part]
-            nc.vector.tensor_reduce(
-                out=burst_terms[i, m][:, place, first:], in_=col_bank[i, part][:, first:, :], axis=AX.X, op=ALU.add
-            )
+        def mirror_sums(i):
+            nc.vector.tensor_reduce(out=burst_terms[i, 1][:, 0, :], in_=mirror_bank[i][:], axis=AX.X, op=ALU.add)
 
         def burst_power(i, g):
-            burst = work.tile([P, PACK], F32, name="burst")
+            burst = work.tile([P, PACK], F32, name="burst", bufs=6)
             nc.vector.tensor_reduce(
-                out=burst[:], in_=burst_terms[i, g][:].rearrange("p s t -> p t s"), axis=AX.X, op=ALU.add
+                out=burst[:], in_=burst_terms[i, g][:].rearrange("p m t -> p t m"), axis=AX.X, op=ALU.add
             )
             powered[i, g] = kept.tile([P, PACK], F32, name="powered")
             nc.gpsimd.tensor_tensor(
@@ -328,15 +326,15 @@ def tile_salad_pa_kernel(tc, f_clu, h_score, W_s2, b_s2, burst_par, out):
                 )
 
         def pixel_weights(i, g):
-            denom = work.tile([P, PACK], F32, name="denom")
+            denom = work.tile([P, PACK], F32, name="denom", bufs=4)
             nc.vector.scalar_tensor_tensor(
                 out=denom[:], in0=powered[i, g][:], scalar=EPS_DENOM, in1=exp_sum[i, g][:], op0=ALU.add, op1=ALU.mult
             )
-            weight[i, g] = work.tile([P, PACK], F32, name="weight")
+            weight[i, g] = work.tile([P, PACK], F32, name="weight", bufs=4)
             nc.vector.reciprocal(out=weight[i, g][:], in_=denom[:])
 
         def scale_numerators(i, g):
-            pm_grouped[i, g] = work.tile([P, CLUSTERS * PACK], BF16, name="pm_grouped", align_bytes=64)
+            pm_grouped[i, g] = work.tile([P, CLUSTERS * PACK], BF16, name="pm_grouped", bufs=4, align_bytes=64)
             nc.vector.tensor_tensor(
                 out=pm_grouped[i, g][:].rearrange("p (k t) -> p k t", t=PACK),
                 in0=expd[i, g][:].rearrange("p t k -> p k t"),
@@ -345,8 +343,8 @@ def tile_salad_pa_kernel(tc, f_clu, h_score, W_s2, b_s2, burst_par, out):
             )
 
         def quantise_pm(i, g):
-            pm_codes[i, g] = work.tile([P, CLUSTERS], U32, name="pm_codes", align_bytes=64)
-            pm_scales[i, g] = work.tile([P, CLUSTERS], U8, name="pm_scales", align_bytes=64)
+            pm_codes[i, g] = work.tile([P, CLUSTERS], U32, name="pm_codes", bufs=4, align_bytes=64)
+            pm_scales[i, g] = work.tile([P, CLUSTERS], U8, name="pm_scales", bufs=4, align_bytes=64)
             nc.vector.quantize_mx(
                 out=pm_codes[i, g][:].bitcast(FP8X4), scales=pm_scales[i, g][:], in_=pm_grouped[i, g][:]
             )
@@ -375,7 +373,10 @@ def tile_salad_pa_kernel(tc, f_clu, h_score, W_s2, b_s2, burst_par, out):
 
         def unit_columns(i):
             v_unit = work.tile([P, CHANNELS], F32, name="v_unit")
-            nc.scalar.activation(out=v_unit[:], in_=vt_bank[i][:], func=ACT.Copy, scale=v_inv[i][:])
+            if i == IMAGES - 1:
+                nc.vector.tensor_scalar_mul(out=v_unit[:], in0=vt_bank[i][:], scalar1=v_inv[i][:])
+            else:
+                nc.scalar.activation(out=v_unit[:], in_=vt_bank[i][:], func=ACT.Copy, scale=v_inv[i][:])
             out_bank[i] = psum_work.tile([P, PACK, CLUSTERS], F32, name="bank")
             for j in range(PACK):
                 nc.tensor.transpose(out=out_bank[i][:, j, :], in_=v_unit[:, j * P : (j + 1) * P], identity=ident[:])
@@ -393,130 +394,118 @@ def tile_salad_pa_kernel(tc, f_clu, h_score, W_s2, b_s2, burst_par, out):
             for g in range(HALVES):
                 quantise_pm(i, g)
             aggregate(i)
-            cluster_norms(i)
 
-        regroup_h(0, 0)
-        prepare_weights()
-        quantise_h(0, 0)
-        score_passes(0, 0)
-        regroup_h(0, 1)
-        add_bias(0, 0)
-        quantise_h(0, 1)
-        score_passes(0, 1)
-        regroup_h(1, 0)
-        regroup_h(1, 1)
-        negative_maxima(0, 0)
-        add_bias(0, 1)
-        products(0, 0)
-        quantise_h(1, 0)
-        score_passes(1, 0)
-        negative_maxima(0, 1)
-        softmax_numerators(0, 0)
-        softmax_numerators(0, 1)
-        squared_norms(0, 0)
-        inverse_norms(0, 0)
-        products(0, 1)
-        add_bias(1, 0)
-        transpose_features(2, 0)
-        quantise_h(1, 1)
-        score_passes(1, 1)
+        for g in range(HALVES):
+            products(0, g)
+            squared_norms(0, g)
+            inverse_norms(0, g)
+        nc.gpsimd.tensor_copy(out=par[:], in_=par_bf[:])
+        prepare_weights_1()
         spread_inverse_norms(0, 0)
-        negative_maxima(1, 0)
-        squared_norms(0, 1)
-        inverse_norms(0, 1)
-        squared_norms(2, 0)
-        products(1, 0)
         spread_inverse_norms(0, 1)
-        add_bias(1, 1)
-        negative_maxima(1, 1)
-        softmax_numerators(1, 0)
-        softmax_numerators(1, 1)
         normalise(0, 0)
+        products(1, 0)
+        prepare_weights_2()
+        quantise_fn(0, 0)
+        burst_rows(0, 0)
+        products(1, 1)
+        normalise(0, 1)
         squared_norms(1, 0)
         inverse_norms(1, 0)
-        products(1, 1)
-        quantise_fn(0, 0)
-        transpose_features(2, 1)
-        burst_rows(0, 0)
-        normalise(0, 1)
-        spread_inverse_norms(1, 0)
-        squared_norms(2, 1)
+        quantise_fn(0, 1)
+        burst_rows(0, 1)
         squared_norms(1, 1)
         inverse_norms(1, 1)
+        spread_inverse_norms(1, 0)
+        transpose_features(2, 1)
+        burst_rows(0, 2)
+        squared_norms(2, 1)
+        products(2, 0)
+        regroup_h(0, 0)
+        normalise(1, 0)
+        spread_inverse_norms(1, 1)
+        regroup_h(0, 1)
+        quantise_fn(1, 0)
+        burst_rows(1, 0)
+        mirror(0)
+        squared_norms(2, 0)
         inverse_norms(2, 0)
         inverse_norms(2, 1)
-        quantise_fn(0, 1)
-        spread_inverse_norms(1, 1)
-        burst_rows(0, 1)
-        normalise(1, 0)
-        transpose_features(0, 0)
-        mirror(0, 0)
-        burst_rows(0, 2)
-        spread_inverse_norms(2, 0)
-        quantise_ft(2, 0)
-        quantise_fn(1, 0)
         normalise(1, 1)
-        mirror_sums(0, 0)
-        mirror(0, 1)
-        transpose_features(0, 1)
-        burst_rows(1, 0)
+        quantise_h(0, 0)
         quantise_fn(1, 1)
-        burst_power(0, 0)
-        spread_inverse_norms(2, 1)
-        normalise(2, 0)
-        mirror_sums(0, 1)
-        mirror(0, 2)
-        transpose_features(1, 0)
+        spread_inverse_norms(2, 0)
         burst_rows(1, 1)
-        quantise_fn(2, 0)
-        normalise(2, 1)
-        mirror_sums(0, 2)
-        burst_power(0, 1)
-        mirror(1, 0)
+        mirror_sums(0)
+        regroup_h(1, 0)
         burst_rows(1, 2)
-        quantise_fn(2, 1)
-        quantise_ft(0, 0)
-        transpose_features(1, 1)
-        mirror_sums(1, 0)
-        mirror(1, 1)
-        burst_rows(2, 0)
         regroup_h(2, 0)
-        quantise_ft(0, 1)
+        quantise_h(0, 1)
+        score_passes(0, 0)
+        normalise(2, 0)
+        spread_inverse_norms(2, 1)
+        add_bias(0, 0)
+        quantise_fn(2, 0)
+        score_passes(0, 1)
+        burst_rows(2, 0)
+        mirror(1)
+        negative_maxima(0, 0)
+        regroup_h(1, 1)
+        normalise(2, 1)
+        add_bias(0, 1)
+        quantise_fn(2, 1)
         burst_rows(2, 1)
-        pm_stage(0)
-        mirror_sums(1, 1)
-        mirror(1, 2)
-        burst_power(1, 0)
-        quantise_ft(2, 1)
-        mirror_sums(1, 2)
-        burst_power(1, 1)
-        mirror(2, 0)
+        negative_maxima(0, 1)
+        mirror_sums(1)
+        quantise_h(1, 0)
         burst_rows(2, 2)
         regroup_h(2, 1)
+        score_passes(1, 0)
+        quantise_h(1, 1)
+        score_passes(1, 1)
+        mirror(2)
+        add_bias(1, 0)
         quantise_h(2, 0)
+        mirror_sums(2)
+        transpose_features(0, 0)
+        softmax_numerators(0, 0)
+        softmax_numerators(0, 1)
+        add_bias(1, 1)
+        negative_maxima(1, 0)
         score_passes(2, 0)
-        quantise_ft(1, 0)
-        quantise_ft(1, 1)
-        mirror_sums(2, 0)
-        mirror(2, 1)
-        unit_columns(0)
-        pm_stage(1)
         quantise_h(2, 1)
+        negative_maxima(1, 1)
+        transpose_features(0, 1)
         score_passes(2, 1)
+        for i in range(IMAGES):
+            for g in range(HALVES):
+                burst_power(i, g)
         add_bias(2, 0)
-        mirror_sums(2, 1)
-        burst_power(2, 0)
+        quantise_ft(0, 0)
         negative_maxima(2, 0)
-        mirror(2, 2)
         add_bias(2, 1)
-        store(0)
+        softmax_numerators(1, 0)
+        softmax_numerators(1, 1)
+        transpose_features(1, 0)
+        quantise_ft(0, 1)
         negative_maxima(2, 1)
-        mirror_sums(2, 2)
-        burst_power(2, 1)
         softmax_numerators(2, 0)
         softmax_numerators(2, 1)
-        unit_columns(1)
+        transpose_features(1, 1)
+        transpose_features(2, 0)
+        pm_stage(0)
+        cluster_norms(0)
+        quantise_ft(1, 0)
+        quantise_ft(1, 1)
+        unit_columns(0)
+        pm_stage(1)
+        cluster_norms(1)
+        store(0)
+        quantise_ft(2, 1)
+        quantise_ft(2, 0)
         pm_stage(2)
+        unit_columns(1)
+        cluster_norms(2)
         store(1)
         unit_columns(2)
         store(2)

@@ -67,9 +67,9 @@ def tile_salad_pa_kernel(tc, f_clu, h_score, W_s2, b_s2, burst_par, out):
         load_half(first_f[1], f_clu[0], 1)
         nc.sync.dma_start(out=par_bf[:], in_=burst_par.partition_broadcast(P))
         nc.sync.dma_start(out=w_sb[:], in_=W_s2)
-        load(f_sb[2], f_clu[2])
-        load(f_sb[1], f_clu[1])
         load(h_sb[0], h_score[0])
+        load(f_sb[1], f_clu[1])
+        load(f_sb[2], f_clu[2])
         nc.sync.dma_start(out=bias_bc[:], in_=b_s2.partition_broadcast(P))
         load(h_sb[1], h_score[1])
         load(h_sb[2], h_score[2])
@@ -85,8 +85,7 @@ def tile_salad_pa_kernel(tc, f_clu, h_score, W_s2, b_s2, burst_par, out):
         nc.gpsimd.memset(neg_half[:], -0.5)
         burst_terms = {}
         for i in range(IMAGES):
-            for g in range(HALVES):
-                burst_terms[i, g] = kept.tile([P, HALVES, PACK], F32, name="burst_terms")
+            burst_terms[i] = kept.tile([P, HALVES, TILES], F32, name="burst_terms")
         warm = const.tile([P, 1], F32)
         nc.scalar.activation(out=warm[:], in_=neg_half[:, 0:1], func=ACT.Sigmoid)
         par = const.tile([P, 3], F32)
@@ -100,7 +99,7 @@ def tile_salad_pa_kernel(tc, f_clu, h_score, W_s2, b_s2, burst_par, out):
         h_grouped, h_codes, h_scales = {}, {}, {}
         score_bank, logits, neg_max, expd, exp_sum = {}, {}, {}, {}, {}
         powered, sigmoids, mirror_bank = {}, {}, {}
-        weight, pm_grouped, pm_codes, pm_scales, vt_bank, v_inv, out_bank = {}, {}, {}, {}, {}, {}, {}
+        denominator, weight, pm_grouped, pm_codes, pm_scales, vt_bank, v_inv, v_unit, out_bank = {}, {}, {}, {}, {}, {}, {}, {}, {}
 
         w_tiles = {}
         w_codes = const.tile([P, CLUSTERS], U32, align_bytes=64)
@@ -221,7 +220,7 @@ def tile_salad_pa_kernel(tc, f_clu, h_score, W_s2, b_s2, burst_par, out):
         def regroup_h(i, g):
             h_view = h_sb[i][:].rearrange("q (j g p t) -> q g p j t", j=PACK, g=HALVES, t=PACK)[:, g]
             h_grouped[i, g] = work.tile([P, PASS * PACK], BF16, name="h_grouped", bufs=4, align_bytes=64)
-            copy = nc.scalar.copy if i == 2 else nc.vector.tensor_copy
+            copy = nc.scalar.copy if i * HALVES + g in (0, 4) else nc.vector.tensor_copy
             copy(out=h_grouped[i, g][:].rearrange("q (t p j) -> q p j t", t=PACK, j=PACK), in_=h_view)
 
         def quantise_h(i, g):
@@ -233,7 +232,7 @@ def tile_salad_pa_kernel(tc, f_clu, h_score, W_s2, b_s2, burst_par, out):
             )
 
         def score_passes(i, g):
-            score_bank[i, g] = psum_rn.tile([P, PACK, CLUSTERS], F32, name="rn_bank")
+            score_bank[i, g] = psum_sim.tile([P, PACK, CLUSTERS], F32, name="sim_ps")
             for t in range(PACK):
                 cols = slice((g * PACK + t) * P, (g * PACK + t + 1) * P)
                 nc.tensor.matmul_mx(
@@ -284,7 +283,7 @@ def tile_salad_pa_kernel(tc, f_clu, h_score, W_s2, b_s2, burst_par, out):
                     func=ACT.Sigmoid,
                     scale=slope,
                     bias=offset,
-                    accum_out=burst_terms[i, g][:, m, t : t + 1],
+                    accum_out=burst_terms[i][:, m, g * PACK + t : g * PACK + t + 1],
                 )
 
         def mirror(i):
@@ -301,20 +300,21 @@ def tile_salad_pa_kernel(tc, f_clu, h_score, W_s2, b_s2, burst_par, out):
                     )
 
         def mirror_sums(i):
-            nc.vector.tensor_reduce(out=burst_terms[i, 1][:, 0, :], in_=mirror_bank[i][:], axis=AX.X, op=ALU.add)
+            nc.vector.tensor_reduce(out=burst_terms[i][:, 0, PACK:], in_=mirror_bank[i][:], axis=AX.X, op=ALU.add)
 
-        def burst_power(i, g):
-            burst = work.tile([P, PACK], F32, name="burst", bufs=6)
+        def burst_power(i):
+            burst = work.tile([P, TILES], F32, name="burst", bufs=3)
             nc.vector.tensor_reduce(
-                out=burst[:], in_=burst_terms[i, g][:].rearrange("p m t -> p t m"), axis=AX.X, op=ALU.add
+                out=burst[:], in_=burst_terms[i][:].rearrange("p m t -> p t m"), axis=AX.X, op=ALU.add
             )
-            powered[i, g] = kept.tile([P, PACK], F32, name="powered")
+            powered[i] = kept.tile([P, TILES], F32, name="powered")
             nc.gpsimd.tensor_tensor(
-                out=powered[i, g][:], in0=burst[:], in1=exponent.to_broadcast([P, PACK]), op=ALU.pow
+                out=powered[i][:], in0=burst[:], in1=exponent.to_broadcast([P, TILES]), op=ALU.pow
             )
 
         def softmax_numerators(i, g):
-            exp_sum[i, g] = kept.tile([P, PACK], F32, name="exp_sum")
+            if g == 0:
+                exp_sum[i] = kept.tile([P, TILES], F32, name="exp_sum")
             expd[i, g] = kept.tile([P, PACK, CLUSTERS], F32, name="expd")
             for t in range(PACK):
                 nc.scalar.activation(
@@ -322,23 +322,26 @@ def tile_salad_pa_kernel(tc, f_clu, h_score, W_s2, b_s2, burst_par, out):
                     in_=logits[i, g][:, t, :],
                     func=ACT.Exp,
                     bias=neg_max[i, g][:, t : t + 1],
-                    accum_out=exp_sum[i, g][:, t : t + 1],
+                    accum_out=exp_sum[i][:, g * PACK + t : g * PACK + t + 1],
                 )
 
-        def pixel_weights(i, g):
-            denom = work.tile([P, PACK], F32, name="denom", bufs=4)
+        def denominators(i):
+            denom = work.tile([P, TILES], F32, name="denom")
             nc.vector.scalar_tensor_tensor(
-                out=denom[:], in0=powered[i, g][:], scalar=EPS_DENOM, in1=exp_sum[i, g][:], op0=ALU.add, op1=ALU.mult
+                out=denom[:], in0=powered[i][:], scalar=EPS_DENOM, in1=exp_sum[i][:], op0=ALU.add, op1=ALU.mult
             )
-            weight[i, g] = work.tile([P, PACK], F32, name="weight", bufs=4)
-            nc.vector.reciprocal(out=weight[i, g][:], in_=denom[:])
+            denominator[i] = denom
+
+        def pixel_weights(i):
+            weight[i] = work.tile([P, TILES], F32, name="weight")
+            nc.vector.reciprocal(out=weight[i][:], in_=denominator[i][:])
 
         def scale_numerators(i, g):
             pm_grouped[i, g] = work.tile([P, CLUSTERS * PACK], BF16, name="pm_grouped", bufs=4, align_bytes=64)
             nc.vector.tensor_tensor(
                 out=pm_grouped[i, g][:].rearrange("p (k t) -> p k t", t=PACK),
                 in0=expd[i, g][:].rearrange("p t k -> p k t"),
-                in1=weight[i, g][:].unsqueeze(1).to_broadcast([P, CLUSTERS, PACK]),
+                in1=weight[i][:, g * PACK : (g + 1) * PACK].unsqueeze(1).to_broadcast([P, CLUSTERS, PACK]),
                 op=ALU.mult,
             )
 
@@ -349,18 +352,18 @@ def tile_salad_pa_kernel(tc, f_clu, h_score, W_s2, b_s2, burst_par, out):
                 out=pm_codes[i, g][:].bitcast(FP8X4), scales=pm_scales[i, g][:], in_=pm_grouped[i, g][:]
             )
 
-        def aggregate(i):
-            vt_bank[i] = psum_work.tile([P, CHANNELS], F32, name="bank")
-            for g in range(HALVES):
-                nc.tensor.matmul_mx(
-                    out=vt_bank[i][:],
-                    lhsT=pm_codes[i, g][:].bitcast(FP8X4),
-                    lhsT_scale=pm_scales[i, g][:],
-                    rhs=ft_codes[i, g][:].bitcast(FP8X4),
-                    rhs_scale=ft_scales[i, g][:],
-                    start=(g == 0),
-                    stop=(g == HALVES - 1),
-                )
+        def aggregate(i, g):
+            if g == 0:
+                vt_bank[i] = psum_sim.tile([P, CHANNELS], F32, name="sim_ps")
+            nc.tensor.matmul_mx(
+                out=vt_bank[i][:],
+                lhsT=pm_codes[i, g][:].bitcast(FP8X4),
+                lhsT_scale=pm_scales[i, g][:],
+                rhs=ft_codes[i, g][:].bitcast(FP8X4),
+                rhs_scale=ft_scales[i, g][:],
+                start=(g == 0),
+                stop=(g == HALVES - 1),
+            )
 
         def cluster_norms(i):
             v_sq = work.tile([P, 1], F32, name="v_sq")
@@ -371,29 +374,46 @@ def tile_salad_pa_kernel(tc, f_clu, h_score, W_s2, b_s2, burst_par, out):
             v_inv[i] = work.tile([P, 1], F32, name="v_inv")
             nc.gpsimd.tensor_tensor(out=v_inv[i][:], in0=v_floored[:], in1=neg_half[:, 0:1], op=ALU.pow)
 
-        def unit_columns(i):
-            v_unit = work.tile([P, CHANNELS], F32, name="v_unit")
-            if i == IMAGES - 1:
-                nc.vector.tensor_scalar_mul(out=v_unit[:], in0=vt_bank[i][:], scalar1=v_inv[i][:])
-            else:
-                nc.scalar.activation(out=v_unit[:], in_=vt_bank[i][:], func=ACT.Copy, scale=v_inv[i][:])
-            out_bank[i] = psum_work.tile([P, PACK, CLUSTERS], F32, name="bank")
-            for j in range(PACK):
-                nc.tensor.transpose(out=out_bank[i][:, j, :], in_=v_unit[:, j * P : (j + 1) * P], identity=ident[:])
+        def scale_columns(i):
+            v_view = vt_bank[i][:].rearrange("k (j q) -> k j q", j=PACK)
+            for part in range(2):
+                groups = slice(2 * part, 2 * part + 2)
+                v_unit[i, part] = work.tile([P, 2, P], F32, name="v_unit", bufs=4)
+                if i == IMAGES - 1 and part == 0:
+                    nc.vector.tensor_scalar_mul(out=v_unit[i, part][:], in0=v_view[:, groups, :], scalar1=v_inv[i][:])
+                else:
+                    nc.scalar.activation(
+                        out=v_unit[i, part][:], in_=v_view[:, groups, :], func=ACT.Copy, scale=v_inv[i][:]
+                    )
+
+        def turn_columns(i):
+            for part in range(2):
+                out_bank[i, part] = psum_rn.tile([P, 2, CLUSTERS], F32, name="rn_bank")
+                for j in range(2):
+                    nc.tensor.transpose(
+                        out=out_bank[i, part][:, j, :], in_=v_unit[i, part][:, j, :], identity=ident[:]
+                    )
 
         def store(i):
-            out_sb = work.tile([P, PACK, CLUSTERS], F32, name="out_sb")
-            nc.scalar.copy(out=out_sb[:], in_=out_bank[i][:])
-            nc.sync.dma_start(out=out[i].rearrange("(q j) k -> q j k", j=PACK), in_=out_sb[:])
+            for part in range(2):
+                out_sb = work.tile([P, 2, CLUSTERS], F32, name="out_sb", bufs=4)
+                copy = nc.scalar.copy if part == 0 else nc.vector.tensor_copy
+                copy(out=out_sb[:], in_=out_bank[i, part][:])
+                nc.sync.dma_start(
+                    out=out[i].rearrange("(q j) k -> q j k", j=PACK)[:, 2 * part : 2 * part + 2, :], in_=out_sb[:]
+                )
 
-        def pm_stage(i):
-            for g in range(HALVES):
-                pixel_weights(i, g)
+
+        def pm_stage(i, first, second):
+            denominators(i)
+            quantise_ft(*first)
+            pixel_weights(i)
+            quantise_ft(*second)
             for g in range(HALVES):
                 scale_numerators(i, g)
             for g in range(HALVES):
                 quantise_pm(i, g)
-            aggregate(i)
+                aggregate(i, g)
 
         for g in range(HALVES):
             products(0, g)
@@ -401,13 +421,15 @@ def tile_salad_pa_kernel(tc, f_clu, h_score, W_s2, b_s2, burst_par, out):
             inverse_norms(0, g)
         nc.gpsimd.tensor_copy(out=par[:], in_=par_bf[:])
         prepare_weights_1()
+        regroup_h(0, 0)
         spread_inverse_norms(0, 0)
+        transpose_features(0, 0)
         spread_inverse_norms(0, 1)
         normalise(0, 0)
-        products(1, 0)
         prepare_weights_2()
         quantise_fn(0, 0)
         burst_rows(0, 0)
+        products(1, 0)
         products(1, 1)
         normalise(0, 1)
         squared_norms(1, 0)
@@ -421,91 +443,85 @@ def tile_salad_pa_kernel(tc, f_clu, h_score, W_s2, b_s2, burst_par, out):
         burst_rows(0, 2)
         squared_norms(2, 1)
         products(2, 0)
-        regroup_h(0, 0)
+        quantise_h(0, 0)
         normalise(1, 0)
         spread_inverse_norms(1, 1)
         regroup_h(0, 1)
         quantise_fn(1, 0)
-        burst_rows(1, 0)
-        mirror(0)
         squared_norms(2, 0)
         inverse_norms(2, 0)
         inverse_norms(2, 1)
+        burst_rows(1, 0)
+        mirror(0)
         normalise(1, 1)
-        quantise_h(0, 0)
+        quantise_h(0, 1)
         quantise_fn(1, 1)
         spread_inverse_norms(2, 0)
         burst_rows(1, 1)
         mirror_sums(0)
-        regroup_h(1, 0)
-        burst_rows(1, 2)
-        regroup_h(2, 0)
-        quantise_h(0, 1)
         score_passes(0, 0)
-        normalise(2, 0)
-        spread_inverse_norms(2, 1)
-        add_bias(0, 0)
-        quantise_fn(2, 0)
         score_passes(0, 1)
+        regroup_h(1, 0)
+        normalise(2, 0)
+        add_bias(0, 0)
+        add_bias(0, 1)
+        burst_rows(1, 2)
+        spread_inverse_norms(2, 1)
+        quantise_fn(2, 0)
+        regroup_h(2, 0)
         burst_rows(2, 0)
         mirror(1)
-        negative_maxima(0, 0)
+        quantise_h(1, 0)
         regroup_h(1, 1)
         normalise(2, 1)
-        add_bias(0, 1)
+        negative_maxima(0, 0)
         quantise_fn(2, 1)
-        burst_rows(2, 1)
         negative_maxima(0, 1)
+        burst_rows(2, 1)
         mirror_sums(1)
-        quantise_h(1, 0)
-        burst_rows(2, 2)
-        regroup_h(2, 1)
         score_passes(1, 0)
         quantise_h(1, 1)
+        add_bias(1, 0)
+        burst_rows(2, 2)
+        regroup_h(2, 1)
         score_passes(1, 1)
         mirror(2)
-        add_bias(1, 0)
+        negative_maxima(1, 0)
+        add_bias(1, 1)
         quantise_h(2, 0)
         mirror_sums(2)
-        transpose_features(0, 0)
+        transpose_features(0, 1)
+        score_passes(2, 0)
+        negative_maxima(1, 1)
+        quantise_h(2, 1)
+        score_passes(2, 1)
         softmax_numerators(0, 0)
         softmax_numerators(0, 1)
-        add_bias(1, 1)
-        negative_maxima(1, 0)
-        score_passes(2, 0)
-        quantise_h(2, 1)
-        negative_maxima(1, 1)
-        transpose_features(0, 1)
-        score_passes(2, 1)
-        for i in range(IMAGES):
-            for g in range(HALVES):
-                burst_power(i, g)
         add_bias(2, 0)
-        quantise_ft(0, 0)
+        transpose_features(1, 0)
+        for i in range(IMAGES):
+            burst_power(i)
         negative_maxima(2, 0)
         add_bias(2, 1)
         softmax_numerators(1, 0)
         softmax_numerators(1, 1)
-        transpose_features(1, 0)
-        quantise_ft(0, 1)
+        transpose_features(1, 1)
         negative_maxima(2, 1)
         softmax_numerators(2, 0)
         softmax_numerators(2, 1)
-        transpose_features(1, 1)
-        transpose_features(2, 0)
-        pm_stage(0)
+        pm_stage(0, (0, 0), (0, 1))
         cluster_norms(0)
-        quantise_ft(1, 0)
-        quantise_ft(1, 1)
-        unit_columns(0)
-        pm_stage(1)
+        transpose_features(2, 0)
+        pm_stage(1, (1, 0), (1, 1))
+        scale_columns(0)
         cluster_norms(1)
+        turn_columns(0)
+        pm_stage(2, (2, 1), (2, 0))
         store(0)
-        quantise_ft(2, 1)
-        quantise_ft(2, 0)
-        pm_stage(2)
-        unit_columns(1)
+        scale_columns(1)
         cluster_norms(2)
+        turn_columns(1)
+        scale_columns(2)
         store(1)
-        unit_columns(2)
+        turn_columns(2)
         store(2)

@@ -122,9 +122,9 @@ def tile_salad_pa_kernel(tc, f_clu, h_score, W_s2, b_s2, burst_par, out):
 
         def transpose_features(i, g):
             if i == 0:
-                f_words = first_f[g][:].bitcast(F32).rearrange("q (j p u) -> q j u p", j=PACK, u=2)
+                f_words = first_f[g][:].bitcast(F32).rearrange("q (j u p) -> q j u p", j=PACK, u=2)
             else:
-                f_words = f_sb[i][:].bitcast(F32).rearrange("q (j g p u) -> q j g u p", j=PACK, g=HALVES, u=2)[:, :, g]
+                f_words = f_sb[i][:].bitcast(F32).rearrange("q (j g u p) -> q j g u p", j=PACK, g=HALVES, u=2)[:, :, g]
             ft_grouped[i, g] = work.tile([P, CHANNELS * PACK], BF16, name="ft_grouped", bufs=6, align_bytes=64)
             grouped_words = ft_grouped[i, g][:].bitcast(F32).rearrange("p (c u) -> p c u", u=2)
             for pair in range(2):
@@ -166,11 +166,11 @@ def tile_salad_pa_kernel(tc, f_clu, h_score, W_s2, b_s2, burst_par, out):
                         accum_out=sum_sq[:, r : r + 1],
                     )
             else:
-                by_tile = ft_grouped[i, g][:].rearrange("p (c t) -> p t c", t=PACK)
+                by_tile = ft_grouped[i, g][:].rearrange("p (c u e) -> p e u c", u=2, e=2)
                 for t in range(PACK):
                     unread = scratch.tile([P, CHANNELS], BF16, name="unread")
                     nc.scalar.activation(
-                        out=unread[:], in_=by_tile[:, t, :], func=ACT.Square, accum_out=sum_sq[:, t : t + 1]
+                        out=unread[:], in_=by_tile[:, t // 2, t % 2, :], func=ACT.Square, accum_out=sum_sq[:, t : t + 1]
                     )
             sums_of_squares[i, g] = sum_sq
 
@@ -189,16 +189,18 @@ def tile_salad_pa_kernel(tc, f_clu, h_score, W_s2, b_s2, burst_par, out):
                 )
 
         def normalise(i, g):
-            f_view = pixels_of(i, g, f_sb, first_f).rearrange("q j (p t) -> q p j t", t=PACK)
+            pairs = PASS // 2
+            f_view = pixels_of(i, g, f_sb, first_f).rearrange("q j (w e) -> q w j e", e=2)
+            columns = rn_bank[i, g][:].rearrange("q r c -> q (r c)")
             if on_tensor(i, g):
-                rn_view = rn_bank[i, g][:].rearrange("q r c -> q (r c)").rearrange("q (p t) -> q p t", t=PACK)
+                rn_view = columns.rearrange("q (w e) -> q w e", e=2)
             else:
-                rn_view = rn_bank[i, g][:].rearrange("q t p -> q p t")
+                rn_view = columns.rearrange("q (e w) -> q w e", e=2)
             fn_grouped[i, g] = work.tile([P, PASS * PACK], BF16, name="fn_grouped", align_bytes=64)
             nc.vector.tensor_tensor(
-                out=fn_grouped[i, g][:].rearrange("q (t p j) -> q p j t", t=PACK, j=PACK),
+                out=fn_grouped[i, g][:].rearrange("q (e w j) -> q w j e", e=2, j=PACK),
                 in0=f_view,
-                in1=rn_view.unsqueeze(2).to_broadcast([P, P, PACK, PACK]),
+                in1=rn_view.unsqueeze(2).to_broadcast([P, pairs, PACK, 2]),
                 op=ALU.mult,
             )
 
@@ -218,10 +220,10 @@ def tile_salad_pa_kernel(tc, f_clu, h_score, W_s2, b_s2, burst_par, out):
             )
 
         def regroup_h(i, g):
-            h_view = h_sb[i][:].rearrange("q (j g p t) -> q g p j t", j=PACK, g=HALVES, t=PACK)[:, g]
+            h_view = h_sb[i][:].rearrange("q (j g w e) -> q g w j e", j=PACK, g=HALVES, e=2)[:, g]
             h_grouped[i, g] = work.tile([P, PASS * PACK], BF16, name="h_grouped", bufs=4, align_bytes=64)
             copy = nc.scalar.copy if i * HALVES + g in (0, 4) else nc.vector.tensor_copy
-            copy(out=h_grouped[i, g][:].rearrange("q (t p j) -> q p j t", t=PACK, j=PACK), in_=h_view)
+            copy(out=h_grouped[i, g][:].rearrange("q (e w j) -> q w j e", e=2, j=PACK), in_=h_view)
 
         def quantise_h(i, g):
             if g == 0:
@@ -339,9 +341,12 @@ def tile_salad_pa_kernel(tc, f_clu, h_score, W_s2, b_s2, burst_par, out):
         def scale_numerators(i, g):
             pm_grouped[i, g] = work.tile([P, CLUSTERS * PACK], BF16, name="pm_grouped", bufs=4, align_bytes=64)
             nc.vector.tensor_tensor(
-                out=pm_grouped[i, g][:].rearrange("p (k t) -> p k t", t=PACK),
-                in0=expd[i, g][:].rearrange("p t k -> p k t"),
-                in1=weight[i][:, g * PACK : (g + 1) * PACK].unsqueeze(1).to_broadcast([P, CLUSTERS, PACK]),
+                out=pm_grouped[i, g][:].rearrange("p (k u e) -> p k u e", u=2, e=2),
+                in0=expd[i, g][:].rearrange("p (e u) k -> p k u e", e=2),
+                in1=weight[i][:, g * PACK : (g + 1) * PACK]
+                .rearrange("p (e u) -> p u e", e=2)
+                .unsqueeze(1)
+                .to_broadcast([P, CLUSTERS, 2, 2]),
                 op=ALU.mult,
             )
 

@@ -222,7 +222,7 @@ def tile_salad_pa_kernel(tc, f_clu, h_score, W_s2, b_s2, burst_par, out):
         def regroup_h(i, g):
             h_view = h_sb[i][:].rearrange("q (j g w e) -> q g w j e", j=PACK, g=HALVES, e=2)[:, g]
             h_grouped[i, g] = work.tile([P, PASS * PACK], BF16, name="h_grouped", bufs=4, align_bytes=64)
-            copy = nc.scalar.copy if i * HALVES + g in (0, 4) else nc.vector.tensor_copy
+            copy = nc.scalar.copy if i * HALVES + g in (0, 1, 4) else nc.vector.tensor_copy
             copy(out=h_grouped[i, g][:].rearrange("q (e w j) -> q w j e", e=2, j=PACK), in_=h_view)
 
         def quantise_h(i, g):
@@ -409,11 +409,7 @@ def tile_salad_pa_kernel(tc, f_clu, h_score, W_s2, b_s2, burst_par, out):
                 )
 
 
-        def pm_stage(i, first, second):
-            denominators(i)
-            quantise_ft(*first)
-            pixel_weights(i)
-            quantise_ft(*second)
+        def pmat(i):
             for g in range(HALVES):
                 scale_numerators(i, g)
             for g in range(HALVES):
@@ -433,17 +429,18 @@ def tile_salad_pa_kernel(tc, f_clu, h_score, W_s2, b_s2, burst_par, out):
         normalise(0, 0)
         prepare_weights_2()
         quantise_fn(0, 0)
-        burst_rows(0, 0)
         products(1, 0)
-        products(1, 1)
-        normalise(0, 1)
+        burst_rows(0, 0)
+        regroup_h(0, 1)
         squared_norms(1, 0)
         inverse_norms(1, 0)
-        quantise_fn(0, 1)
-        burst_rows(0, 1)
+        products(1, 1)
+        normalise(0, 1)
         squared_norms(1, 1)
         inverse_norms(1, 1)
         spread_inverse_norms(1, 0)
+        quantise_fn(0, 1)
+        burst_rows(0, 1)
         transpose_features(2, 1)
         burst_rows(0, 2)
         squared_norms(2, 1)
@@ -451,7 +448,7 @@ def tile_salad_pa_kernel(tc, f_clu, h_score, W_s2, b_s2, burst_par, out):
         quantise_h(0, 0)
         normalise(1, 0)
         spread_inverse_norms(1, 1)
-        regroup_h(0, 1)
+        quantise_h(0, 1)
         quantise_fn(1, 0)
         squared_norms(2, 0)
         inverse_norms(2, 0)
@@ -459,15 +456,15 @@ def tile_salad_pa_kernel(tc, f_clu, h_score, W_s2, b_s2, burst_par, out):
         burst_rows(1, 0)
         mirror(0)
         normalise(1, 1)
-        quantise_h(0, 1)
+        regroup_h(1, 0)
         quantise_fn(1, 1)
         spread_inverse_norms(2, 0)
         burst_rows(1, 1)
         mirror_sums(0)
         score_passes(0, 0)
         score_passes(0, 1)
-        regroup_h(1, 0)
         normalise(2, 0)
+        burst_power(0)
         add_bias(0, 0)
         add_bias(0, 1)
         burst_rows(1, 2)
@@ -484,44 +481,56 @@ def tile_salad_pa_kernel(tc, f_clu, h_score, W_s2, b_s2, burst_par, out):
         negative_maxima(0, 1)
         burst_rows(2, 1)
         mirror_sums(1)
-        score_passes(1, 0)
         quantise_h(1, 1)
+        score_passes(1, 0)
+        burst_power(1)
+        regroup_h(2, 1)
         add_bias(1, 0)
         burst_rows(2, 2)
-        regroup_h(2, 1)
         score_passes(1, 1)
         mirror(2)
+        quantise_h(2, 0)
         negative_maxima(1, 0)
         add_bias(1, 1)
-        quantise_h(2, 0)
         mirror_sums(2)
-        transpose_features(0, 1)
         score_passes(2, 0)
-        negative_maxima(1, 1)
-        quantise_h(2, 1)
-        score_passes(2, 1)
         softmax_numerators(0, 0)
         softmax_numerators(0, 1)
+        transpose_features(0, 1)
+        quantise_h(2, 1)
+        negative_maxima(1, 1)
+        burst_power(2)
+        score_passes(2, 1)
         add_bias(2, 0)
         transpose_features(1, 0)
-        for i in range(IMAGES):
-            burst_power(i)
+        quantise_ft(0, 0)
         negative_maxima(2, 0)
         add_bias(2, 1)
+        denominators(0)
         softmax_numerators(1, 0)
         softmax_numerators(1, 1)
         transpose_features(1, 1)
+        quantise_ft(0, 1)
         negative_maxima(2, 1)
         softmax_numerators(2, 0)
         softmax_numerators(2, 1)
-        pm_stage(0, (0, 0), (0, 1))
+        pixel_weights(0)
+        quantise_ft(1, 0)
+        pmat(0)
         cluster_norms(0)
         transpose_features(2, 0)
-        pm_stage(1, (1, 0), (1, 1))
+        denominators(1)
+        quantise_ft(1, 1)
+        pixel_weights(1)
+        quantise_ft(2, 1)
+        pmat(1)
         scale_columns(0)
         cluster_norms(1)
         turn_columns(0)
-        pm_stage(2, (2, 1), (2, 0))
+        denominators(2)
+        quantise_ft(2, 0)
+        pixel_weights(2)
+        pmat(2)
         store(0)
         scale_columns(1)
         cluster_norms(2)

@@ -47,7 +47,10 @@ def tile_salad_pa_kernel(tc, f_clu, h_score, W_s2, b_s2, burst_par, out):
         def half(g):
             return slice(g * PASS, (g + 1) * PASS)
 
-        first_f = [inputs.tile([P, PACK * PASS], BF16, name="first_f") for g in range(HALVES)]
+        first_f = [
+            inputs.tile([P, PACK, n], BF16, name=name)
+            for n, name in ((PASS // 2, "first_a"), (PASS // 2, "first_b"), (PASS, "first_c"))
+        ]
         f_sb = [None] + [inputs.tile([P, PACK * PIXELS], BF16, name="f_sb") for i in range(1, IMAGES)]
         h_sb = [inputs.tile([P, PACK * PIXELS], BF16, name="h_sb") for i in range(IMAGES)]
         w_sb = const.tile([P, CHANNELS], BF16)
@@ -57,14 +60,12 @@ def tile_salad_pa_kernel(tc, f_clu, h_score, W_s2, b_s2, burst_par, out):
         def load(tile, source):
             nc.sync.dma_start(out=tile[:], in_=source.rearrange("(q j) n -> q (j n)", j=PACK))
 
-        def load_half(tile, source, g):
-            nc.sync.dma_start(
-                out=tile[:].rearrange("q (j n) -> q j n", j=PACK),
-                in_=source.rearrange("(q j) n -> q j n", j=PACK)[:, :, half(g)],
-            )
-
-        load_half(first_f[0], f_clu[0], 0)
-        load_half(first_f[1], f_clu[0], 1)
+        first_pixel = 0
+        for piece in first_f:
+            n = piece[:].shape[2]
+            columns = slice(first_pixel, first_pixel + n)
+            nc.sync.dma_start(out=piece[:], in_=f_clu[0].rearrange("(q j) n -> q j n", j=PACK)[:, :, columns])
+            first_pixel += n
         nc.sync.dma_start(out=par_bf[:], in_=burst_par.partition_broadcast(P))
         nc.sync.dma_start(out=w_sb[:], in_=W_s2)
         load(h_sb[0], h_score[0])
@@ -74,10 +75,10 @@ def tile_salad_pa_kernel(tc, f_clu, h_score, W_s2, b_s2, burst_par, out):
         load(h_sb[1], h_score[1])
         load(h_sb[2], h_score[2])
 
-        def pixels_of(i, g, tiles, first):
+        def features(i, g):
             if i == 0:
-                return first[g][:].rearrange("q (j n) -> q j n", j=PACK)
-            return tiles[i][:].rearrange("q (j n) -> q j n", j=PACK)[:, :, half(g)]
+                return [piece[:] for piece in (first_f[:2] if g == 0 else first_f[2:])]
+            return [f_sb[i][:].rearrange("q (j n) -> q j n", j=PACK)[:, :, half(g)]]
 
         ident = const.tile([P, P], F32)
         make_identity(nc, ident[:])
@@ -121,18 +122,22 @@ def tile_salad_pa_kernel(tc, f_clu, h_score, W_s2, b_s2, burst_par, out):
             nc.vector.quantize_mx(out=w_codes[:].bitcast(FP8X4), scales=w_scales[:], in_=w_tiles["grouped"][:])
 
         def transpose_features(i, g):
-            if i == 0:
-                f_words = first_f[g][:].bitcast(F32).rearrange("q (j u p) -> q j u p", j=PACK, u=2)
-            else:
-                f_words = f_sb[i][:].bitcast(F32).rearrange("q (j g u p) -> q j g u p", j=PACK, g=HALVES, u=2)[:, :, g]
+            f_words = [
+                words[:, :, first : first + P]
+                for words in (piece.bitcast(F32) for piece in features(i, g))
+                for first in range(0, words.shape[2], P)
+            ]
             ft_grouped[i, g] = work.tile([P, CHANNELS * PACK], BF16, name="ft_grouped", bufs=6, align_bytes=64)
             grouped_words = ft_grouped[i, g][:].bitcast(F32).rearrange("p (c u) -> p c u", u=2)
             for pair in range(2):
-                ft_ps = psum_work.tile([P, 2, 2, P], F32, name="bank")
+                if i == 0:
+                    ft_ps = psum_sim.tile([P, 2, 2, P], F32, name="sim_ps")
+                else:
+                    ft_ps = psum_work.tile([P, 2, 2, P], F32, name="bank")
                 for u in range(2):
                     for jj in range(2):
                         nc.tensor.transpose(
-                            out=ft_ps[:, u, jj, :], in_=f_words[:, 2 * pair + jj, u, :], identity=ident[:]
+                            out=ft_ps[:, u, jj, :], in_=f_words[u][:, 2 * pair + jj, :], identity=ident[:]
                         )
                 nc.scalar.copy(
                     out=grouped_words[:, pair * 2 * P : (pair + 1) * 2 * P, :],
@@ -144,9 +149,12 @@ def tile_salad_pa_kernel(tc, f_clu, h_score, W_s2, b_s2, burst_par, out):
 
         def products(i, g):
             norm_bank[i, g] = psum_work.tile([P, PACK, P], F32, name="bank")
+            runs = [
+                piece[:, :, first : first + P] for piece in features(i, g) for first in range(0, piece.shape[2], P)
+            ]
             for r in range(PACK):
                 for j in range(PACK):
-                    run = pixels_of(i, g, f_sb, first_f)[:, j, r * P : (r + 1) * P]
+                    run = runs[r][:, j, :]
                     nc.tensor.matmul(
                         out=norm_bank[i, g][:, r, :], lhsT=run, rhs=run, start=(j == 0), stop=(j == PACK - 1)
                     )
@@ -189,20 +197,23 @@ def tile_salad_pa_kernel(tc, f_clu, h_score, W_s2, b_s2, burst_par, out):
                 )
 
         def normalise(i, g):
-            pairs = PASS // 2
-            f_view = pixels_of(i, g, f_sb, first_f).rearrange("q j (w e) -> q w j e", e=2)
             columns = rn_bank[i, g][:].rearrange("q r c -> q (r c)")
             if on_tensor(i, g):
                 rn_view = columns.rearrange("q (w e) -> q w e", e=2)
             else:
                 rn_view = columns.rearrange("q (e w) -> q w e", e=2)
             fn_grouped[i, g] = work.tile([P, PASS * PACK], BF16, name="fn_grouped", align_bytes=64)
-            nc.vector.tensor_tensor(
-                out=fn_grouped[i, g][:].rearrange("q (e w j) -> q w j e", e=2, j=PACK),
-                in0=f_view,
-                in1=rn_view.unsqueeze(2).to_broadcast([P, pairs, PACK, 2]),
-                op=ALU.mult,
-            )
+            fn_view = fn_grouped[i, g][:].rearrange("q (e w j) -> q w j e", e=2, j=PACK)
+            pieces = features(i, g)
+            pairs = PASS // 2 // len(pieces)
+            for n, piece in enumerate(pieces):
+                w = slice(n * pairs, (n + 1) * pairs)
+                nc.vector.tensor_tensor(
+                    out=fn_view[:, w],
+                    in0=piece.rearrange("q j (w e) -> q w j e", e=2),
+                    in1=rn_view[:, w].unsqueeze(2).to_broadcast([P, pairs, PACK, 2]),
+                    op=ALU.mult,
+                )
 
         def quantise_fn(i, g):
             if g == 0:
@@ -222,7 +233,7 @@ def tile_salad_pa_kernel(tc, f_clu, h_score, W_s2, b_s2, burst_par, out):
         def regroup_h(i, g):
             h_view = h_sb[i][:].rearrange("q (j g w e) -> q g w j e", j=PACK, g=HALVES, e=2)[:, g]
             h_grouped[i, g] = work.tile([P, PASS * PACK], BF16, name="h_grouped", bufs=4, align_bytes=64)
-            copy = nc.scalar.copy if i * HALVES + g in (0, 1, 4) else nc.vector.tensor_copy
+            copy = nc.scalar.copy if i * HALVES + g in (1, 2, 4) else nc.vector.tensor_copy
             copy(out=h_grouped[i, g][:].rearrange("q (e w j) -> q w j e", e=2, j=PACK), in_=h_view)
 
         def quantise_h(i, g):
@@ -423,50 +434,52 @@ def tile_salad_pa_kernel(tc, f_clu, h_score, W_s2, b_s2, burst_par, out):
         nc.gpsimd.tensor_copy(out=par[:], in_=par_bf[:])
         prepare_weights_1()
         regroup_h(0, 0)
+        regroup_h(0, 1)
         spread_inverse_norms(0, 0)
         transpose_features(0, 0)
         spread_inverse_norms(0, 1)
+        transpose_features(0, 1)
         normalise(0, 0)
         prepare_weights_2()
         quantise_fn(0, 0)
-        products(1, 0)
         burst_rows(0, 0)
-        regroup_h(0, 1)
-        squared_norms(1, 0)
-        inverse_norms(1, 0)
+        regroup_h(1, 0)
+        products(1, 0)
         products(1, 1)
         normalise(0, 1)
+        squared_norms(1, 0)
+        inverse_norms(1, 0)
+        products(2, 0)
         squared_norms(1, 1)
         inverse_norms(1, 1)
         spread_inverse_norms(1, 0)
         quantise_fn(0, 1)
         burst_rows(0, 1)
+        squared_norms(2, 0)
+        inverse_norms(2, 0)
+        spread_inverse_norms(1, 1)
         transpose_features(2, 1)
         burst_rows(0, 2)
         squared_norms(2, 1)
-        products(2, 0)
+        inverse_norms(2, 1)
         quantise_h(0, 0)
         normalise(1, 0)
-        spread_inverse_norms(1, 1)
+        spread_inverse_norms(2, 0)
         quantise_h(0, 1)
         quantise_fn(1, 0)
-        squared_norms(2, 0)
-        inverse_norms(2, 0)
-        inverse_norms(2, 1)
         burst_rows(1, 0)
         mirror(0)
         normalise(1, 1)
-        regroup_h(1, 0)
+        quantise_ft(0, 0)
         quantise_fn(1, 1)
-        spread_inverse_norms(2, 0)
-        burst_rows(1, 1)
-        mirror_sums(0)
         score_passes(0, 0)
         score_passes(0, 1)
         normalise(2, 0)
-        burst_power(0)
+        mirror_sums(0)
         add_bias(0, 0)
         add_bias(0, 1)
+        burst_rows(1, 1)
+        burst_power(0)
         burst_rows(1, 2)
         spread_inverse_norms(2, 1)
         quantise_fn(2, 0)
@@ -492,33 +505,31 @@ def tile_salad_pa_kernel(tc, f_clu, h_score, W_s2, b_s2, burst_par, out):
         quantise_h(2, 0)
         negative_maxima(1, 0)
         add_bias(1, 1)
+        quantise_ft(0, 1)
         mirror_sums(2)
         score_passes(2, 0)
         softmax_numerators(0, 0)
         softmax_numerators(0, 1)
-        transpose_features(0, 1)
         quantise_h(2, 1)
         negative_maxima(1, 1)
         burst_power(2)
         score_passes(2, 1)
         add_bias(2, 0)
         transpose_features(1, 0)
-        quantise_ft(0, 0)
-        negative_maxima(2, 0)
-        add_bias(2, 1)
         denominators(0)
         softmax_numerators(1, 0)
         softmax_numerators(1, 1)
+        negative_maxima(2, 0)
+        add_bias(2, 1)
+        pixel_weights(0)
         transpose_features(1, 1)
-        quantise_ft(0, 1)
         negative_maxima(2, 1)
         softmax_numerators(2, 0)
         softmax_numerators(2, 1)
-        pixel_weights(0)
+        transpose_features(2, 0)
         quantise_ft(1, 0)
         pmat(0)
         cluster_norms(0)
-        transpose_features(2, 0)
         denominators(1)
         quantise_ft(1, 1)
         pixel_weights(1)

@@ -23,7 +23,6 @@ HALVES = PIXELS // PASS
 TILES = HALVES * PACK
 HALF_IMAGES = IMAGES * HALVES
 PARTS = ((0, 0), (0, 1), (1, 1))
-MIRRORED = 1
 HALVES_ON_TENSOR = 5
 EPS_NORM_SQ = 1e-24
 EPS_DENOM = 1e-6
@@ -108,7 +107,7 @@ def tile_salad_pa_kernel(tc, f_clu, h_score, W_s2, b_s2, burst_par, out):
 
         def prepare_weights_1():
             w_words = w_sb[:].bitcast(F32).rearrange("k (q u) -> k u q", u=2)
-            w_ps = psum_work.tile([P, 2, CLUSTERS], F32, name="bank")
+            w_ps = psum_sim.tile([P, 2, CLUSTERS], F32, name="sim_ps")
             for u in range(2):
                 nc.tensor.transpose(out=w_ps[:, u, :], in_=w_words[:, u, :], identity=ident[:])
             w_grouped = const.tile([P, CLUSTERS * PACK], BF16, align_bytes=64)
@@ -132,6 +131,8 @@ def tile_salad_pa_kernel(tc, f_clu, h_score, W_s2, b_s2, burst_par, out):
             for pair in range(2):
                 if i == 0:
                     ft_ps = psum_sim.tile([P, 2, 2, P], F32, name="sim_ps")
+                elif on_tensor(i, g):
+                    ft_ps = psum_rn.tile([P, 2, 2, P], F32, name="rn_bank")
                 else:
                     ft_ps = psum_work.tile([P, 2, 2, P], F32, name="bank")
                 for u in range(2):
@@ -148,16 +149,20 @@ def tile_salad_pa_kernel(tc, f_clu, h_score, W_s2, b_s2, burst_par, out):
             return i * HALVES + g < HALVES_ON_TENSOR
 
         def products(i, g):
-            norm_bank[i, g] = psum_work.tile([P, PACK, P], F32, name="bank")
+            banks = 2 if i == 0 else 1
+            norm_bank[i, g] = []
             runs = [
                 piece[:, :, first : first + P] for piece in features(i, g) for first in range(0, piece.shape[2], P)
             ]
-            for r in range(PACK):
-                for j in range(PACK):
-                    run = runs[r][:, j, :]
-                    nc.tensor.matmul(
-                        out=norm_bank[i, g][:, r, :], lhsT=run, rhs=run, start=(j == 0), stop=(j == PACK - 1)
-                    )
+            for b in range(banks):
+                norm_ps = psum_work.tile([P, PACK // banks, P], F32, name="bank")
+                for r in range(PACK // banks):
+                    norm_bank[i, g].append(norm_ps[:, r, :])
+                    for j in range(PACK):
+                        run = runs[b * (PACK // banks) + r][:, j, :]
+                        nc.tensor.matmul(
+                            out=norm_bank[i, g][-1], lhsT=run, rhs=run, start=(j == 0), stop=(j == PACK - 1)
+                        )
 
         def squared_norms(i, g):
             sum_sq = work.tile([P, PACK], F32, name="sum_sq", bufs=6)
@@ -166,7 +171,7 @@ def tile_salad_pa_kernel(tc, f_clu, h_score, W_s2, b_s2, burst_par, out):
                     unread = scratch.tile([P, P], F32, name="masked")
                     nc.vector.scalar_tensor_tensor(
                         out=unread[:],
-                        in0=norm_bank[i, g][:, r, :],
+                        in0=norm_bank[i, g][r],
                         scalar=1.0,
                         in1=ident[:],
                         op0=ALU.mult,
@@ -274,6 +279,7 @@ def tile_salad_pa_kernel(tc, f_clu, h_score, W_s2, b_s2, burst_par, out):
         def burst_rows(i, part):
             g, m = PARTS[part]
             for t in range(PACK):
+                first = t * P if g == 1 else 0
                 rows = slice((g * PACK + t) * P, (g * PACK + t + 1) * P)
                 sim_ps = psum_sim.tile([P, PASS], F32, name="sim_ps")
                 nc.tensor.matmul_mx(
@@ -285,14 +291,14 @@ def tile_salad_pa_kernel(tc, f_clu, h_score, W_s2, b_s2, burst_par, out):
                     start=True,
                     stop=True,
                 )
-                if part == MIRRORED:
-                    values = scratch.tile([P, PASS], F32, name="mirrored", bufs=2 * PACK)
-                    sigmoids[i, t] = values
+                if m == 1:
+                    values = scratch.tile([P, PASS], F32, name="mirrored", bufs=4 * PACK)
+                    sigmoids[i, g, t] = values
                 else:
                     values = scratch.tile([P, PASS], BF16, name="unread")
                 nc.scalar.activation(
-                    out=values[:],
-                    in_=sim_ps[:],
+                    out=values[:, first:],
+                    in_=sim_ps[:, first:],
                     func=ACT.Sigmoid,
                     scale=slope,
                     bias=offset,
@@ -302,14 +308,15 @@ def tile_salad_pa_kernel(tc, f_clu, h_score, W_s2, b_s2, burst_par, out):
         def mirror(i):
             mirror_bank[i] = psum_work.tile([P, PACK, P], F32, name="bank")
             for t in range(PACK):
-                for r in range(PACK):
+                blocks = [(0, r) for r in range(PACK)] + [(1, r) for r in range(t)]
+                for n, (g, r) in enumerate(blocks):
                     nc.tensor.matmul(
                         out=mirror_bank[i][:, t, :],
-                        lhsT=sigmoids[i, r][:, t * P : (t + 1) * P],
+                        lhsT=sigmoids[i, g, r][:, t * P : (t + 1) * P],
                         rhs=ident[:],
                         is_transpose=True,
-                        start=(r == 0),
-                        stop=(r == PACK - 1),
+                        start=(n == 0),
+                        stop=(n == len(blocks) - 1),
                     )
 
         def mirror_sums(i):
@@ -447,6 +454,7 @@ def tile_salad_pa_kernel(tc, f_clu, h_score, W_s2, b_s2, burst_par, out):
         products(1, 0)
         products(1, 1)
         normalise(0, 1)
+        quantise_h(0, 0)
         squared_norms(1, 0)
         inverse_norms(1, 0)
         products(2, 0)
@@ -462,7 +470,6 @@ def tile_salad_pa_kernel(tc, f_clu, h_score, W_s2, b_s2, burst_par, out):
         burst_rows(0, 2)
         squared_norms(2, 1)
         inverse_norms(2, 1)
-        quantise_h(0, 0)
         normalise(1, 0)
         spread_inverse_norms(2, 0)
         quantise_h(0, 1)
@@ -475,72 +482,72 @@ def tile_salad_pa_kernel(tc, f_clu, h_score, W_s2, b_s2, burst_par, out):
         score_passes(0, 0)
         score_passes(0, 1)
         normalise(2, 0)
-        mirror_sums(0)
         add_bias(0, 0)
         add_bias(0, 1)
         burst_rows(1, 1)
+        mirror_sums(0)
+        quantise_h(1, 0)
         burst_power(0)
         burst_rows(1, 2)
         spread_inverse_norms(2, 1)
         quantise_fn(2, 0)
         regroup_h(2, 0)
+        score_passes(1, 0)
+        regroup_h(1, 1)
+        add_bias(1, 0)
         burst_rows(2, 0)
         mirror(1)
-        quantise_h(1, 0)
-        regroup_h(1, 1)
         normalise(2, 1)
         negative_maxima(0, 0)
         quantise_fn(2, 1)
+        quantise_h(1, 1)
         negative_maxima(0, 1)
         burst_rows(2, 1)
-        mirror_sums(1)
-        quantise_h(1, 1)
-        score_passes(1, 0)
-        burst_power(1)
-        regroup_h(2, 1)
-        add_bias(1, 0)
-        burst_rows(2, 2)
         score_passes(1, 1)
-        mirror(2)
-        quantise_h(2, 0)
+        mirror_sums(1)
         negative_maxima(1, 0)
+        burst_power(1)
         add_bias(1, 1)
-        quantise_ft(0, 1)
-        mirror_sums(2)
+        burst_rows(2, 2)
+        quantise_h(2, 0)
+        negative_maxima(1, 1)
         score_passes(2, 0)
+        transpose_features(1, 0)
+        mirror(2)
         softmax_numerators(0, 0)
         softmax_numerators(0, 1)
-        quantise_h(2, 1)
-        negative_maxima(1, 1)
-        burst_power(2)
-        score_passes(2, 1)
+        quantise_ft(0, 1)
+        quantise_ft(2, 1)
+        regroup_h(2, 1)
         add_bias(2, 0)
-        transpose_features(1, 0)
+        quantise_h(2, 1)
+        score_passes(2, 1)
+        mirror_sums(2)
+        negative_maxima(2, 0)
+        burst_power(2)
         denominators(0)
         softmax_numerators(1, 0)
         softmax_numerators(1, 1)
-        negative_maxima(2, 0)
+        transpose_features(1, 1)
         add_bias(2, 1)
         pixel_weights(0)
-        transpose_features(1, 1)
+        quantise_ft(1, 0)
         negative_maxima(2, 1)
         softmax_numerators(2, 0)
         softmax_numerators(2, 1)
         transpose_features(2, 0)
-        quantise_ft(1, 0)
         pmat(0)
         cluster_norms(0)
         denominators(1)
         quantise_ft(1, 1)
         pixel_weights(1)
-        quantise_ft(2, 1)
+        denominators(2)
         pmat(1)
         scale_columns(0)
         cluster_norms(1)
         turn_columns(0)
-        denominators(2)
-        quantise_ft(2, 0)
         pixel_weights(2)
+        quantise_ft(2, 0)
         pmat(2)
         store(0)
         scale_columns(1)

@@ -126,8 +126,9 @@ def tile_salad_pa_kernel(tc, f_clu, h_score, W_s2, b_s2, burst_par, out):
                 for words in (piece.bitcast(F32) for piece in features(i, g))
                 for first in range(0, words.shape[2], P)
             ]
-            ft_grouped[i, g] = work.tile([P, CHANNELS * PACK], BF16, name="ft_grouped", bufs=6, align_bytes=64)
-            grouped_words = ft_grouped[i, g][:].bitcast(F32).rearrange("p (c u) -> p c u", u=2)
+            if i not in ft_grouped:
+                ft_grouped[i] = kept.tile([P, HALVES, CHANNELS * PACK], BF16, name="ft_grouped", bufs=IMAGES, align_bytes=64)
+            grouped_words = ft_grouped[i][:, g, :].bitcast(F32).rearrange("p (c u) -> p c u", u=2)
             for pair in range(2):
                 if i == 0:
                     ft_ps = psum_sim.tile([P, 2, 2, P], F32, name="sim_ps")
@@ -179,7 +180,7 @@ def tile_salad_pa_kernel(tc, f_clu, h_score, W_s2, b_s2, burst_par, out):
                         accum_out=sum_sq[:, r : r + 1],
                     )
             else:
-                by_tile = ft_grouped[i, g][:].rearrange("p (c u e) -> p e u c", u=2, e=2)
+                by_tile = ft_grouped[i][:, g, :].rearrange("p (c u e) -> p e u c", u=2, e=2)
                 for t in range(PACK):
                     unread = scratch.tile([P, CHANNELS], BF16, name="unread")
                     nc.scalar.activation(
@@ -228,11 +229,13 @@ def tile_salad_pa_kernel(tc, f_clu, h_score, W_s2, b_s2, burst_par, out):
                 out=fn_codes[i][:, half(g)].bitcast(FP8X4), scales=fn_scales[i][:, half(g)], in_=fn_grouped[i, g][:]
             )
 
-        def quantise_ft(i, g):
-            ft_codes[i, g] = kept.tile([P, CHANNELS], U32, name="ft_codes", align_bytes=64)
-            ft_scales[i, g] = kept.tile([P, CHANNELS], U8, name="ft_scales", align_bytes=64)
+        def quantise_ft(i):
+            ft_codes[i] = kept.tile([P, HALVES * CHANNELS], U32, name="ft_codes", bufs=IMAGES, align_bytes=64)
+            ft_scales[i] = kept.tile([P, HALVES * CHANNELS], U8, name="ft_scales", bufs=IMAGES, align_bytes=64)
             nc.vector.quantize_mx(
-                out=ft_codes[i, g][:].bitcast(FP8X4), scales=ft_scales[i, g][:], in_=ft_grouped[i, g][:]
+                out=ft_codes[i][:].bitcast(FP8X4),
+                scales=ft_scales[i][:],
+                in_=ft_grouped[i][:].rearrange("p g c -> p (g c)"),
             )
 
         def regroup_h(i, g):
@@ -264,17 +267,18 @@ def tile_salad_pa_kernel(tc, f_clu, h_score, W_s2, b_s2, burst_par, out):
                 )
 
         def add_bias(i, g):
-            logits[i, g] = kept.tile([P, PACK, CLUSTERS], F32, name="logits")
+            if g == 0:
+                logits[i] = kept.tile([P, TILES, CLUSTERS], F32, name="logits", bufs=IMAGES)
             nc.vector.tensor_tensor(
-                out=logits[i, g][:],
+                out=logits[i][:, g * PACK : (g + 1) * PACK, :],
                 in0=score_bank[i, g][:],
                 in1=bias_bc[:].unsqueeze(1).to_broadcast([P, PACK, CLUSTERS]),
                 op=ALU.add,
             )
 
-        def negative_maxima(i, g):
-            neg_max[i, g] = kept.tile([P, PACK], F32, name="neg_max")
-            nc.vector.tensor_reduce(out=neg_max[i, g][:], in_=logits[i, g][:], axis=AX.X, op=ALU.max, negate=True)
+        def negative_maxima(i):
+            neg_max[i] = kept.tile([P, TILES], F32, name="neg_max", bufs=IMAGES)
+            nc.vector.tensor_reduce(out=neg_max[i][:], in_=logits[i][:], axis=AX.X, op=ALU.max, negate=True)
 
         def burst_rows(i, part):
             g, m = PARTS[part]
@@ -332,17 +336,16 @@ def tile_salad_pa_kernel(tc, f_clu, h_score, W_s2, b_s2, burst_par, out):
                 out=powered[i][:], in0=burst[:], in1=exponent.to_broadcast([P, TILES]), op=ALU.pow
             )
 
-        def softmax_numerators(i, g):
-            if g == 0:
-                exp_sum[i] = kept.tile([P, TILES], F32, name="exp_sum")
-            expd[i, g] = kept.tile([P, PACK, CLUSTERS], F32, name="expd")
-            for t in range(PACK):
+        def softmax_numerators(i):
+            exp_sum[i] = kept.tile([P, TILES], F32, name="exp_sum", bufs=IMAGES)
+            expd[i] = kept.tile([P, TILES, CLUSTERS], F32, name="expd", bufs=IMAGES)
+            for t in range(TILES):
                 nc.scalar.activation(
-                    out=expd[i, g][:, t, :],
-                    in_=logits[i, g][:, t, :],
+                    out=expd[i][:, t, :],
+                    in_=logits[i][:, t, :],
                     func=ACT.Exp,
-                    bias=neg_max[i, g][:, t : t + 1],
-                    accum_out=exp_sum[i][:, g * PACK + t : g * PACK + t + 1],
+                    bias=neg_max[i][:, t : t + 1],
+                    accum_out=exp_sum[i][:, t : t + 1],
                 )
 
         def denominators(i):
@@ -357,11 +360,12 @@ def tile_salad_pa_kernel(tc, f_clu, h_score, W_s2, b_s2, burst_par, out):
             nc.vector.reciprocal(out=weight[i][:], in_=denominator[i][:])
 
         def scale_numerators(i, g):
+            tiles = slice(g * PACK, (g + 1) * PACK)
             pm_grouped[i, g] = work.tile([P, CLUSTERS * PACK], BF16, name="pm_grouped", bufs=4, align_bytes=64)
             nc.vector.tensor_tensor(
                 out=pm_grouped[i, g][:].rearrange("p (k u e) -> p k u e", u=2, e=2),
-                in0=expd[i, g][:].rearrange("p (e u) k -> p k u e", e=2),
-                in1=weight[i][:, g * PACK : (g + 1) * PACK]
+                in0=expd[i][:, tiles, :].rearrange("p (e u) k -> p k u e", e=2),
+                in1=weight[i][:, tiles]
                 .rearrange("p (e u) -> p u e", e=2)
                 .unsqueeze(1)
                 .to_broadcast([P, CLUSTERS, 2, 2]),
@@ -378,12 +382,13 @@ def tile_salad_pa_kernel(tc, f_clu, h_score, W_s2, b_s2, burst_par, out):
         def aggregate(i, g):
             if g == 0:
                 vt_bank[i] = psum_sim.tile([P, CHANNELS], F32, name="sim_ps")
+            channels = slice(g * CHANNELS, (g + 1) * CHANNELS)
             nc.tensor.matmul_mx(
                 out=vt_bank[i][:],
                 lhsT=pm_codes[i, g][:].bitcast(FP8X4),
                 lhsT_scale=pm_scales[i, g][:],
-                rhs=ft_codes[i, g][:].bitcast(FP8X4),
-                rhs_scale=ft_scales[i, g][:],
+                rhs=ft_codes[i][:, channels].bitcast(FP8X4),
+                rhs_scale=ft_scales[i][:, channels],
                 start=(g == 0),
                 stop=(g == HALVES - 1),
             )
@@ -432,6 +437,9 @@ def tile_salad_pa_kernel(tc, f_clu, h_score, W_s2, b_s2, burst_par, out):
                 scale_numerators(i, g)
             for g in range(HALVES):
                 quantise_pm(i, g)
+
+        def aggregate_image(i):
+            for g in range(HALVES):
                 aggregate(i, g)
 
         for g in range(HALVES):
@@ -477,7 +485,7 @@ def tile_salad_pa_kernel(tc, f_clu, h_score, W_s2, b_s2, burst_par, out):
         burst_rows(1, 0)
         mirror(0)
         normalise(1, 1)
-        quantise_ft(0, 0)
+        quantise_ft(0)
         quantise_fn(1, 1)
         score_passes(0, 0)
         score_passes(0, 1)
@@ -498,57 +506,51 @@ def tile_salad_pa_kernel(tc, f_clu, h_score, W_s2, b_s2, burst_par, out):
         burst_rows(2, 0)
         mirror(1)
         normalise(2, 1)
-        negative_maxima(0, 0)
-        quantise_fn(2, 1)
         quantise_h(1, 1)
-        negative_maxima(0, 1)
+        quantise_fn(2, 1)
+        negative_maxima(0)
         burst_rows(2, 1)
         score_passes(1, 1)
         mirror_sums(1)
-        negative_maxima(1, 0)
         burst_power(1)
         add_bias(1, 1)
         burst_rows(2, 2)
         quantise_h(2, 0)
-        negative_maxima(1, 1)
+        negative_maxima(1)
         score_passes(2, 0)
-        transpose_features(1, 0)
         mirror(2)
-        softmax_numerators(0, 0)
-        softmax_numerators(0, 1)
-        quantise_ft(0, 1)
-        quantise_ft(2, 1)
+        softmax_numerators(0)
         regroup_h(2, 1)
         add_bias(2, 0)
         quantise_h(2, 1)
         score_passes(2, 1)
+        transpose_features(1, 0)
         mirror_sums(2)
-        negative_maxima(2, 0)
-        burst_power(2)
         denominators(0)
-        softmax_numerators(1, 0)
-        softmax_numerators(1, 1)
+        softmax_numerators(1)
         transpose_features(1, 1)
         add_bias(2, 1)
+        burst_power(2)
         pixel_weights(0)
-        quantise_ft(1, 0)
-        negative_maxima(2, 1)
-        softmax_numerators(2, 0)
-        softmax_numerators(2, 1)
-        transpose_features(2, 0)
+        negative_maxima(2)
+        softmax_numerators(2)
         pmat(0)
+        aggregate_image(0)
         cluster_norms(0)
+        transpose_features(2, 0)
         denominators(1)
-        quantise_ft(1, 1)
         pixel_weights(1)
-        denominators(2)
         pmat(1)
+        quantise_ft(1)
+        denominators(2)
+        aggregate_image(1)
         scale_columns(0)
         cluster_norms(1)
         turn_columns(0)
         pixel_weights(2)
-        quantise_ft(2, 0)
         pmat(2)
+        quantise_ft(2)
+        aggregate_image(2)
         store(0)
         scale_columns(1)
         cluster_norms(2)

@@ -21,9 +21,9 @@ PIXELS = 1024
 CLUSTERS = 128
 HALVES = PIXELS // PASS
 TILES = HALVES * PACK
-HALF_IMAGES = IMAGES * HALVES
 PARTS = ((0, 0), (0, 1), (1, 1))
 HALVES_ON_TENSOR = 5
+REGROUPED_BY_SCALAR = (1, 2, 4)
 EPS_NORM_SQ = 1e-24
 EPS_DENOM = 1e-6
 
@@ -47,10 +47,10 @@ def tile_salad_pa_kernel(tc, f_clu, h_score, W_s2, b_s2, burst_par, out):
             return slice(g * PASS, (g + 1) * PASS)
 
         first_f = [
-            inputs.tile([P, PACK, n], BF16, name=name)
+            inputs.tile([P, PACK, n], BF16, name=name, bufs=1)
             for n, name in ((PASS // 2, "first_a"), (PASS // 2, "first_b"), (PASS, "first_c"))
         ]
-        f_sb = [None] + [inputs.tile([P, PACK * PIXELS], BF16, name="f_sb") for i in range(1, IMAGES)]
+        f_sb = [None] + [inputs.tile([P, PACK * PIXELS], BF16, name="f_sb", bufs=2) for i in range(1, IMAGES)]
         h_sb = [inputs.tile([P, PACK * PIXELS], BF16, name="h_sb") for i in range(IMAGES)]
         w_sb = const.tile([P, CHANNELS], BF16)
         par_bf = const.tile([P, 3], BF16)
@@ -83,9 +83,7 @@ def tile_salad_pa_kernel(tc, f_clu, h_score, W_s2, b_s2, burst_par, out):
         make_identity(nc, ident[:])
         neg_half = const.tile([P, PACK], F32)
         nc.gpsimd.memset(neg_half[:], -0.5)
-        burst_terms = {}
-        for i in range(IMAGES):
-            burst_terms[i] = kept.tile([P, HALVES, TILES], F32, name="burst_terms")
+        burst_terms = [const.tile([P, HALVES, TILES], F32, name=f"burst_terms_{i}") for i in range(IMAGES)]
         warm = const.tile([P, 1], F32)
         nc.scalar.activation(out=warm[:], in_=neg_half[:, 0:1], func=ACT.Sigmoid)
         par = const.tile([P, 3], F32)
@@ -98,27 +96,26 @@ def tile_salad_pa_kernel(tc, f_clu, h_score, W_s2, b_s2, burst_par, out):
         fn_grouped, fn_codes, fn_scales = {}, {}, {}
         h_grouped, h_codes, h_scales = {}, {}, {}
         score_bank, logits, neg_max, expd, exp_sum = {}, {}, {}, {}, {}
-        powered, sigmoids, mirror_bank = {}, {}, {}
-        denominator, weight, pm_grouped, pm_codes, pm_scales, vt_bank, v_inv, v_unit, out_bank = {}, {}, {}, {}, {}, {}, {}, {}, {}
+        powered, sigmoids, mirror_bank, denominator, weight = {}, {}, {}, {}, {}
+        pm_grouped, pm_codes, pm_scales = {}, {}, {}
+        vt_bank, v_inv, v_unit, out_bank = {}, {}, {}, {}
 
-        w_tiles = {}
+        w_grouped = const.tile([P, CLUSTERS * PACK], BF16, align_bytes=64)
         w_codes = const.tile([P, CLUSTERS], U32, align_bytes=64)
         w_scales = const.tile([P, CLUSTERS], U8, align_bytes=64)
 
-        def prepare_weights_1():
+        def transpose_weights():
             w_words = w_sb[:].bitcast(F32).rearrange("k (q u) -> k u q", u=2)
             w_ps = psum_sim.tile([P, 2, CLUSTERS], F32, name="sim_ps")
             for u in range(2):
                 nc.tensor.transpose(out=w_ps[:, u, :], in_=w_words[:, u, :], identity=ident[:])
-            w_grouped = const.tile([P, CLUSTERS * PACK], BF16, align_bytes=64)
             nc.vector.tensor_copy(
                 out=w_grouped[:].bitcast(F32).rearrange("q (k u) -> q k u", u=2),
                 in_=w_ps[:].rearrange("q u k -> q k u"),
             )
-            w_tiles["grouped"] = w_grouped
 
-        def prepare_weights_2():
-            nc.vector.quantize_mx(out=w_codes[:].bitcast(FP8X4), scales=w_scales[:], in_=w_tiles["grouped"][:])
+        def quantise_weights():
+            nc.vector.quantize_mx(out=w_codes[:].bitcast(FP8X4), scales=w_scales[:], in_=w_grouped[:])
 
         def transpose_features(i, g):
             f_words = [
@@ -127,7 +124,9 @@ def tile_salad_pa_kernel(tc, f_clu, h_score, W_s2, b_s2, burst_par, out):
                 for first in range(0, words.shape[2], P)
             ]
             if i not in ft_grouped:
-                ft_grouped[i] = kept.tile([P, HALVES, CHANNELS * PACK], BF16, name="ft_grouped", bufs=IMAGES, align_bytes=64)
+                ft_grouped[i] = kept.tile(
+                    [P, HALVES, CHANNELS * PACK], BF16, name="ft_grouped", bufs=IMAGES, align_bytes=64
+                )
             grouped_words = ft_grouped[i][:, g, :].bitcast(F32).rearrange("p (c u) -> p c u", u=2)
             for pair in range(2):
                 if i == 0:
@@ -240,16 +239,20 @@ def tile_salad_pa_kernel(tc, f_clu, h_score, W_s2, b_s2, burst_par, out):
 
         def regroup_h(i, g):
             h_view = h_sb[i][:].rearrange("q (j g w e) -> q g w j e", j=PACK, g=HALVES, e=2)[:, g]
-            h_grouped[i, g] = work.tile([P, PASS * PACK], BF16, name="h_grouped", bufs=4, align_bytes=64)
-            copy = nc.scalar.copy if i * HALVES + g in (1, 2, 4) else nc.vector.tensor_copy
-            copy(out=h_grouped[i, g][:].rearrange("q (e w j) -> q w j e", e=2, j=PACK), in_=h_view)
-
-        def quantise_h(i, g):
             if g == 0:
+                h_grouped[i] = kept.tile([P, HALVES, PASS * PACK], BF16, name="h_grouped", bufs=IMAGES, align_bytes=64)
+            copy = nc.scalar.copy if i * HALVES + g in REGROUPED_BY_SCALAR else nc.vector.tensor_copy
+            copy(out=h_grouped[i][:, g, :].rearrange("q (e w j) -> q w j e", e=2, j=PACK), in_=h_view)
+
+        def quantise_h(i, *halves):
+            if i not in h_codes:
                 h_codes[i] = work.tile([P, PIXELS], U32, name="h_codes", align_bytes=64)
                 h_scales[i] = work.tile([P, PIXELS], U8, name="h_scales", align_bytes=64)
+            columns = slice(halves[0] * PASS, (halves[-1] + 1) * PASS)
             nc.vector.quantize_mx(
-                out=h_codes[i][:, half(g)].bitcast(FP8X4), scales=h_scales[i][:, half(g)], in_=h_grouped[i, g][:]
+                out=h_codes[i][:, columns].bitcast(FP8X4),
+                scales=h_scales[i][:, columns],
+                in_=h_grouped[i][:, halves[0] : halves[-1] + 1, :].rearrange("q g n -> q (g n)"),
             )
 
         def score_passes(i, g):
@@ -296,7 +299,7 @@ def tile_salad_pa_kernel(tc, f_clu, h_score, W_s2, b_s2, burst_par, out):
                     stop=True,
                 )
                 if m == 1:
-                    values = scratch.tile([P, PASS], F32, name="mirrored", bufs=4 * PACK)
+                    values = scratch.tile([P, PASS], F32, name="mirrored", bufs=2 * PACK)
                     sigmoids[i, g, t] = values
                 else:
                     values = scratch.tile([P, PASS], BF16, name="unread")
@@ -404,50 +407,46 @@ def tile_salad_pa_kernel(tc, f_clu, h_score, W_s2, b_s2, burst_par, out):
 
         def scale_columns(i):
             v_view = vt_bank[i][:].rearrange("k (j q) -> k j q", j=PACK)
-            for part in range(2):
-                groups = slice(2 * part, 2 * part + 2)
-                v_unit[i, part] = work.tile([P, 2, P], F32, name="v_unit", bufs=4)
-                if i == IMAGES - 1 and part == 0:
-                    nc.vector.tensor_scalar_mul(out=v_unit[i, part][:], in0=v_view[:, groups, :], scalar1=v_inv[i][:])
+            v_unit[i] = []
+            for part, groups in enumerate(store_groups(i)):
+                unit = work.tile([P, len(groups), P], F32, name="v_unit", bufs=4)
+                in_ = v_view[:, groups[0] : groups[-1] + 1, :]
+                if part == 1:
+                    nc.vector.tensor_scalar_mul(out=unit[:], in0=in_, scalar1=v_inv[i][:])
                 else:
-                    nc.scalar.activation(
-                        out=v_unit[i, part][:], in_=v_view[:, groups, :], func=ACT.Copy, scale=v_inv[i][:]
-                    )
+                    nc.scalar.activation(out=unit[:], in_=in_, func=ACT.Copy, scale=v_inv[i][:])
+                v_unit[i].append(unit)
+
+        def store_groups(i):
+            return (range(0, 2), range(2, 4)) if i == IMAGES - 1 else (range(0, 4),)
 
         def turn_columns(i):
-            for part in range(2):
-                out_bank[i, part] = psum_rn.tile([P, 2, CLUSTERS], F32, name="rn_bank")
-                for j in range(2):
-                    nc.tensor.transpose(
-                        out=out_bank[i, part][:, j, :], in_=v_unit[i, part][:, j, :], identity=ident[:]
-                    )
+            out_bank[i] = []
+            for unit, groups in zip(v_unit[i], store_groups(i)):
+                turned = psum_rn.tile([P, len(groups), CLUSTERS], F32, name="rn_bank")
+                for n in range(len(groups)):
+                    nc.tensor.transpose(out=turned[:, n, :], in_=unit[:, n, :], identity=ident[:])
+                out_bank[i].append(turned)
 
         def store(i):
-            for part in range(2):
-                out_sb = work.tile([P, 2, CLUSTERS], F32, name="out_sb", bufs=4)
-                copy = nc.scalar.copy if part == 0 else nc.vector.tensor_copy
-                copy(out=out_sb[:], in_=out_bank[i, part][:])
+            for part, groups in enumerate(store_groups(i)):
+                out_sb = work.tile([P, len(groups), CLUSTERS], F32, name="out_sb", bufs=4)
+                copy = nc.vector.tensor_copy if part == 1 else nc.scalar.copy
+                copy(out=out_sb[:], in_=out_bank[i][part][:])
                 nc.sync.dma_start(
-                    out=out[i].rearrange("(q j) k -> q j k", j=PACK)[:, 2 * part : 2 * part + 2, :], in_=out_sb[:]
+                    out=out[i].rearrange("(q j) k -> q j k", j=PACK)[:, groups[0] : groups[-1] + 1, :], in_=out_sb[:]
                 )
 
-
-        def pmat(i):
+        def both(stage, i):
             for g in range(HALVES):
-                scale_numerators(i, g)
-            for g in range(HALVES):
-                quantise_pm(i, g)
-
-        def aggregate_image(i):
-            for g in range(HALVES):
-                aggregate(i, g)
+                stage(i, g)
 
         for g in range(HALVES):
             products(0, g)
             squared_norms(0, g)
             inverse_norms(0, g)
         nc.gpsimd.tensor_copy(out=par[:], in_=par_bf[:])
-        prepare_weights_1()
+        transpose_weights()
         regroup_h(0, 0)
         regroup_h(0, 1)
         spread_inverse_norms(0, 0)
@@ -455,7 +454,7 @@ def tile_salad_pa_kernel(tc, f_clu, h_score, W_s2, b_s2, burst_par, out):
         spread_inverse_norms(0, 1)
         transpose_features(0, 1)
         normalise(0, 0)
-        prepare_weights_2()
+        quantise_weights()
         quantise_fn(0, 0)
         burst_rows(0, 0)
         regroup_h(1, 0)
@@ -487,11 +486,9 @@ def tile_salad_pa_kernel(tc, f_clu, h_score, W_s2, b_s2, burst_par, out):
         normalise(1, 1)
         quantise_ft(0)
         quantise_fn(1, 1)
-        score_passes(0, 0)
-        score_passes(0, 1)
+        both(score_passes, 0)
         normalise(2, 0)
-        add_bias(0, 0)
-        add_bias(0, 1)
+        both(add_bias, 0)
         burst_rows(1, 1)
         mirror_sums(0)
         quantise_h(1, 0)
@@ -513,44 +510,46 @@ def tile_salad_pa_kernel(tc, f_clu, h_score, W_s2, b_s2, burst_par, out):
         score_passes(1, 1)
         mirror_sums(1)
         burst_power(1)
+        regroup_h(2, 1)
         add_bias(1, 1)
         burst_rows(2, 2)
-        quantise_h(2, 0)
-        negative_maxima(1)
-        score_passes(2, 0)
         mirror(2)
         softmax_numerators(0)
-        regroup_h(2, 1)
-        add_bias(2, 0)
-        quantise_h(2, 1)
-        score_passes(2, 1)
+        quantise_h(2, 0, 1)
+        negative_maxima(1)
+        both(score_passes, 2)
         transpose_features(1, 0)
         mirror_sums(2)
-        denominators(0)
+        add_bias(2, 0)
         softmax_numerators(1)
         transpose_features(1, 1)
         add_bias(2, 1)
+        denominators(0)
         burst_power(2)
         pixel_weights(0)
         negative_maxima(2)
+        both(scale_numerators, 0)
         softmax_numerators(2)
-        pmat(0)
-        aggregate_image(0)
+        denominators(1)
+        quantise_pm(0, 0)
+        pixel_weights(1)
+        quantise_pm(0, 1)
+        both(aggregate, 0)
         cluster_norms(0)
         transpose_features(2, 0)
-        denominators(1)
-        pixel_weights(1)
-        pmat(1)
+        both(scale_numerators, 1)
+        both(quantise_pm, 1)
         quantise_ft(1)
+        both(aggregate, 1)
         denominators(2)
-        aggregate_image(1)
+        pixel_weights(2)
         scale_columns(0)
         cluster_norms(1)
         turn_columns(0)
-        pixel_weights(2)
-        pmat(2)
+        both(scale_numerators, 2)
+        both(quantise_pm, 2)
         quantise_ft(2)
-        aggregate_image(2)
+        both(aggregate, 2)
         store(0)
         scale_columns(1)
         cluster_norms(2)

from contextlib import ExitStack

import concourse.mybir as mybir
from concourse.masks import make_identity

F32 = mybir.dt.float32
BF16 = mybir.dt.bfloat16
U32 = mybir.dt.uint32
U8 = mybir.dt.uint8
FP8X4 = mybir.dt.float8_e4m3fn_x4
ACT = mybir.ActivationFunctionType
ALU = mybir.AluOpType
AX = mybir.AxisListType

P = 128
PACK = 4
PASS = P * PACK
IMAGES = 3
CHANNELS = 512
PIXELS = 1024
CLUSTERS = 128
HALVES = PIXELS // PASS
TILES = HALVES * PACK
PARTS = ((0, 0), (0, 1), (1, 1))
HALVES_ON_TENSOR = 5
REGROUPED_BY_SCALAR = (1, 2, 4)
EPS_NORM_SQ = 1e-24
EPS_DENOM = 1e-6

FLOPS = IMAGES * 2 * (CLUSTERS * CHANNELS * PIXELS + PIXELS * PIXELS * CHANNELS + CHANNELS * CLUSTERS * PIXELS)


def tile_salad_pa_kernel(tc, f_clu, h_score, W_s2, b_s2, burst_par, out):
    nc = tc.nc
    with ExitStack() as stack:
        const = stack.enter_context(tc.tile_pool(name="const", bufs=1))
        inputs = stack.enter_context(tc.tile_pool(name="inputs", bufs=IMAGES))
        kept = stack.enter_context(tc.tile_pool(name="kept", bufs=IMAGES * HALVES))
        work = stack.enter_context(tc.tile_pool(name="work", bufs=2))
        scratch = stack.enter_context(tc.tile_pool(name="scratch", bufs=4))
        psum_sim = stack.enter_context(tc.psum_pool(name="psum_sim", bufs=4))
        psum_rn = stack.enter_context(tc.psum_pool(name="psum_rn", bufs=2))
        psum_work = stack.enter_context(tc.psum_pool(name="psum_work", bufs=2))
        stack.enter_context(tc.manual_schedule())

        def half(g):
            return slice(g * PASS, (g + 1) * PASS)

        first_f = [
            inputs.tile([P, PACK, n], BF16, name=name, bufs=1)
            for n, name in ((PASS // 2, "first_a"), (PASS // 2, "first_b"), (PASS, "first_c"))
        ]
        f_sb = [None] + [inputs.tile([P, PACK * PIXELS], BF16, name="f_sb", bufs=2) for i in range(1, IMAGES)]
        h_sb = [inputs.tile([P, PACK * PIXELS], BF16, name="h_sb") for i in range(IMAGES)]
        w_sb = const.tile([P, CHANNELS], BF16)
        par_bf = const.tile([P, 3], BF16)
        bias_bc = const.tile([P, CLUSTERS], BF16)

        def load(tile, source):
            nc.sync.dma_start(out=tile[:], in_=source.rearrange("(q j) n -> q (j n)", j=PACK))

        first_pixel = 0
        for piece in first_f:
            n = piece[:].shape[2]
            columns = slice(first_pixel, first_pixel + n)
            nc.sync.dma_start(out=piece[:], in_=f_clu[0].rearrange("(q j) n -> q j n", j=PACK)[:, :, columns])
            first_pixel += n
        nc.sync.dma_start(out=par_bf[:], in_=burst_par.partition_broadcast(P))
        nc.sync.dma_start(out=w_sb[:], in_=W_s2)
        load(h_sb[0], h_score[0])
        load(f_sb[1], f_clu[1])
        load(f_sb[2], f_clu[2])
        nc.sync.dma_start(out=bias_bc[:], in_=b_s2.partition_broadcast(P))
        load(h_sb[1], h_score[1])
        load(h_sb[2], h_score[2])

        def features(i, g):
            if i == 0:
                return [piece[:] for piece in (first_f[:2] if g == 0 else first_f[2:])]
            return [f_sb[i][:].rearrange("q (j n) -> q j n", j=PACK)[:, :, half(g)]]

        ident = const.tile([P, P], F32)
        make_identity(nc, ident[:])
        neg_half = const.tile([P, PACK], F32)
        nc.gpsimd.memset(neg_half[:], -0.5)
        burst_terms = [const.tile([P, HALVES, TILES], F32, name=f"burst_terms_{i}") for i in range(IMAGES)]
        warm = const.tile([P, 1], F32)
        nc.scalar.activation(out=warm[:], in_=neg_half[:, 0:1], func=ACT.Sigmoid)
        par = const.tile([P, 3], F32)
        slope = par[:, 0:1]
        offset = par[:, 1:2]
        exponent = par[:, 2:3]

        ft_grouped, ft_codes, ft_scales = {}, {}, {}
        norm_bank, sums_of_squares, inv_norm, rn_bank = {}, {}, {}, {}
        fn_grouped, fn_codes, fn_scales = {}, {}, {}
        h_grouped, h_codes, h_scales = {}, {}, {}
        score_bank, logits, neg_max, expd, exp_sum = {}, {}, {}, {}, {}
        powered, sigmoids, mirror_bank, denominator, weight = {}, {}, {}, {}, {}
        pm_grouped, pm_codes, pm_scales = {}, {}, {}
        vt_bank, v_inv, v_unit, out_bank = {}, {}, {}, {}

        w_grouped = const.tile([P, CLUSTERS * PACK], BF16, align_bytes=64)
        w_codes = const.tile([P, CLUSTERS], U32, align_bytes=64)
        w_scales = const.tile([P, CLUSTERS], U8, align_bytes=64)

        def transpose_weights():
            w_words = w_sb[:].bitcast(F32).rearrange("k (q u) -> k u q", u=2)
            w_ps = psum_sim.tile([P, 2, CLUSTERS], F32, name="sim_ps")
            for u in range(2):
                nc.tensor.transpose(out=w_ps[:, u, :], in_=w_words[:, u, :], identity=ident[:])
            nc.vector.tensor_copy(
                out=w_grouped[:].bitcast(F32).rearrange("q (k u) -> q k u", u=2),
                in_=w_ps[:].rearrange("q u k -> q k u"),
            )

        def quantise_weights():
            nc.vector.quantize_mx(out=w_codes[:].bitcast(FP8X4), scales=w_scales[:], in_=w_grouped[:])

        def transpose_features(i, g):
            f_words = [
                words[:, :, first : first + P]
                for words in (piece.bitcast(F32) for piece in features(i, g))
                for first in range(0, words.shape[2], P)
            ]
            if i not in ft_grouped:
                ft_grouped[i] = kept.tile(
                    [P, HALVES, CHANNELS * PACK], BF16, name="ft_grouped", bufs=IMAGES, align_bytes=64
                )
            grouped_words = ft_grouped[i][:, g, :].bitcast(F32).rearrange("p (c u) -> p c u", u=2)
            for pair in range(2):
                if i == 0:
                    ft_ps = psum_sim.tile([P, 2, 2, P], F32, name="sim_ps")
                elif on_tensor(i, g):
                    ft_ps = psum_rn.tile([P, 2, 2, P], F32, name="rn_bank")
                else:
                    ft_ps = psum_work.tile([P, 2, 2, P], F32, name="bank")
                for u in range(2):
                    for jj in range(2):
                        nc.tensor.transpose(
                            out=ft_ps[:, u, jj, :], in_=f_words[u][:, 2 * pair + jj, :], identity=ident[:]
                        )
                nc.scalar.copy(
                    out=grouped_words[:, pair * 2 * P : (pair + 1) * 2 * P, :],
                    in_=ft_ps[:].rearrange("p u jj q -> p (jj q) u"),
                )

        def on_tensor(i, g):
            return i * HALVES + g < HALVES_ON_TENSOR

        def products(i, g):
            banks = 2 if i == 0 else 1
            norm_bank[i, g] = []
            runs = [
                piece[:, :, first : first + P] for piece in features(i, g) for first in range(0, piece.shape[2], P)
            ]
            for b in range(banks):
                norm_ps = psum_work.tile([P, PACK // banks, P], F32, name="bank")
                for r in range(PACK // banks):
                    norm_bank[i, g].append(norm_ps[:, r, :])
                    for j in range(PACK):
                        run = runs[b * (PACK // banks) + r][:, j, :]
                        nc.tensor.matmul(
                            out=norm_bank[i, g][-1], lhsT=run, rhs=run, start=(j == 0), stop=(j == PACK - 1)
                        )

        def squared_norms(i, g):
            sum_sq = work.tile([P, PACK], F32, name="sum_sq", bufs=6)
            if on_tensor(i, g):
                for r in range(PACK):
                    unread = scratch.tile([P, P], F32, name="masked")
                    nc.vector.scalar_tensor_tensor(
                        out=unread[:],
                        in0=norm_bank[i, g][r],
                        scalar=1.0,
                        in1=ident[:],
                        op0=ALU.mult,
                        op1=ALU.mult,
                        accum_out=sum_sq[:, r : r + 1],
                    )
            else:
                by_tile = ft_grouped[i][:, g, :].rearrange("p (c u e) -> p e u c", u=2, e=2)
                for t in range(PACK):
                    unread = scratch.tile([P, CHANNELS], BF16, name="unread")
                    nc.scalar.activation(
                        out=unread[:], in_=by_tile[:, t // 2, t % 2, :], func=ACT.Square, accum_out=sum_sq[:, t : t + 1]
                    )
            sums_of_squares[i, g] = sum_sq

        def inverse_norms(i, g):
            sum_sq = sums_of_squares[i, g]
            floored = work.tile([P, PACK], F32, name="floored")
            nc.gpsimd.tensor_scalar_max(out=floored[:], in0=sum_sq[:], scalar1=EPS_NORM_SQ)
            inv_norm[i, g] = work.tile([P, PACK], F32, name="inv_norm", bufs=6)
            nc.gpsimd.tensor_tensor(out=inv_norm[i, g][:], in0=floored[:], in1=neg_half[:], op=ALU.pow)

        def spread_inverse_norms(i, g):
            rn_bank[i, g] = psum_rn.tile([P, PACK, P], F32, name="rn_bank")
            for r in range(PACK):
                nc.tensor.transpose(
                    out=rn_bank[i, g][:, r, :], in_=inv_norm[i, g][:, r : r + 1].to_broadcast([P, P]), identity=ident[:]
                )

        def normalise(i, g):
            columns = rn_bank[i, g][:].rearrange("q r c -> q (r c)")
            if on_tensor(i, g):
                rn_view = columns.rearrange("q (w e) -> q w e", e=2)
            else:
                rn_view = columns.rearrange("q (e w) -> q w e", e=2)
            fn_grouped[i, g] = work.tile([P, PASS * PACK], BF16, name="fn_grouped", align_bytes=64)
            fn_view = fn_grouped[i, g][:].rearrange("q (e w j) -> q w j e", e=2, j=PACK)
            pieces = features(i, g)
            pairs = PASS // 2 // len(pieces)
            for n, piece in enumerate(pieces):
                w = slice(n * pairs, (n + 1) * pairs)
                nc.vector.tensor_tensor(
                    out=fn_view[:, w],
                    in0=piece.rearrange("q j (w e) -> q w j e", e=2),
                    in1=rn_view[:, w].unsqueeze(2).to_broadcast([P, pairs, PACK, 2]),
                    op=ALU.mult,
                )

        def quantise_fn(i, g):
            if g == 0:
                fn_codes[i] = work.tile([P, PIXELS], U32, name="fn_codes", align_bytes=64)
                fn_scales[i] = work.tile([P, PIXELS], U8, name="fn_scales", align_bytes=64)
            nc.vector.quantize_mx(
                out=fn_codes[i][:, half(g)].bitcast(FP8X4), scales=fn_scales[i][:, half(g)], in_=fn_grouped[i, g][:]
            )

        def quantise_ft(i):
            ft_codes[i] = kept.tile([P, HALVES * CHANNELS], U32, name="ft_codes", bufs=IMAGES, align_bytes=64)
            ft_scales[i] = kept.tile([P, HALVES * CHANNELS], U8, name="ft_scales", bufs=IMAGES, align_bytes=64)
            nc.vector.quantize_mx(
                out=ft_codes[i][:].bitcast(FP8X4),
                scales=ft_scales[i][:],
                in_=ft_grouped[i][:].rearrange("p g c -> p (g c)"),
            )

        def regroup_h(i, g):
            h_view = h_sb[i][:].rearrange("q (j g w e) -> q g w j e", j=PACK, g=HALVES, e=2)[:, g]
            if g == 0:
                h_grouped[i] = kept.tile([P, HALVES, PASS * PACK], BF16, name="h_grouped", bufs=IMAGES, align_bytes=64)
            copy = nc.scalar.copy if i * HALVES + g in REGROUPED_BY_SCALAR else nc.vector.tensor_copy
            copy(out=h_grouped[i][:, g, :].rearrange("q (e w j) -> q w j e", e=2, j=PACK), in_=h_view)

        def quantise_h(i, *halves):
            if i not in h_codes:
                h_codes[i] = work.tile([P, PIXELS], U32, name="h_codes", align_bytes=64)
                h_scales[i] = work.tile([P, PIXELS], U8, name="h_scales", align_bytes=64)
            columns = slice(halves[0] * PASS, (halves[-1] + 1) * PASS)
            nc.vector.quantize_mx(
                out=h_codes[i][:, columns].bitcast(FP8X4),
                scales=h_scales[i][:, columns],
                in_=h_grouped[i][:, halves[0] : halves[-1] + 1, :].rearrange("q g n -> q (g n)"),
            )

        def score_passes(i, g):
            score_bank[i, g] = psum_sim.tile([P, PACK, CLUSTERS], F32, name="sim_ps")
            for t in range(PACK):
                cols = slice((g * PACK + t) * P, (g * PACK + t + 1) * P)
                nc.tensor.matmul_mx(
                    out=score_bank[i, g][:, t, :],
                    lhsT=h_codes[i][:, cols].bitcast(FP8X4),
                    lhsT_scale=h_scales[i][:, cols],
                    rhs=w_codes[:].bitcast(FP8X4),
                    rhs_scale=w_scales[:],
                    start=True,
                    stop=True,
                )

        def add_bias(i, g):
            if g == 0:
                logits[i] = kept.tile([P, TILES, CLUSTERS], F32, name="logits", bufs=IMAGES)
            nc.vector.tensor_tensor(
                out=logits[i][:, g * PACK : (g + 1) * PACK, :],
                in0=score_bank[i, g][:],
                in1=bias_bc[:].unsqueeze(1).to_broadcast([P, PACK, CLUSTERS]),
                op=ALU.add,
            )

        def negative_maxima(i):
            neg_max[i] = kept.tile([P, TILES], F32, name="neg_max", bufs=IMAGES)
            nc.vector.tensor_reduce(out=neg_max[i][:], in_=logits[i][:], axis=AX.X, op=ALU.max, negate=True)

        def burst_rows(i, part):
            g, m = PARTS[part]
            for t in range(PACK):
                first = t * P if g == 1 else 0
                rows = slice((g * PACK + t) * P, (g * PACK + t + 1) * P)
                sim_ps = psum_sim.tile([P, PASS], F32, name="sim_ps")
                nc.tensor.matmul_mx(
                    out=sim_ps[:],
                    lhsT=fn_codes[i][:, rows].bitcast(FP8X4),
                    lhsT_scale=fn_scales[i][:, rows],
                    rhs=fn_codes[i][:, half(m)].bitcast(FP8X4),
                    rhs_scale=fn_scales[i][:, half(m)],
                    start=True,
                    stop=True,
                )
                if m == 1:
                    values = scratch.tile([P, PASS], F32, name="mirrored", bufs=2 * PACK)
                    sigmoids[i, g, t] = values
                else:
                    values = scratch.tile([P, PASS], BF16, name="unread")
                nc.scalar.activation(
                    out=values[:, first:],
                    in_=sim_ps[:, first:],
                    func=ACT.Sigmoid,
                    scale=slope,
                    bias=offset,
                    accum_out=burst_terms[i][:, m, g * PACK + t : g * PACK + t + 1],
                )

        def mirror(i):
            mirror_bank[i] = psum_work.tile([P, PACK, P], F32, name="bank")
            for t in range(PACK):
                blocks = [(0, r) for r in range(PACK)] + [(1, r) for r in range(t)]
                for n, (g, r) in enumerate(blocks):
                    nc.tensor.matmul(
                        out=mirror_bank[i][:, t, :],
                        lhsT=sigmoids[i, g, r][:, t * P : (t + 1) * P],
                        rhs=ident[:],
                        is_transpose=True,
                        start=(n == 0),
                        stop=(n == len(blocks) - 1),
                    )

        def mirror_sums(i):
            nc.vector.tensor_reduce(out=burst_terms[i][:, 0, PACK:], in_=mirror_bank[i][:], axis=AX.X, op=ALU.add)

        def burst_power(i):
            burst = work.tile([P, TILES], F32, name="burst", bufs=3)
            nc.vector.tensor_reduce(
                out=burst[:], in_=burst_terms[i][:].rearrange("p m t -> p t m"), axis=AX.X, op=ALU.add
            )
            powered[i] = kept.tile([P, TILES], F32, name="powered")
            nc.gpsimd.tensor_tensor(
                out=powered[i][:], in0=burst[:], in1=exponent.to_broadcast([P, TILES]), op=ALU.pow
            )

        def softmax_numerators(i):
            exp_sum[i] = kept.tile([P, TILES], F32, name="exp_sum", bufs=IMAGES)
            expd[i] = kept.tile([P, TILES, CLUSTERS], F32, name="expd", bufs=IMAGES)
            for t in range(TILES):
                nc.scalar.activation(
                    out=expd[i][:, t, :],
                    in_=logits[i][:, t, :],
                    func=ACT.Exp,
                    bias=neg_max[i][:, t : t + 1],
                    accum_out=exp_sum[i][:, t : t + 1],
                )

        def denominators(i):
            denom = work.tile([P, TILES], F32, name="denom")
            nc.vector.scalar_tensor_tensor(
                out=denom[:], in0=powered[i][:], scalar=EPS_DENOM, in1=exp_sum[i][:], op0=ALU.add, op1=ALU.mult
            )
            denominator[i] = denom

        def pixel_weights(i):
            weight[i] = work.tile([P, TILES], F32, name="weight")
            nc.vector.reciprocal(out=weight[i][:], in_=denominator[i][:])

        def scale_numerators(i, g):
            tiles = slice(g * PACK, (g + 1) * PACK)
            pm_grouped[i, g] = work.tile([P, CLUSTERS * PACK], BF16, name="pm_grouped", bufs=4, align_bytes=64)
            nc.vector.tensor_tensor(
                out=pm_grouped[i, g][:].rearrange("p (k u e) -> p k u e", u=2, e=2),
                in0=expd[i][:, tiles, :].rearrange("p (e u) k -> p k u e", e=2),
                in1=weight[i][:, tiles]
                .rearrange("p (e u) -> p u e", e=2)
                .unsqueeze(1)
                .to_broadcast([P, CLUSTERS, 2, 2]),
                op=ALU.mult,
            )

        def quantise_pm(i, g):
            pm_codes[i, g] = work.tile([P, CLUSTERS], U32, name="pm_codes", bufs=4, align_bytes=64)
            pm_scales[i, g] = work.tile([P, CLUSTERS], U8, name="pm_scales", bufs=4, align_bytes=64)
            nc.vector.quantize_mx(
                out=pm_codes[i, g][:].bitcast(FP8X4), scales=pm_scales[i, g][:], in_=pm_grouped[i, g][:]
            )

        def aggregate(i, g):
            if g == 0:
                vt_bank[i] = psum_sim.tile([P, CHANNELS], F32, name="sim_ps")
            channels = slice(g * CHANNELS, (g + 1) * CHANNELS)
            nc.tensor.matmul_mx(
                out=vt_bank[i][:],
                lhsT=pm_codes[i, g][:].bitcast(FP8X4),
                lhsT_scale=pm_scales[i, g][:],
                rhs=ft_codes[i][:, channels].bitcast(FP8X4),
                rhs_scale=ft_scales[i][:, channels],
                start=(g == 0),
                stop=(g == HALVES - 1),
            )

        def cluster_norms(i):
            v_sq = work.tile([P, 1], F32, name="v_sq")
            unread = scratch.tile([P, CHANNELS], BF16, name="unread")
            nc.scalar.activation(out=unread[:], in_=vt_bank[i][:], func=ACT.Square, accum_out=v_sq[:])
            v_floored = work.tile([P, 1], F32, name="v_floored")
            nc.gpsimd.tensor_scalar_max(out=v_floored[:], in0=v_sq[:], scalar1=EPS_NORM_SQ)
            v_inv[i] = work.tile([P, 1], F32, name="v_inv")
            nc.gpsimd.tensor_tensor(out=v_inv[i][:], in0=v_floored[:], in1=neg_half[:, 0:1], op=ALU.pow)

        def scale_columns(i):
            v_view = vt_bank[i][:].rearrange("k (j q) -> k j q", j=PACK)
            v_unit[i] = []
            for part, groups in enumerate(store_groups(i)):
                unit = work.tile([P, len(groups), P], F32, name="v_unit", bufs=4)
                in_ = v_view[:, groups[0] : groups[-1] + 1, :]
                if part == 1:
                    nc.vector.tensor_scalar_mul(out=unit[:], in0=in_, scalar1=v_inv[i][:])
                else:
                    nc.scalar.activation(out=unit[:], in_=in_, func=ACT.Copy, scale=v_inv[i][:])
                v_unit[i].append(unit)

        def store_groups(i):
            return (range(0, 2), range(2, 4)) if i == IMAGES - 1 else (range(0, 4),)

        def turn_columns(i):
            out_bank[i] = []
            for unit, groups in zip(v_unit[i], store_groups(i)):
                turned = psum_rn.tile([P, len(groups), CLUSTERS], F32, name="rn_bank")
                for n in range(len(groups)):
                    nc.tensor.transpose(out=turned[:, n, :], in_=unit[:, n, :], identity=ident[:])
                out_bank[i].append(turned)

        def store(i):
            for part, groups in enumerate(store_groups(i)):
                out_sb = work.tile([P, len(groups), CLUSTERS], F32, name="out_sb", bufs=4)
                copy = nc.vector.tensor_copy if part == 1 else nc.scalar.copy
                copy(out=out_sb[:], in_=out_bank[i][part][:])
                nc.sync.dma_start(
                    out=out[i].rearrange("(q j) k -> q j k", j=PACK)[:, groups[0] : groups[-1] + 1, :], in_=out_sb[:]
                )

        def both(stage, i):
            for g in range(HALVES):
                stage(i, g)

        for g in range(HALVES):
            products(0, g)
            squared_norms(0, g)
            inverse_norms(0, g)
        nc.gpsimd.tensor_copy(out=par[:], in_=par_bf[:])
        transpose_weights()
        regroup_h(0, 0)
        regroup_h(0, 1)
        spread_inverse_norms(0, 0)
        transpose_features(0, 0)
        spread_inverse_norms(0, 1)
        transpose_features(0, 1)
        normalise(0, 0)
        quantise_weights()
        quantise_fn(0, 0)
        burst_rows(0, 0)
        regroup_h(1, 0)
        products(1, 0)
        products(1, 1)
        normalise(0, 1)
        quantise_h(0, 0)
        squared_norms(1, 0)
        inverse_norms(1, 0)
        products(2, 0)
        squared_norms(1, 1)
        inverse_norms(1, 1)
        spread_inverse_norms(1, 0)
        quantise_fn(0, 1)
        burst_rows(0, 1)
        squared_norms(2, 0)
        inverse_norms(2, 0)
        spread_inverse_norms(1, 1)
        transpose_features(2, 1)
        burst_rows(0, 2)
        squared_norms(2, 1)
        inverse_norms(2, 1)
        normalise(1, 0)
        spread_inverse_norms(2, 0)
        quantise_h(0, 1)
        quantise_fn(1, 0)
        burst_rows(1, 0)
        mirror(0)
        normalise(1, 1)
        quantise_ft(0)
        quantise_fn(1, 1)
        both(score_passes, 0)
        normalise(2, 0)
        both(add_bias, 0)
        burst_rows(1, 1)
        mirror_sums(0)
        quantise_h(1, 0)
        burst_power(0)
        burst_rows(1, 2)
        spread_inverse_norms(2, 1)
        quantise_fn(2, 0)
        regroup_h(2, 0)
        score_passes(1, 0)
        regroup_h(1, 1)
        add_bias(1, 0)
        burst_rows(2, 0)
        mirror(1)
        normalise(2, 1)
        quantise_h(1, 1)
        quantise_fn(2, 1)
        negative_maxima(0)
        burst_rows(2, 1)
        score_passes(1, 1)
        mirror_sums(1)
        burst_power(1)
        regroup_h(2, 1)
        add_bias(1, 1)
        burst_rows(2, 2)
        mirror(2)
        softmax_numerators(0)
        quantise_h(2, 0, 1)
        negative_maxima(1)
        both(score_passes, 2)
        transpose_features(1, 0)
        mirror_sums(2)
        add_bias(2, 0)
        softmax_numerators(1)
        transpose_features(1, 1)
        add_bias(2, 1)
        denominators(0)
        burst_power(2)
        pixel_weights(0)
        negative_maxima(2)
        both(scale_numerators, 0)
        softmax_numerators(2)
        denominators(1)
        quantise_pm(0, 0)
        pixel_weights(1)
        quantise_pm(0, 1)
        both(aggregate, 0)
        cluster_norms(0)
        transpose_features(2, 0)
        both(scale_numerators, 1)
        both(quantise_pm, 1)
        quantise_ft(1)
        both(aggregate, 1)
        denominators(2)
        pixel_weights(2)
        scale_columns(0)
        cluster_norms(1)
        turn_columns(0)
        both(scale_numerators, 2)
        both(quantise_pm, 2)
        quantise_ft(2)
        both(aggregate, 2)
        store(0)
        scale_columns(1)
        cluster_norms(2)
        turn_columns(1)
        scale_columns(2)
        store(1)
        turn_columns(2)
        store(2)
